import numpy as np
import ml_dtypes


def mxq(x, axis, fmt="e4m3"):
    dtype, down = {"e4m3": (ml_dtypes.float8_e4m3fn, 7), "e5m2": (ml_dtypes.float8_e5m2, 14)}[fmt]
    v = np.moveaxis(np.asarray(x, np.float32).astype(ml_dtypes.bfloat16).astype(np.float64), axis, -1)
    blocks = v.reshape(v.shape[:-1] + (-1, 32))
    amax = np.abs(blocks).max(-1, keepdims=True)
    byte = np.maximum(np.where(amax > 0, np.frexp(amax)[1] - 1 + 127, 0) - down, 1)
    scale = np.exp2(byte - 127.0)
    codes = (blocks / scale).astype(np.float32).astype(dtype).astype(np.float64)
    return np.moveaxis((codes * scale).reshape(v.shape), -1, axis)


WIDE = False


def mx_kscale(k):
    if not WIDE:
        return np.ones(k)
    levels = np.array([20, -20, 10, -10, 0])
    a = np.random.permutation(np.resize(levels, k // 512 * 4)).reshape(k // 512, 4)
    idx = np.arange(k)
    return np.exp2(a[idx // 512, idx % 128 // 32])


BF16 = ml_dtypes.bfloat16


def bf(x):
    return np.asarray(x, np.float32).astype(BF16)


def f64(x):
    return np.asarray(x).astype(np.float64)


B, D, S = 1024, 512, 512
EPS = 1e-5


def sigmoid(v):
    return 1.0 / (1.0 + np.exp(-v))


def norm_parts(v):
    mu = v.mean(-1, keepdims=True)
    rstd = 1.0 / np.sqrt(((v - mu) ** 2).mean(-1, keepdims=True) + EPS)
    return (v - mu) * rstd, rstd


def norm_backward(dhat, vhat, rstd):
    return rstd * (dhat - dhat.mean(-1, keepdims=True) - vhat * (dhat * vhat).mean(-1, keepdims=True))


def setup_inputs():
    a = mx_kscale(B)[:, None]
    x = bf(np.random.standard_normal((B, D)))
    p0 = bf(np.random.standard_normal((B, S)))
    p1 = bf(np.random.standard_normal((B, S)))
    Wi = bf(np.random.standard_normal((4 * S, D)) / np.sqrt(D))
    Ws = bf(np.random.standard_normal((4 * S, 2 * S)) / np.sqrt(2 * S))
    lni_g = bf(1.0 + 0.1 * np.random.standard_normal(4 * S))
    lni_b = bf(0.1 * np.random.standard_normal(4 * S))
    lns_g = bf(1.0 + 0.1 * np.random.standard_normal(4 * S))
    lns_b = bf(0.1 * np.random.standard_normal(4 * S))
    lnh_g = bf(1.0 + 0.1 * np.random.standard_normal(S))
    lnh_b = bf(0.1 * np.random.standard_normal(S))
    g = bf(np.random.standard_normal((B, S)) * np.exp2(np.random.randint(-12, 1, (B, 1))) / a)
    ihat, _ = norm_parts(f64(x) @ f64(Wi).T)
    shat, rstd_s = norm_parts(np.concatenate([f64(p0), f64(p1)], axis=1) @ f64(Ws).T)
    gates = ihat * f64(lni_g) + f64(lni_b) + shat * f64(lns_g) + f64(lns_b)
    return {"x": x,
            "s_prev0": bf(f64(p0) * a),
            "s_prev1": bf(f64(p1) * a),
            "Wi": Wi, "Ws": Ws,
            "lni_g": lni_g, "lni_b": lni_b, "lns_g": lns_g, "lns_b": lns_b,
            "lnh_g": lnh_g, "lnh_b": lnh_b,
            "gates": np.asarray(gates, np.float32),
            "shat": np.asarray(shat, np.float32),
            "rstd_s": np.asarray(rstd_s, np.float32),
            "grad_out": g}


def reference(x, s_prev0, s_prev1, Wi, Ws, lni_g, lni_b, lns_g, lns_b, lnh_g, lnh_b, gates, shat, rstd_s, grad_out):
    p0, p1 = f64(s_prev0), f64(s_prev1)
    gt, sh, rs = f64(gates), f64(shat), f64(rstd_s)
    sg, sb = f64(lns_g), f64(lns_b)
    r = sigmoid(gt[:, :S])
    i = sigmoid(gt[:, S:2 * S])
    l = sigmoid(gt[:, 3 * S:])
    s_n = sh[:, 2 * S:3 * S] * sg[2 * S:3 * S] + sb[2 * S:3 * S]
    n = np.tanh(gt[:, 2 * S:3 * S] - r * s_n)
    c = l * p0 + (1.0 - l) * p1
    h = n + i * (c - n)
    hhat, rh = norm_parts(h)
    dh = norm_backward(f64(grad_out) * f64(lnh_g), hhat, rh)
    du = dh * (1.0 - i) * (1.0 - n * n)
    dsg = np.concatenate([-du * s_n * r * (1.0 - r),
                          dh * (c - n) * i * (1.0 - i),
                          du * (1.0 - r),
                          dh * i * (p0 - p1) * l * (1.0 - l)], axis=1)
    da = norm_backward(dsg * sg, sh, rs)
    s = np.concatenate([p0, p1], axis=1)
    return mxq(da, 0, "e5m2").T @ mxq(s, 0, "e4m3")

@@ -1,0 +1,307 @@
+from contextlib import ExitStack
+
+import concourse.mybir as mybir
+
+F32 = mybir.dt.float32
+BF16 = mybir.dt.bfloat16
+U32 = mybir.dt.uint32
+U8 = mybir.dt.uint8
+E4M3X4 = mybir.dt.float8_e4m3fn_x4
+E5M2X4 = mybir.dt.float8_e5m2_x4
+ALU = mybir.AluOpType
+ACT = mybir.ActivationFunctionType
+
+P = 128
+S = 512
+GATES = 4 * S
+PACK = 4
+PASSES = 2
+CHUNKS = PASSES * PACK
+EPS = 1e-5
+RUN = 4
+
+BLOCK_COEF = (0.125, -0.25, -0.25, -0.125)
+
+FLOPS = 2 * GATES * (2 * S) * (PASSES * PACK * P)
+BYTES = (
+    2 * (PASSES * PACK * P) * GATES * 4
+    + 3 * (PASSES * PACK * P) * S * 2
+    + (PASSES * PACK * P) * 4
+    + (GATES + S + S) * 2
+    + GATES * 2 * S * 4
+)
+
+
+def tile_lngru2dcell_v_kernel(
+    tc, x, s_prev0, s_prev1, Wi, Ws, lni_g, lni_b, lns_g, lns_b, lnh_g, lnh_b, gates, shat, rstd_s, grad_out, out
+):
+    nc = tc.nc
+    r_cols = slice(0 * S, 1 * S)
+    i_cols = slice(1 * S, 2 * S)
+    n_cols = slice(2 * S, 3 * S)
+    l_cols = slice(3 * S, 4 * S)
+
+    gates_v = gates.rearrange("(c p j) w -> c p j w", p=P, j=PACK)
+    shat_v = shat.rearrange("(c p j) w -> c p j w", p=P, j=PACK)
+    grad_v = grad_out.rearrange("(c p j) w -> c p j w", p=P, j=PACK)
+    p0_v = s_prev0.rearrange("(c p j) w -> c p (j w)", p=P, j=PACK)
+    p1_v = s_prev1.rearrange("(c p j) w -> c p (j w)", p=P, j=PACK)
+
+    with ExitStack() as ctx:
+        keep = ctx.enter_context(tc.tile_pool(name="keep", bufs=1))
+        work = ctx.enter_context(tc.tile_pool(name="work", bufs=2))
+        grads = ctx.enter_context(tc.tile_pool(name="grads", bufs=3))
+        psum = ctx.enter_context(tc.psum_pool(name="psum", bufs=8))
+
+        g_sb = [keep.tile([P, PACK, GATES], F32, name="gates%d" % c) for c in range(PASSES)]
+        h_sb = [keep.tile([P, PACK, GATES], F32, name="shat%d" % c) for c in range(PASSES)]
+        p0_sb = keep.tile([P, PASSES, PACK, S], BF16)
+        p1_sb = keep.tile([P, PASSES, PACK, S], BF16)
+        s_codes = keep.tile([P, PASSES, 2 * S], U32, align_bytes=64)
+        s_scales = keep.tile([P, PASSES, 2 * S], U8, align_bytes=64)
+        da_codes = keep.tile([P, PASSES, GATES], U32, align_bytes=64)
+        da_scales = keep.tile([P, PASSES, GATES], U8, align_bytes=64)
+        sgk_bc = keep.tile([P, GATES], BF16)
+        sgn_bc = keep.tile([P, S], BF16)
+        sbn_bc = keep.tile([P, S], BF16)
+        lnh_bc = keep.tile([P, S], BF16)
+        rs_sb = keep.tile([P, CHUNKS], F32)
+        rsn_sb = keep.tile([P, CHUNKS], F32)
+        neg_half = keep.tile([P, 1], F32)
+        dve_sums = keep.tile([P, CHUNKS, 8], F32)
+        act_stats = keep.tile([P, CHUNKS, 16], F32)
+        pool_stats = keep.tile([P, CHUNKS, 2], F32)
+        unread_v = keep.tile([P, S], F32)
+        unread_w = keep.tile([P, GATES], F32)
+        unread_a = keep.tile([P, S], BF16)
+
+        for c in range(PASSES):
+            nc.sync.dma_start(out=p0_sb[:, c].rearrange("p j w -> p (j w)"), in_=p0_v[c])
+            nc.sync.dma_start(out=p1_sb[:, c].rearrange("p j w -> p (j w)"), in_=p1_v[c])
+        for k in range(CHUNKS):
+            c, j = divmod(k, PACK)
+            nc.sync.dma_start(out=g_sb[c][:, j, :], in_=gates_v[c, :, j, :])
+            nc.sync.dma_start(out=h_sb[c][:, j, :], in_=shat_v[c, :, j, :])
+        nc.scalar.dma_start(out=sgk_bc[:], in_=lns_g.partition_broadcast(P))
+        nc.scalar.dma_start(out=sbn_bc[:], in_=lns_b[n_cols].partition_broadcast(P))
+        nc.scalar.dma_start(out=lnh_bc[:], in_=lnh_g.partition_broadcast(P))
+        nc.scalar.dma_start(
+            out=rs_sb[:].rearrange("p (c j) -> p c j", j=PACK),
+            in_=rstd_s.rearrange("(c p j) o -> p c (j o)", p=P, j=PACK),
+        )
+
+        nc.gpsimd.memset(neg_half[:], -0.5)
+        nc.scalar.mul(out=rsn_sb[:], in_=rs_sb[:], mul=-1.0 / S)
+        nc.vector.tensor_copy(out=sgn_bc[:], in_=sgk_bc[:, n_cols])
+        for b in range(4):
+            cols = slice(b * S, (b + 1) * S)
+            nc.vector.tensor_scalar_mul(out=sgk_bc[:, cols], in0=sgk_bc[:, cols], scalar1=BLOCK_COEF[b])
+
+        grad_tiles = {}
+        chunk_tiles = {}
+
+        def load_grad(k):
+            c, j = divmod(k, PACK)
+            go = grads.tile([P, S], BF16)
+            nc.sync.dma_start(out=go[:], in_=grad_v[c, :, j, :])
+            grad_tiles[k] = go
+
+        def regrouped(rows):
+            return rows.rearrange("p j (q i) -> p q j i", i=RUN)
+
+        def quantise(grouped, codes, scales, x4):
+            nc.vector.quantize_mx(out=codes.bitcast(x4), scales=scales, in_=grouped[:].rearrange("p w j -> p (w j)"))
+
+        def quantise_s(c):
+            waiting = None
+            for half, src in enumerate((p0_sb, p1_sb)):
+                cols = slice(half * S, (half + 1) * S)
+                grouped = work.tile([P, S, PACK], BF16, align_bytes=64)
+                nc.vector.tensor_copy(
+                    out=grouped[:].rearrange("p (q i) j -> p q j i", i=RUN), in_=regrouped(src[:, c])
+                )
+                if waiting is not None:
+                    quantise(*waiting)
+                waiting = (grouped, s_codes[:, c, cols], s_scales[:, c, cols], E4M3X4)
+            quantise(*waiting)
+
+        def gate_tanh(k):
+            c, j = divmod(k, PACK)
+            g = g_sb[c]
+            nc.scalar.activation(out=g[:, j, 0 : 2 * S], in_=g[:, j, 0 : 2 * S], func=ACT.Tanh, scale=0.5)
+            nc.scalar.activation(out=g[:, j, l_cols], in_=g[:, j, l_cols], func=ACT.Tanh, scale=0.5)
+
+        def candidate(k):
+            c, j = divmod(k, PACK)
+            g, h = g_sb[c], h_sb[c]
+            rs2 = work.tile([P, S], F32)
+            nc.vector.tensor_tensor(out=rs2[:], in0=h[:, j, n_cols], in1=sgn_bc[:], op=ALU.mult)
+            nc.vector.tensor_tensor(out=rs2[:], in0=rs2[:], in1=sbn_bc[:], op=ALU.add)
+            nc.vector.scalar_tensor_tensor(
+                out=rs2[:], in0=g[:, j, r_cols], scalar=1.0, in1=rs2[:], op0=ALU.add, op1=ALU.mult
+            )
+            nc.vector.scalar_tensor_tensor(
+                out=g[:, j, n_cols], in0=rs2[:], scalar=-0.5, in1=g[:, j, n_cols], op0=ALU.mult, op1=ALU.add
+            )
+            nc.scalar.activation(out=g[:, j, n_cols], in_=g[:, j, n_cols], func=ACT.Tanh)
+            t1 = work.tile([P, S], F32)
+            nc.vector.tensor_tensor(out=t1[:], in0=p0_sb[:, c, j, :], in1=p1_sb[:, c, j, :], op=ALU.subtract)
+            nc.vector.scalar_tensor_tensor(
+                out=t1[:], in0=g[:, j, l_cols], scalar=1.0, in1=t1[:], op0=ALU.add, op1=ALU.mult
+            )
+            chunk_tiles[k] = {"rs2": rs2, "t1": t1}
+
+        def hidden(k):
+            c, j = divmod(k, PACK)
+            g = g_sb[c]
+            n = g[:, j, n_cols]
+            t1 = chunk_tiles[k]["t1"]
+            t3 = work.tile([P, S], F32)
+            nc.vector.tensor_tensor(out=t3[:], in0=p1_sb[:, c, j, :], in1=n, op=ALU.subtract)
+            nc.vector.scalar_tensor_tensor(
+                out=t3[:], in0=t1[:], scalar=0.5, in1=t3[:], op0=ALU.mult, op1=ALU.add
+            )
+            nc.vector.scalar_tensor_tensor(
+                out=t3[:], in0=g[:, j, i_cols], scalar=1.0, in1=t3[:], op0=ALU.add, op1=ALU.mult
+            )
+            hc = work.tile([P, S], F32)
+            nc.vector.scalar_tensor_tensor(
+                out=hc[:], in0=t3[:], scalar=0.5, in1=n, op0=ALU.mult, op1=ALU.add, accum_out=dve_sums[:, k, 0:1]
+            )
+            nc.scalar.activation(out=n, in_=n, func=ACT.Square)
+            e = work.tile([P, S], F32)
+            nc.vector.scalar_tensor_tensor(
+                out=e[:], in0=grad_tiles[k][:], scalar=1.0, in1=lnh_bc[:], op0=ALU.mult, op1=ALU.mult,
+                accum_out=dve_sums[:, k, 1:2],
+            )
+            neg_mu = act_stats[:, k, 0:1]
+            ssq = act_stats[:, k, 1:2]
+            nc.scalar.mul(out=neg_mu, in_=dve_sums[:, k, 0:1], mul=-1.0 / S)
+            nc.scalar.activation(out=hc[:], in_=hc[:], func=ACT.Identity, bias=neg_mu, scale=1.0)
+            nc.scalar.activation(out=unread_a[:], in_=hc[:], func=ACT.Square, accum_out=ssq)
+            nc.gpsimd.tensor_scalar(
+                out=pool_stats[:, k, 0:1], in0=ssq, scalar1=1.0 / S, scalar2=EPS, op0=ALU.mult, op1=ALU.add
+            )
+            nc.gpsimd.tensor_tensor(
+                out=pool_stats[:, k, 1:2], in0=pool_stats[:, k, 0:1], in1=neg_half[:], op=ALU.pow
+            )
+            chunk_tiles[k]["t3"] = t3
+            chunk_tiles[k]["hc"] = hc
+            chunk_tiles[k]["e"] = e
+
+        def hidden_norm_backward(k):
+            hc, e = chunk_tiles[k]["hc"], chunk_tiles[k]["e"]
+            nc.vector.scalar_tensor_tensor(
+                out=unread_v[:], in0=e[:], scalar=1.0, in1=hc[:], op0=ALU.mult, op1=ALU.mult,
+                accum_out=dve_sums[:, k, 2:3],
+            )
+            rh = pool_stats[:, k, 1:2]
+            a = act_stats[:, k, 2:3]
+            a_neg = act_stats[:, k, 3:4]
+            rh2 = act_stats[:, k, 4:5]
+            d_and_q = act_stats[:, k, 5:7]
+            b = act_stats[:, k, 7:8]
+            nc.scalar.activation(out=a, in_=rh, func=ACT.Copy, scale=rs_sb[:, k : k + 1])
+            nc.scalar.activation(out=a_neg, in_=rh, func=ACT.Copy, scale=rsn_sb[:, k : k + 1])
+            nc.scalar.activation(out=rh2, in_=rh, func=ACT.Square)
+            nc.scalar.activation(out=d_and_q, in_=dve_sums[:, k, 1:3], func=ACT.Copy, scale=a_neg)
+            nc.scalar.activation(out=b, in_=act_stats[:, k, 6:7], func=ACT.Copy, scale=rh2)
+            nc.scalar.activation(out=e[:], in_=e[:], func=ACT.Identity, bias=act_stats[:, k, 5:6], scale=a)
+            nc.vector.scalar_tensor_tensor(out=hc[:], in0=hc[:], scalar=b, in1=e[:], op0=ALU.mult, op1=ALU.add)
+
+        def gate_gradients(k):
+            c, j = divmod(k, PACK)
+            g, h = g_sb[c], h_sb[c]
+            tiles = chunk_tiles[k]
+            rs2, t1, t3, dh, w = tiles["rs2"], tiles["t1"], tiles["t3"], tiles["hc"], tiles["e"]
+            tanh_r, tanh_i, nsq, tanh_l = g[:, j, r_cols], g[:, j, i_cols], g[:, j, n_cols], g[:, j, l_cols]
+            nc.vector.scalar_tensor_tensor(
+                out=t1[:], in0=tanh_l, scalar=-1.0, in1=t1[:], op0=ALU.add, op1=ALU.mult
+            )
+            nc.vector.scalar_tensor_tensor(
+                out=w[:], in0=tanh_i, scalar=-1.0, in1=dh[:], op0=ALU.add, op1=ALU.mult
+            )
+            nc.vector.scalar_tensor_tensor(
+                out=dh[:], in0=tanh_i, scalar=1.0, in1=dh[:], op0=ALU.add, op1=ALU.mult
+            )
+            nc.vector.scalar_tensor_tensor(
+                out=nsq, in0=nsq, scalar=-1.0, in1=w[:], op0=ALU.add, op1=ALU.mult
+            )
+            nc.vector.tensor_tensor(out=tanh_l, in0=dh[:], in1=t1[:], op=ALU.mult)
+            nc.vector.tensor_tensor(out=tanh_i, in0=w[:], in1=t3[:], op=ALU.mult)
+            nc.vector.scalar_tensor_tensor(
+                out=nsq, in0=tanh_r, scalar=-1.0, in1=nsq, op0=ALU.add, op1=ALU.mult
+            )
+            nc.vector.tensor_tensor(out=tanh_r, in0=nsq, in1=rs2[:], op=ALU.mult)
+            nc.vector.scalar_tensor_tensor(
+                out=g[:, j, :], in0=g[:, j, :], scalar=1.0, in1=sgk_bc[:], op0=ALU.mult, op1=ALU.mult,
+                accum_out=dve_sums[:, k, 3:4],
+            )
+            nc.vector.scalar_tensor_tensor(
+                out=unread_w[:], in0=g[:, j, :], scalar=1.0, in1=h[:, j, :], op0=ALU.mult, op1=ALU.mult,
+                accum_out=dve_sums[:, k, 4:5],
+            )
+            neg_means = act_stats[:, k, 8:10]
+            nc.scalar.mul(out=neg_means, in_=dve_sums[:, k, 3:5], mul=-1.0 / GATES)
+            nc.scalar.activation(
+                out=h[:, j, :], in_=h[:, j, :], func=ACT.Identity,
+                bias=act_stats[:, k, 8:9], scale=act_stats[:, k, 9:10],
+            )
+
+        def quantise_da(c):
+            waiting = None
+            for b in range(4):
+                cols = slice(b * S, (b + 1) * S)
+                grouped = work.tile([P, S, PACK], BF16, align_bytes=64)
+                nc.vector.tensor_tensor(
+                    out=grouped[:].rearrange("p (q i) j -> p q j i", i=RUN),
+                    in0=regrouped(g_sb[c][:, :, cols]),
+                    in1=regrouped(h_sb[c][:, :, cols]),
+                    op=ALU.add,
+                )
+                if waiting is not None:
+                    quantise(*waiting)
+                waiting = (grouped, da_codes[:, c, cols], da_scales[:, c, cols], E5M2X4)
+            quantise(*waiting)
+
+        load_grad(0)
+        load_grad(1)
+        for c in range(PASSES):
+            quantise_s(c)
+        gate_tanh(0)
+        candidate(0)
+        hidden(0)
+        for k in range(CHUNKS):
+            if k + 2 < CHUNKS:
+                load_grad(k + 2)
+            if k + 1 < CHUNKS:
+                gate_tanh(k + 1)
+                candidate(k + 1)
+            hidden_norm_backward(k)
+            if k + 1 < CHUNKS:
+                hidden(k + 1)
+            gate_gradients(k)
+            if k % PACK == PACK - 1:
+                quantise_da(k // PACK)
+
+        for m in range(GATES // P):
+            rows = slice(m * P, (m + 1) * P)
+            result = work.tile([P, 2 * S], F32)
+            for half in range(2):
+                cols = slice(half * S, (half + 1) * S)
+                acc = psum.tile([P, S], F32)
+                for c in range(PASSES):
+                    nc.tensor.matmul_mx(
+                        out=acc[:],
+                        lhsT=da_codes[:, c, rows].bitcast(E5M2X4),
+                        lhsT_scale=da_scales[:, c, rows],
+                        rhs=s_codes[:, c, cols].bitcast(E4M3X4),
+                        rhs_scale=s_scales[:, c, cols],
+                        start=(c == 0),
+                        stop=(c == PASSES - 1),
+                    )
+                if half == 0:
+                    nc.scalar.copy(out=result[:, cols], in_=acc[:])
+                else:
+                    nc.vector.tensor_copy(out=result[:, cols], in_=acc[:])
+            nc.sync.dma_start(out=out[rows, :], in_=result[:])

@@ -1,6 +1,7 @@
 from contextlib import ExitStack
 
 import concourse.mybir as mybir
+from concourse.masks import make_identity
 
 F32 = mybir.dt.float32
 BF16 = mybir.dt.bfloat16
@@ -13,6 +14,7 @@ ACT = mybir.ActivationFunctionType
 
 P = 128
 S = 512
+SQ = S // P
 GATES = 4 * S
 PACK = 4
 PASSES = 2
@@ -21,6 +23,10 @@ EPS = 1e-5
 RUN = 4
 
 BLOCK_COEF = (0.125, -0.25, -0.25, -0.125)
+BLOCK_R = 0
+BLOCK_I = 1
+BLOCK_N = 2
+BLOCK_L = 3
 
 FLOPS = 2 * GATES * (2 * S) * (PASSES * PACK * P)
 BYTES = (
@@ -36,75 +42,142 @@ def tile_lngru2dcell_v_kernel(
     tc, x, s_prev0, s_prev1, Wi, Ws, lni_g, lni_b, lns_g, lns_b, lnh_g, lnh_b, gates, shat, rstd_s, grad_out, out
 ):
     nc = tc.nc
-    r_cols = slice(0 * S, 1 * S)
-    i_cols = slice(1 * S, 2 * S)
-    n_cols = slice(2 * S, 3 * S)
-    l_cols = slice(3 * S, 4 * S)
+    r_cols = slice(BLOCK_R * S, (BLOCK_R + 1) * S)
+    i_cols = slice(BLOCK_I * S, (BLOCK_I + 1) * S)
+    n_cols = slice(BLOCK_N * S, (BLOCK_N + 1) * S)
+    l_cols = slice(BLOCK_L * S, (BLOCK_L + 1) * S)
+    whole = slice(0, GATES)
 
     gates_v = gates.rearrange("(c p j) w -> c p j w", p=P, j=PACK)
     shat_v = shat.rearrange("(c p j) w -> c p j w", p=P, j=PACK)
-    grad_v = grad_out.rearrange("(c p j) w -> c p j w", p=P, j=PACK)
+    go_v = grad_out.rearrange("(c p j) w -> c p (j w)", p=P, j=PACK)
     p0_v = s_prev0.rearrange("(c p j) w -> c p (j w)", p=P, j=PACK)
     p1_v = s_prev1.rearrange("(c p j) w -> c p (j w)", p=P, j=PACK)
 
     with ExitStack() as ctx:
         keep = ctx.enter_context(tc.tile_pool(name="keep", bufs=1))
         work = ctx.enter_context(tc.tile_pool(name="work", bufs=2))
-        grads = ctx.enter_context(tc.tile_pool(name="grads", bufs=3))
         psum = ctx.enter_context(tc.psum_pool(name="psum", bufs=8))
 
         g_sb = [keep.tile([P, PACK, GATES], F32, name="gates%d" % c) for c in range(PASSES)]
         h_sb = [keep.tile([P, PACK, GATES], F32, name="shat%d" % c) for c in range(PASSES)]
         p0_sb = keep.tile([P, PASSES, PACK, S], BF16)
         p1_sb = keep.tile([P, PASSES, PACK, S], BF16)
+        go_sb = keep.tile([P, PASSES, PACK, S], BF16)
         s_codes = keep.tile([P, PASSES, 2 * S], U32, align_bytes=64)
         s_scales = keep.tile([P, PASSES, 2 * S], U8, align_bytes=64)
         da_codes = keep.tile([P, PASSES, GATES], U32, align_bytes=64)
         da_scales = keep.tile([P, PASSES, GATES], U8, align_bytes=64)
-        sgk_bc = keep.tile([P, GATES], BF16)
         sgn_bc = keep.tile([P, S], BF16)
-        sbn_bc = keep.tile([P, S], BF16)
         lnh_bc = keep.tile([P, S], BF16)
+        ident_f = keep.tile([P, P], F32)
+        ident_b = keep.tile([P, P], BF16)
+        neg_ident_b = keep.tile([P, P], BF16)
+        vec_rows = keep.tile([P, P], BF16)
+        vec_cols = keep.tile([P, 5 * SQ], F32)
+        coef_cols = keep.tile([P, 4 * SQ], F32)
         rs_sb = keep.tile([P, CHUNKS], F32)
         rsn_sb = keep.tile([P, CHUNKS], F32)
         neg_half = keep.tile([P, 1], F32)
-        dve_sums = keep.tile([P, CHUNKS, 8], F32)
+        dve_sums = keep.tile([P, CHUNKS, 16], F32)
         act_stats = keep.tile([P, CHUNKS, 16], F32)
         pool_stats = keep.tile([P, CHUNKS, 2], F32)
         unread_v = keep.tile([P, S], F32)
-        unread_w = keep.tile([P, GATES], F32)
         unread_a = keep.tile([P, S], BF16)
 
-        for c in range(PASSES):
-            nc.sync.dma_start(out=p0_sb[:, c].rearrange("p j w -> p (j w)"), in_=p0_v[c])
-            nc.sync.dma_start(out=p1_sb[:, c].rearrange("p j w -> p (j w)"), in_=p1_v[c])
-        for k in range(CHUNKS):
-            c, j = divmod(k, PACK)
-            nc.sync.dma_start(out=g_sb[c][:, j, :], in_=gates_v[c, :, j, :])
-            nc.sync.dma_start(out=h_sb[c][:, j, :], in_=shat_v[c, :, j, :])
-        nc.scalar.dma_start(out=sgk_bc[:], in_=lns_g.partition_broadcast(P))
-        nc.scalar.dma_start(out=sbn_bc[:], in_=lns_b[n_cols].partition_broadcast(P))
+        nc.vector.memset(vec_rows[:], 0.0)
+        nc.scalar.dma_start(out=vec_rows[0 : 4 * SQ, :], in_=lns_g.rearrange("(r w) -> r w", w=P))
+        nc.scalar.dma_start(out=vec_rows[4 * SQ : 5 * SQ, :], in_=lns_b[n_cols].rearrange("(r w) -> r w", w=P))
+        nc.scalar.dma_start(out=sgn_bc[:], in_=lns_g[n_cols].partition_broadcast(P))
         nc.scalar.dma_start(out=lnh_bc[:], in_=lnh_g.partition_broadcast(P))
         nc.scalar.dma_start(
             out=rs_sb[:].rearrange("p (c j) -> p c j", j=PACK),
             in_=rstd_s.rearrange("(c p j) o -> p c (j o)", p=P, j=PACK),
         )
+        for c in range(PASSES):
+            nc.sync.dma_start(out=p0_sb[:, c].rearrange("p j w -> p (j w)"), in_=p0_v[c])
+            nc.sync.dma_start(out=p1_sb[:, c].rearrange("p j w -> p (j w)"), in_=p1_v[c])
+            for j in range(PACK):
+                nc.sync.dma_start(out=g_sb[c][:, j, :], in_=gates_v[c, :, j, :])
+                nc.sync.dma_start(out=h_sb[c][:, j, :], in_=shat_v[c, :, j, :])
+                if j == 0:
+                    nc.sync.dma_start(out=go_sb[:, c].rearrange("p j w -> p (j w)"), in_=go_v[c])
 
         nc.gpsimd.memset(neg_half[:], -0.5)
-        nc.scalar.mul(out=rsn_sb[:], in_=rs_sb[:], mul=-1.0 / S)
-        nc.vector.tensor_copy(out=sgn_bc[:], in_=sgk_bc[:, n_cols])
+        make_identity(nc, ident_f[:])
+        make_identity(nc, ident_b[:])
+        nc.vector.tensor_scalar_mul(out=neg_ident_b[:], in0=ident_b[:], scalar1=-1.0)
+        vec_bank = psum.tile([P, P], BF16, tag="bank")
+        nc.tensor.transpose(vec_bank[:], vec_rows[:], ident_b[:])
+        nc.vector.tensor_copy(out=vec_cols[:], in_=vec_bank[:, 0 : 5 * SQ])
         for b in range(4):
-            cols = slice(b * S, (b + 1) * S)
-            nc.vector.tensor_scalar_mul(out=sgk_bc[:, cols], in0=sgk_bc[:, cols], scalar1=BLOCK_COEF[b])
+            sq = slice(b * SQ, (b + 1) * SQ)
+            nc.vector.tensor_scalar_mul(out=coef_cols[:, sq], in0=vec_cols[:, sq], scalar1=BLOCK_COEF[b])
+        nc.vector.tensor_scalar_mul(out=sgn_bc[:], in0=sgn_bc[:], scalar1=BLOCK_COEF[BLOCK_N])
+        nc.scalar.mul(out=rsn_sb[:], in_=rs_sb[:], mul=-1.0 / S)
 
-        grad_tiles = {}
-        chunk_tiles = {}
+        temps = {}
+        sn_banks = {}
+        d01_banks = {}
 
-        def load_grad(k):
-            c, j = divmod(k, PACK)
-            go = grads.tile([P, S], BF16)
-            nc.sync.dma_start(out=go[:], in_=grad_v[c, :, j, :])
-            grad_tiles[k] = go
+        def gate(k, cols):
+            return g_sb[k // PACK][:, k % PACK, cols]
+
+        def shat_of(k, cols):
+            return h_sb[k // PACK][:, k % PACK, cols]
+
+        def state(p_sb, k):
+            return p_sb[:, k // PACK, k % PACK, :]
+
+        def rs2(k):
+            return temps[k][:, 0, :]
+
+        def t1(k):
+            return temps[k][:, 1, :]
+
+        def t3(k):
+            return temps[k][:, 2, :]
+
+        def hc(k):
+            return temps[k][:, 3, :]
+
+        def e_of(k):
+            return temps[k][:, 4, :]
+
+        def te(k):
+            return temps[k][:, 5, :]
+
+        def stt(out, in0, scalar, in1, op0, op1, accum_out=None):
+            nc.vector.scalar_tensor_tensor(
+                out=out, in0=in0, scalar=scalar, in1=in1, op0=op0, op1=op1, accum_out=accum_out
+            )
+
+        def tt(out, in0, in1, op):
+            nc.vector.tensor_tensor(out=out, in0=in0, in1=in1, op=op)
+
+        def to_columns(rows):
+            bank = psum.tile([P, S], F32, tag="bank")
+            for q in range(SQ):
+                sq = slice(q * P, (q + 1) * P)
+                nc.tensor.transpose(bank[:, sq], rows[:, sq], ident_f[:])
+            return bank
+
+        def scale_columns(bank, dst, scale_cols, bias_cols=None):
+            for q in range(SQ):
+                sq = slice(q * P, (q + 1) * P)
+                if bias_cols is None:
+                    nc.scalar.activation(out=dst[:, sq], in_=bank[:, sq], func=ACT.Copy, scale=scale_cols[:, q : q + 1])
+                else:
+                    nc.scalar.activation(
+                        out=dst[:, sq], in_=bank[:, sq], func=ACT.Identity,
+                        scale=scale_cols[:, q : q + 1], bias=bias_cols[:, q : q + 1],
+                    )
+
+        def to_rows(squares):
+            return to_columns(squares)
+
+        def coef_of(block):
+            return coef_cols[:, block * SQ : (block + 1) * SQ]
 
         def regrouped(rows):
             return rows.rearrange("p j (q i) -> p q j i", i=RUN)
@@ -125,183 +198,172 @@ def tile_lngru2dcell_v_kernel(
                 waiting = (grouped, s_codes[:, c, cols], s_scales[:, c, cols], E4M3X4)
             quantise(*waiting)
 
-        def gate_tanh(k):
-            c, j = divmod(k, PACK)
-            g = g_sb[c]
-            nc.scalar.activation(out=g[:, j, 0 : 2 * S], in_=g[:, j, 0 : 2 * S], func=ACT.Tanh, scale=0.5)
-            nc.scalar.activation(out=g[:, j, l_cols], in_=g[:, j, l_cols], func=ACT.Tanh, scale=0.5)
+        def form_da(c, block):
+            cols = slice(block * S, (block + 1) * S)
+            grouped = work.tile([P, S, PACK], BF16, align_bytes=64)
+            tt(
+                grouped[:].rearrange("p (q i) j -> p q j i", i=RUN),
+                regrouped(g_sb[c][:, :, cols]),
+                regrouped(h_sb[c][:, :, cols]),
+                ALU.add,
+            )
+            return (grouped, da_codes[:, c, cols], da_scales[:, c, cols], E5M2X4)
 
-        def candidate(k):
-            c, j = divmod(k, PACK)
-            g, h = g_sb[c], h_sb[c]
-            rs2 = work.tile([P, S], F32)
-            nc.vector.tensor_tensor(out=rs2[:], in0=h[:, j, n_cols], in1=sgn_bc[:], op=ALU.mult)
-            nc.vector.tensor_tensor(out=rs2[:], in0=rs2[:], in1=sbn_bc[:], op=ALU.add)
-            nc.vector.scalar_tensor_tensor(
-                out=rs2[:], in0=g[:, j, r_cols], scalar=1.0, in1=rs2[:], op0=ALU.add, op1=ALU.mult
-            )
-            nc.vector.scalar_tensor_tensor(
-                out=g[:, j, n_cols], in0=rs2[:], scalar=-0.5, in1=g[:, j, n_cols], op0=ALU.mult, op1=ALU.add
-            )
-            nc.scalar.activation(out=g[:, j, n_cols], in_=g[:, j, n_cols], func=ACT.Tanh)
-            t1 = work.tile([P, S], F32)
-            nc.vector.tensor_tensor(out=t1[:], in0=p0_sb[:, c, j, :], in1=p1_sb[:, c, j, :], op=ALU.subtract)
-            nc.vector.scalar_tensor_tensor(
-                out=t1[:], in0=g[:, j, l_cols], scalar=1.0, in1=t1[:], op0=ALU.add, op1=ALU.mult
-            )
-            chunk_tiles[k] = {"rs2": rs2, "t1": t1}
+        def prepare(k):
+            bank = to_columns(shat_of(k, n_cols))
+            nc.scalar.activation(out=gate(k, slice(0, 2 * S)), in_=gate(k, slice(0, 2 * S)), func=ACT.Tanh, scale=0.5)
+            nc.scalar.activation(out=gate(k, l_cols), in_=gate(k, l_cols), func=ACT.Tanh, scale=0.5)
+            sn_squares = work.tile([P, S], F32)
+            scale_columns(bank, sn_squares, vec_cols[:, BLOCK_N * SQ : (BLOCK_N + 1) * SQ], vec_cols[:, 4 * SQ : 5 * SQ])
+            diff = psum.tile([P, S], F32, tag="bank")
+            nc.tensor.matmul(out=diff[:], lhsT=ident_b[:], rhs=state(p0_sb, k), start=True, stop=False)
+            nc.tensor.matmul(out=diff[:], lhsT=neg_ident_b[:], rhs=state(p1_sb, k), start=False, stop=True)
+            d01_banks[k] = diff
+            sn_banks[k] = to_rows(sn_squares)
 
-        def hidden(k):
-            c, j = divmod(k, PACK)
-            g = g_sb[c]
-            n = g[:, j, n_cols]
-            t1 = chunk_tiles[k]["t1"]
-            t3 = work.tile([P, S], F32)
-            nc.vector.tensor_tensor(out=t3[:], in0=p1_sb[:, c, j, :], in1=n, op=ALU.subtract)
-            nc.vector.scalar_tensor_tensor(
-                out=t3[:], in0=t1[:], scalar=0.5, in1=t3[:], op0=ALU.mult, op1=ALU.add
-            )
-            nc.vector.scalar_tensor_tensor(
-                out=t3[:], in0=g[:, j, i_cols], scalar=1.0, in1=t3[:], op0=ALU.add, op1=ALU.mult
-            )
-            hc = work.tile([P, S], F32)
-            nc.vector.scalar_tensor_tensor(
-                out=hc[:], in0=t3[:], scalar=0.5, in1=n, op0=ALU.mult, op1=ALU.add, accum_out=dve_sums[:, k, 0:1]
-            )
-            nc.scalar.activation(out=n, in_=n, func=ACT.Square)
-            e = work.tile([P, S], F32)
-            nc.vector.scalar_tensor_tensor(
-                out=e[:], in0=grad_tiles[k][:], scalar=1.0, in1=lnh_bc[:], op0=ALU.mult, op1=ALU.mult,
-                accum_out=dve_sums[:, k, 1:2],
-            )
+        def hidden_statistics(k):
             neg_mu = act_stats[:, k, 0:1]
             ssq = act_stats[:, k, 1:2]
             nc.scalar.mul(out=neg_mu, in_=dve_sums[:, k, 0:1], mul=-1.0 / S)
-            nc.scalar.activation(out=hc[:], in_=hc[:], func=ACT.Identity, bias=neg_mu, scale=1.0)
-            nc.scalar.activation(out=unread_a[:], in_=hc[:], func=ACT.Square, accum_out=ssq)
+            nc.scalar.activation(out=hc(k), in_=hc(k), func=ACT.Identity, bias=neg_mu, scale=1.0)
+            nc.scalar.activation(out=unread_a[:], in_=hc(k), func=ACT.Square, accum_out=ssq)
             nc.gpsimd.tensor_scalar(
                 out=pool_stats[:, k, 0:1], in0=ssq, scalar1=1.0 / S, scalar2=EPS, op0=ALU.mult, op1=ALU.add
             )
             nc.gpsimd.tensor_tensor(
                 out=pool_stats[:, k, 1:2], in0=pool_stats[:, k, 0:1], in1=neg_half[:], op=ALU.pow
             )
-            chunk_tiles[k]["t3"] = t3
-            chunk_tiles[k]["hc"] = hc
-            chunk_tiles[k]["e"] = e
 
-        def hidden_norm_backward(k):
-            hc, e = chunk_tiles[k]["hc"], chunk_tiles[k]["e"]
-            nc.vector.scalar_tensor_tensor(
-                out=unread_v[:], in0=e[:], scalar=1.0, in1=hc[:], op0=ALU.mult, op1=ALU.mult,
-                accum_out=dve_sums[:, k, 2:3],
-            )
+        def hidden_norm_scalars(k):
             rh = pool_stats[:, k, 1:2]
             a = act_stats[:, k, 2:3]
             a_neg = act_stats[:, k, 3:4]
             rh2 = act_stats[:, k, 4:5]
-            d_and_q = act_stats[:, k, 5:7]
-            b = act_stats[:, k, 7:8]
+            d = act_stats[:, k, 5:6]
+            b_coef = act_stats[:, k, 6:7]
             nc.scalar.activation(out=a, in_=rh, func=ACT.Copy, scale=rs_sb[:, k : k + 1])
             nc.scalar.activation(out=a_neg, in_=rh, func=ACT.Copy, scale=rsn_sb[:, k : k + 1])
             nc.scalar.activation(out=rh2, in_=rh, func=ACT.Square)
-            nc.scalar.activation(out=d_and_q, in_=dve_sums[:, k, 1:3], func=ACT.Copy, scale=a_neg)
-            nc.scalar.activation(out=b, in_=act_stats[:, k, 6:7], func=ACT.Copy, scale=rh2)
-            nc.scalar.activation(out=e[:], in_=e[:], func=ACT.Identity, bias=act_stats[:, k, 5:6], scale=a)
-            nc.vector.scalar_tensor_tensor(out=hc[:], in0=hc[:], scalar=b, in1=e[:], op0=ALU.mult, op1=ALU.add)
+            nc.scalar.activation(out=d, in_=dve_sums[:, k, 1:2], func=ACT.Copy, scale=a_neg)
+            nc.scalar.activation(out=b_coef, in_=rh2, func=ACT.Copy, scale=a_neg)
+            nc.scalar.activation(out=te(k), in_=e_of(k), func=ACT.Identity, bias=d, scale=a)
 
-        def gate_gradients(k):
-            c, j = divmod(k, PACK)
-            g, h = g_sb[c], h_sb[c]
-            tiles = chunk_tiles[k]
-            rs2, t1, t3, dh, w = tiles["rs2"], tiles["t1"], tiles["t3"], tiles["hc"], tiles["e"]
-            tanh_r, tanh_i, nsq, tanh_l = g[:, j, r_cols], g[:, j, i_cols], g[:, j, n_cols], g[:, j, l_cols]
-            nc.vector.scalar_tensor_tensor(
-                out=t1[:], in0=tanh_l, scalar=-1.0, in1=t1[:], op0=ALU.add, op1=ALU.mult
-            )
-            nc.vector.scalar_tensor_tensor(
-                out=w[:], in0=tanh_i, scalar=-1.0, in1=dh[:], op0=ALU.add, op1=ALU.mult
-            )
-            nc.vector.scalar_tensor_tensor(
-                out=dh[:], in0=tanh_i, scalar=1.0, in1=dh[:], op0=ALU.add, op1=ALU.mult
-            )
-            nc.vector.scalar_tensor_tensor(
-                out=nsq, in0=nsq, scalar=-1.0, in1=w[:], op0=ALU.add, op1=ALU.mult
-            )
-            nc.vector.tensor_tensor(out=tanh_l, in0=dh[:], in1=t1[:], op=ALU.mult)
-            nc.vector.tensor_tensor(out=tanh_i, in0=w[:], in1=t3[:], op=ALU.mult)
-            nc.vector.scalar_tensor_tensor(
-                out=nsq, in0=tanh_r, scalar=-1.0, in1=nsq, op0=ALU.add, op1=ALU.mult
-            )
-            nc.vector.tensor_tensor(out=tanh_r, in0=nsq, in1=rs2[:], op=ALU.mult)
-            nc.vector.scalar_tensor_tensor(
-                out=g[:, j, :], in0=g[:, j, :], scalar=1.0, in1=sgk_bc[:], op0=ALU.mult, op1=ALU.mult,
-                accum_out=dve_sums[:, k, 3:4],
-            )
-            nc.vector.scalar_tensor_tensor(
-                out=unread_w[:], in0=g[:, j, :], scalar=1.0, in1=h[:, j, :], op0=ALU.mult, op1=ALU.mult,
-                accum_out=dve_sums[:, k, 4:5],
-            )
-            neg_means = act_stats[:, k, 8:10]
-            nc.scalar.mul(out=neg_means, in_=dve_sums[:, k, 3:5], mul=-1.0 / GATES)
+        def mean_terms(k):
+            neg_mean_f = act_stats[:, k, 8:9]
+            neg_mean_fs = act_stats[:, k, 9:10]
             nc.scalar.activation(
-                out=h[:, j, :], in_=h[:, j, :], func=ACT.Identity,
-                bias=act_stats[:, k, 8:9], scale=act_stats[:, k, 9:10],
+                out=act_stats[:, k, 10:14], in_=dve_sums[:, k, 3:7], func=ACT.Copy, scale=-1.0 / GATES,
+                accum_out=neg_mean_f,
             )
-
-        def quantise_da(c):
-            waiting = None
-            for b in range(4):
-                cols = slice(b * S, (b + 1) * S)
-                grouped = work.tile([P, S, PACK], BF16, align_bytes=64)
-                nc.vector.tensor_tensor(
-                    out=grouped[:].rearrange("p (q i) j -> p q j i", i=RUN),
-                    in0=regrouped(g_sb[c][:, :, cols]),
-                    in1=regrouped(h_sb[c][:, :, cols]),
-                    op=ALU.add,
+            nc.scalar.mul(out=neg_mean_fs, in_=dve_sums[:, k, 7:8], mul=-1.0 / GATES)
+            for block in range(4):
+                cols = slice(block * S, (block + 1) * S)
+                nc.scalar.activation(
+                    out=shat_of(k, cols), in_=shat_of(k, cols), func=ACT.Identity, bias=neg_mean_f, scale=neg_mean_fs
                 )
-                if waiting is not None:
+
+        def round_of_work(f, b):
+            fwd = f is not None
+            bwd = b is not None
+            if fwd:
+                tmp = work.tile([P, 6, S], F32)
+                temps[f] = tmp
+            if bwd:
+                i_factor = to_rows(t3(b))
+                l_factor = to_rows(t1(b))
+                r_factor = to_rows(rs2(b))
+                tt(dve_sums[:, b, 8:9], dve_sums[:, b, 2:3], act_stats[:, b, 6:7], ALU.mult)
+            if fwd:
+                stt(rs2(f), gate(f, r_cols), 1.0, sn_banks[f][:], ALU.add, ALU.mult)
+                stt(t1(f), gate(f, l_cols), 1.0, d01_banks[f][:], ALU.add, ALU.mult)
+                stt(gate(f, n_cols), rs2(f), -0.5, gate(f, n_cols), ALU.mult, ALU.add)
+                nc.scalar.activation(out=gate(f, n_cols), in_=gate(f, n_cols), func=ACT.Tanh)
+                scale_columns(to_columns(rs2(f)), rs2(f), coef_of(BLOCK_R))
+            if bwd:
+                stt(hc(b), hc(b), dve_sums[:, b, 8:9], te(b), ALU.mult, ALU.add)
+            if fwd:
+                stt(e_of(f), state(go_sb, f), 1.0, lnh_bc[:], ALU.mult, ALU.mult, accum_out=dve_sums[:, f, 1:2])
+                if f + 1 < CHUNKS:
+                    prepare(f + 1)
+            if bwd:
+                stt(e_of(b), gate(b, i_cols), -1.0, hc(b), ALU.add, ALU.mult)
+                stt(hc(b), gate(b, i_cols), 1.0, hc(b), ALU.add, ALU.mult)
+                stt(gate(b, n_cols), gate(b, n_cols), -1.0, e_of(b), ALU.add, ALU.mult)
+            if fwd:
+                tt(t3(f), state(p1_sb, f), gate(f, n_cols), ALU.subtract)
+            if bwd:
+                stt(gate(b, i_cols), i_factor[:], 1.0, e_of(b), ALU.mult, ALU.mult, accum_out=dve_sums[:, b, 3:4])
+            if fwd:
+                stt(t3(f), t1(f), 0.5, t3(f), ALU.mult, ALU.add)
+            if bwd:
+                stt(e_of(b), gate(b, r_cols), -1.0, gate(b, n_cols), ALU.add, ALU.mult)
+            if fwd:
+                stt(t3(f), gate(f, i_cols), 1.0, t3(f), ALU.add, ALU.mult)
+            if bwd:
+                stt(gate(b, l_cols), l_factor[:], 1.0, hc(b), ALU.mult, ALU.mult, accum_out=dve_sums[:, b, 4:5])
+            if fwd:
+                stt(hc(f), t3(f), 0.5, gate(f, n_cols), ALU.mult, ALU.add, accum_out=dve_sums[:, f, 0:1])
+                hidden_statistics(f)
+                scale_columns(to_columns(t3(f)), t3(f), coef_of(BLOCK_I))
+                nc.scalar.activation(out=gate(f, n_cols), in_=gate(f, n_cols), func=ACT.Square)
+            if bwd:
+                stt(gate(b, n_cols), e_of(b), 1.0, sgn_bc[:], ALU.mult, ALU.mult, accum_out=dve_sums[:, b, 5:6])
+            if fwd:
+                stt(t1(f), gate(f, l_cols), -1.0, t1(f), ALU.add, ALU.mult)
+                scale_columns(to_columns(t1(f)), t1(f), coef_of(BLOCK_L))
+                hidden_norm_scalars(f)
+            if bwd:
+                stt(gate(b, r_cols), r_factor[:], 1.0, e_of(b), ALU.mult, ALU.mult, accum_out=dve_sums[:, b, 6:7])
+            if fwd:
+                stt(unread_v[:], e_of(f), 1.0, hc(f), ALU.mult, ALU.mult, accum_out=dve_sums[:, f, 2:3])
+            if bwd:
+                stt(
+                    temps[b][:, 0:4, :].rearrange("p a w -> p (a w)"), gate(b, whole), 1.0, shat_of(b, whole),
+                    ALU.mult, ALU.mult, accum_out=dve_sums[:, b, 7:8],
+                )
+                mean_terms(b)
+
+        def multiply(block):
+            for m in range(block * SQ, (block + 1) * SQ):
+                rows = slice(m * P, (m + 1) * P)
+                result = work.tile([P, 2 * S], F32)
+                for half in range(2):
+                    cols = slice(half * S, (half + 1) * S)
+                    acc = psum.tile([P, S], F32, tag="bank")
+                    for c in range(PASSES):
+                        nc.tensor.matmul_mx(
+                            out=acc[:],
+                            lhsT=da_codes[:, c, rows].bitcast(E5M2X4),
+                            lhsT_scale=da_scales[:, c, rows],
+                            rhs=s_codes[:, c, cols].bitcast(E4M3X4),
+                            rhs_scale=s_scales[:, c, cols],
+                            start=(c == 0),
+                            stop=(c == PASSES - 1),
+                        )
+                    if half == 0:
+                        nc.scalar.copy(out=result[:, cols], in_=acc[:])
+                    else:
+                        nc.vector.tensor_copy(out=result[:, cols], in_=acc[:])
+                nc.sync.dma_start(out=out[rows, :], in_=result[:])
+
+        with tc.manual_schedule():
+            quantise_s(0)
+            prepare(0)
+            round_of_work(0, None)
+            for k in range(CHUNKS):
+                round_of_work(k + 1 if k + 1 < CHUNKS else None, k)
+                if k == 1:
+                    quantise_s(1)
+                if k == PACK:
+                    waiting = None
+                    for block in range(4):
+                        formed = form_da(0, block)
+                        if waiting is not None:
+                            quantise(*waiting)
+                        waiting = formed
                     quantise(*waiting)
-                waiting = (grouped, da_codes[:, c, cols], da_scales[:, c, cols], E5M2X4)
-            quantise(*waiting)
-
-        load_grad(0)
-        load_grad(1)
-        for c in range(PASSES):
-            quantise_s(c)
-        gate_tanh(0)
-        candidate(0)
-        hidden(0)
-        for k in range(CHUNKS):
-            if k + 2 < CHUNKS:
-                load_grad(k + 2)
-            if k + 1 < CHUNKS:
-                gate_tanh(k + 1)
-                candidate(k + 1)
-            hidden_norm_backward(k)
-            if k + 1 < CHUNKS:
-                hidden(k + 1)
-            gate_gradients(k)
-            if k % PACK == PACK - 1:
-                quantise_da(k // PACK)
-
-        for m in range(GATES // P):
-            rows = slice(m * P, (m + 1) * P)
-            result = work.tile([P, 2 * S], F32)
-            for half in range(2):
-                cols = slice(half * S, (half + 1) * S)
-                acc = psum.tile([P, S], F32)
-                for c in range(PASSES):
-                    nc.tensor.matmul_mx(
-                        out=acc[:],
-                        lhsT=da_codes[:, c, rows].bitcast(E5M2X4),
-                        lhsT_scale=da_scales[:, c, rows],
-                        rhs=s_codes[:, c, cols].bitcast(E4M3X4),
-                        rhs_scale=s_scales[:, c, cols],
-                        start=(c == 0),
-                        stop=(c == PASSES - 1),
-                    )
-                if half == 0:
-                    nc.scalar.copy(out=result[:, cols], in_=acc[:])
-                else:
-                    nc.vector.tensor_copy(out=result[:, cols], in_=acc[:])
-            nc.sync.dma_start(out=out[rows, :], in_=result[:])
+            for block in range(4):
+                quantise(*form_da(1, block))
+                if block > 0:
+                    multiply(block - 1)
+            multiply(3)

@@ -77,11 +77,11 @@ def tile_lngru2dcell_v_kernel(
         vec_cols = keep.tile([P, 5 * SQ], F32)
         coef_cols = keep.tile([P, 4 * SQ], F32)
         rs_sb = keep.tile([P, CHUNKS], F32)
-        rsn_sb = keep.tile([P, CHUNKS], F32)
-        neg_half = keep.tile([P, 1], F32)
+        rs_pairs = keep.tile([P, CHUNKS, 2], F32)
+        powers = keep.tile([P, 2], F32)
         dve_sums = keep.tile([P, CHUNKS, 16], F32)
         act_stats = keep.tile([P, CHUNKS, 16], F32)
-        pool_stats = keep.tile([P, CHUNKS, 2], F32)
+        pool_stats = keep.tile([P, CHUNKS, 8], F32)
         unread_v = keep.tile([P, S], F32)
         unread_a = keep.tile([P, S], BF16)
 
@@ -95,15 +95,16 @@ def tile_lngru2dcell_v_kernel(
             in_=rstd_s.rearrange("(c p j) o -> p c (j o)", p=P, j=PACK),
         )
         for c in range(PASSES):
-            nc.sync.dma_start(out=p0_sb[:, c].rearrange("p j w -> p (j w)"), in_=p0_v[c])
-            nc.sync.dma_start(out=p1_sb[:, c].rearrange("p j w -> p (j w)"), in_=p1_v[c])
             for j in range(PACK):
-                nc.sync.dma_start(out=g_sb[c][:, j, :], in_=gates_v[c, :, j, :])
                 nc.sync.dma_start(out=h_sb[c][:, j, :], in_=shat_v[c, :, j, :])
+                nc.sync.dma_start(out=g_sb[c][:, j, :], in_=gates_v[c, :, j, :])
                 if j == 0:
+                    nc.sync.dma_start(out=p0_sb[:, c].rearrange("p j w -> p (j w)"), in_=p0_v[c])
+                    nc.sync.dma_start(out=p1_sb[:, c].rearrange("p j w -> p (j w)"), in_=p1_v[c])
                     nc.sync.dma_start(out=go_sb[:, c].rearrange("p j w -> p (j w)"), in_=go_v[c])
 
-        nc.gpsimd.memset(neg_half[:], -0.5)
+        nc.gpsimd.memset(powers[:, 0:1], -0.5)
+        nc.gpsimd.memset(powers[:, 1:2], -1.0)
         make_identity(nc, ident_f[:])
         make_identity(nc, ident_b[:])
         nc.vector.tensor_scalar_mul(out=neg_ident_b[:], in0=ident_b[:], scalar1=-1.0)
@@ -114,7 +115,8 @@ def tile_lngru2dcell_v_kernel(
             sq = slice(b * SQ, (b + 1) * SQ)
             nc.vector.tensor_scalar_mul(out=coef_cols[:, sq], in0=vec_cols[:, sq], scalar1=BLOCK_COEF[b])
         nc.vector.tensor_scalar_mul(out=sgn_bc[:], in0=sgn_bc[:], scalar1=BLOCK_COEF[BLOCK_N])
-        nc.scalar.mul(out=rsn_sb[:], in_=rs_sb[:], mul=-1.0 / S)
+        nc.vector.tensor_copy(out=rs_pairs[:, :, 0], in_=rs_sb[:])
+        nc.vector.tensor_scalar_mul(out=rs_pairs[:, :, 1], in0=rs_sb[:], scalar1=-1.0 / S)
 
         temps = {}
         sn_banks = {}
@@ -224,28 +226,25 @@ def tile_lngru2dcell_v_kernel(
         def hidden_statistics(k):
             neg_mu = act_stats[:, k, 0:1]
             ssq = act_stats[:, k, 1:2]
+            d = act_stats[:, k, 2:3]
+            var_eps = pool_stats[:, k, 0:1]
+            rh = pool_stats[:, k, 1:2]
+            a = pool_stats[:, k, 3:4]
+            a_neg = pool_stats[:, k, 4:5]
             nc.scalar.mul(out=neg_mu, in_=dve_sums[:, k, 0:1], mul=-1.0 / S)
-            nc.scalar.activation(out=hc(k), in_=hc(k), func=ACT.Identity, bias=neg_mu, scale=1.0)
-            nc.scalar.activation(out=unread_a[:], in_=hc(k), func=ACT.Square, accum_out=ssq)
-            nc.gpsimd.tensor_scalar(
-                out=pool_stats[:, k, 0:1], in0=ssq, scalar1=1.0 / S, scalar2=EPS, op0=ALU.mult, op1=ALU.add
+            nc.scalar.activation(out=unread_a[:], in_=hc(k), func=ACT.Square, bias=neg_mu, scale=1.0, accum_out=ssq)
+            nc.gpsimd.tensor_scalar(out=var_eps, in0=ssq, scalar1=1.0 / S, scalar2=EPS, op0=ALU.mult, op1=ALU.add)
+            nc.gpsimd.tensor_tensor(
+                out=pool_stats[:, k, 1:3], in0=var_eps.to_broadcast([P, 2]), in1=powers[:], op=ALU.pow
             )
             nc.gpsimd.tensor_tensor(
-                out=pool_stats[:, k, 1:2], in0=pool_stats[:, k, 0:1], in1=neg_half[:], op=ALU.pow
+                out=pool_stats[:, k, 3:5], in0=rh.to_broadcast([P, 2]), in1=rs_pairs[:, k, :], op=ALU.mult
             )
+            nc.scalar.activation(out=hc(k), in_=hc(k), func=ACT.Identity, bias=neg_mu, scale=1.0)
+            return (a, a_neg, d)
 
-        def hidden_norm_scalars(k):
-            rh = pool_stats[:, k, 1:2]
-            a = act_stats[:, k, 2:3]
-            a_neg = act_stats[:, k, 3:4]
-            rh2 = act_stats[:, k, 4:5]
-            d = act_stats[:, k, 5:6]
-            b_coef = act_stats[:, k, 6:7]
-            nc.scalar.activation(out=a, in_=rh, func=ACT.Copy, scale=rs_sb[:, k : k + 1])
-            nc.scalar.activation(out=a_neg, in_=rh, func=ACT.Copy, scale=rsn_sb[:, k : k + 1])
-            nc.scalar.activation(out=rh2, in_=rh, func=ACT.Square)
+        def scaled_e(k, a, a_neg, d):
             nc.scalar.activation(out=d, in_=dve_sums[:, k, 1:2], func=ACT.Copy, scale=a_neg)
-            nc.scalar.activation(out=b_coef, in_=rh2, func=ACT.Copy, scale=a_neg)
             nc.scalar.activation(out=te(k), in_=e_of(k), func=ACT.Identity, bias=d, scale=a)
 
         def mean_terms(k):
@@ -272,10 +271,16 @@ def tile_lngru2dcell_v_kernel(
                 i_factor = to_rows(t3(b))
                 l_factor = to_rows(t1(b))
                 r_factor = to_rows(rs2(b))
-                tt(dve_sums[:, b, 8:9], dve_sums[:, b, 2:3], act_stats[:, b, 6:7], ALU.mult)
+                stt(unread_v[:], e_of(b), 1.0, hc(b), ALU.mult, ALU.mult, accum_out=dve_sums[:, b, 2:3])
             if fwd:
                 stt(rs2(f), gate(f, r_cols), 1.0, sn_banks[f][:], ALU.add, ALU.mult)
                 stt(t1(f), gate(f, l_cols), 1.0, d01_banks[f][:], ALU.add, ALU.mult)
+            if bwd:
+                nc.vector.tensor_scalar(
+                    out=dve_sums[:, b, 8:9], in0=dve_sums[:, b, 2:3],
+                    scalar1=pool_stats[:, b, 2:3], scalar2=pool_stats[:, b, 4:5], op0=ALU.mult, op1=ALU.mult,
+                )
+            if fwd:
                 stt(gate(f, n_cols), rs2(f), -0.5, gate(f, n_cols), ALU.mult, ALU.add)
                 nc.scalar.activation(out=gate(f, n_cols), in_=gate(f, n_cols), func=ACT.Tanh)
                 scale_columns(to_columns(rs2(f)), rs2(f), coef_of(BLOCK_R))
@@ -303,19 +308,16 @@ def tile_lngru2dcell_v_kernel(
                 stt(gate(b, l_cols), l_factor[:], 1.0, hc(b), ALU.mult, ALU.mult, accum_out=dve_sums[:, b, 4:5])
             if fwd:
                 stt(hc(f), t3(f), 0.5, gate(f, n_cols), ALU.mult, ALU.add, accum_out=dve_sums[:, f, 0:1])
-                hidden_statistics(f)
+                norm_scalars = hidden_statistics(f)
                 scale_columns(to_columns(t3(f)), t3(f), coef_of(BLOCK_I))
                 nc.scalar.activation(out=gate(f, n_cols), in_=gate(f, n_cols), func=ACT.Square)
             if bwd:
                 stt(gate(b, n_cols), e_of(b), 1.0, sgn_bc[:], ALU.mult, ALU.mult, accum_out=dve_sums[:, b, 5:6])
+                stt(gate(b, r_cols), r_factor[:], 1.0, e_of(b), ALU.mult, ALU.mult, accum_out=dve_sums[:, b, 6:7])
             if fwd:
                 stt(t1(f), gate(f, l_cols), -1.0, t1(f), ALU.add, ALU.mult)
                 scale_columns(to_columns(t1(f)), t1(f), coef_of(BLOCK_L))
-                hidden_norm_scalars(f)
-            if bwd:
-                stt(gate(b, r_cols), r_factor[:], 1.0, e_of(b), ALU.mult, ALU.mult, accum_out=dve_sums[:, b, 6:7])
-            if fwd:
-                stt(unread_v[:], e_of(f), 1.0, hc(f), ALU.mult, ALU.mult, accum_out=dve_sums[:, f, 2:3])
+                scaled_e(f, *norm_scalars)
             if bwd:
                 stt(
                     temps[b][:, 0:4, :].rearrange("p a w -> p (a w)"), gate(b, whole), 1.0, shat_of(b, whole),
@@ -323,10 +325,17 @@ def tile_lngru2dcell_v_kernel(
                 )
                 mean_terms(b)
 
+        results = [
+            tile_of_pass0[:, j, side * 2 * S : (side + 1) * 2 * S]
+            for tile_of_pass0 in (g_sb[0], h_sb[0])
+            for j in range(PACK)
+            for side in range(2)
+        ]
+
         def multiply(block):
             for m in range(block * SQ, (block + 1) * SQ):
                 rows = slice(m * P, (m + 1) * P)
-                result = work.tile([P, 2 * S], F32)
+                result = results[m]
                 for half in range(2):
                     cols = slice(half * S, (half + 1) * S)
                     acc = psum.tile([P, S], F32, tag="bank")
@@ -340,16 +349,16 @@ def tile_lngru2dcell_v_kernel(
                             start=(c == 0),
                             stop=(c == PASSES - 1),
                         )
-                    if half == 0:
-                        nc.scalar.copy(out=result[:, cols], in_=acc[:])
-                    else:
+                    if (2 * m + half) % 4 == 3:
                         nc.vector.tensor_copy(out=result[:, cols], in_=acc[:])
-                nc.sync.dma_start(out=out[rows, :], in_=result[:])
+                    else:
+                        nc.scalar.copy(out=result[:, cols], in_=acc[:])
+                nc.sync.dma_start(out=out[rows, :], in_=result)
 
         with tc.manual_schedule():
-            quantise_s(0)
             prepare(0)
             round_of_work(0, None)
+            quantise_s(0)
             for k in range(CHUNKS):
                 round_of_work(k + 1 if k + 1 < CHUNKS else None, k)
                 if k == 1:

@@ -20,6 +20,8 @@ PACK = 4
 PASSES = 2
 CHUNKS = PASSES * PACK
 EPS = 1e-5
+DA_PIECE = 256
+STAGED = 3
 RUN = 4
 
 BLOCK_COEF = (0.125, -0.25, -0.25, -0.125)
@@ -200,9 +202,9 @@ def tile_lngru2dcell_v_kernel(
                 waiting = (grouped, s_codes[:, c, cols], s_scales[:, c, cols], E4M3X4)
             quantise(*waiting)
 
-        def form_da(c, block):
-            cols = slice(block * S, (block + 1) * S)
-            grouped = work.tile([P, S, PACK], BF16, align_bytes=64)
+        def form_da(c, piece, width):
+            cols = slice(piece * width, (piece + 1) * width)
+            grouped = work.tile([P, width, PACK], BF16, align_bytes=64)
             tt(
                 grouped[:].rearrange("p (q i) j -> p q j i", i=RUN),
                 regrouped(g_sb[c][:, :, cols]),
@@ -325,35 +327,29 @@ def tile_lngru2dcell_v_kernel(
                 )
                 mean_terms(b)
 
-        results = [
-            tile_of_pass0[:, j, side * 2 * S : (side + 1) * 2 * S]
-            for tile_of_pass0 in (g_sb[0], h_sb[0])
-            for j in range(PACK)
-            for side in range(2)
-        ]
+        stages = {}
 
-        def multiply(block):
-            for m in range(block * SQ, (block + 1) * SQ):
-                rows = slice(m * P, (m + 1) * P)
-                result = results[m]
-                for half in range(2):
-                    cols = slice(half * S, (half + 1) * S)
-                    acc = psum.tile([P, S], F32, tag="bank")
-                    for c in range(PASSES):
-                        nc.tensor.matmul_mx(
-                            out=acc[:],
-                            lhsT=da_codes[:, c, rows].bitcast(E5M2X4),
-                            lhsT_scale=da_scales[:, c, rows],
-                            rhs=s_codes[:, c, cols].bitcast(E4M3X4),
-                            rhs_scale=s_scales[:, c, cols],
-                            start=(c == 0),
-                            stop=(c == PASSES - 1),
-                        )
-                    if (2 * m + half) % 4 == 3:
-                        nc.vector.tensor_copy(out=result[:, cols], in_=acc[:])
-                    else:
-                        nc.scalar.copy(out=result[:, cols], in_=acc[:])
-                nc.sync.dma_start(out=out[rows, :], in_=result)
+        def multiply(m):
+            rows = slice(m * P, (m + 1) * P)
+            if m % STAGED == 0:
+                stage = work.tile([P, STAGED, 2 * S], F32, tag="tmp")
+                stages[m // STAGED] = stage
+            result = stages[m // STAGED][:, m % STAGED, :]
+            for half in range(2):
+                cols = slice(half * S, (half + 1) * S)
+                acc = psum.tile([P, S], F32, tag="bank")
+                for c in range(PASSES):
+                    nc.tensor.matmul_mx(
+                        out=acc[:],
+                        lhsT=da_codes[:, c, rows].bitcast(E5M2X4),
+                        lhsT_scale=da_scales[:, c, rows],
+                        rhs=s_codes[:, c, cols].bitcast(E4M3X4),
+                        rhs_scale=s_scales[:, c, cols],
+                        start=(c == 0),
+                        stop=(c == PASSES - 1),
+                    )
+                nc.scalar.copy(out=result[:, cols], in_=acc[:])
+            nc.sync.dma_start(out=out[rows, :], in_=result)
 
         with tc.manual_schedule():
             prepare(0)
@@ -363,16 +359,13 @@ def tile_lngru2dcell_v_kernel(
                 round_of_work(k + 1 if k + 1 < CHUNKS else None, k)
                 if k == 1:
                     quantise_s(1)
-                if k == PACK:
-                    waiting = None
-                    for block in range(4):
-                        formed = form_da(0, block)
-                        if waiting is not None:
-                            quantise(*waiting)
-                        waiting = formed
-                    quantise(*waiting)
-            for block in range(4):
-                quantise(*form_da(1, block))
-                if block > 0:
-                    multiply(block - 1)
-            multiply(3)
+            waiting = None
+            for piece in range(GATES // DA_PIECE + 1):
+                for c in range(PASSES):
+                    formed = form_da(c, piece, DA_PIECE) if piece < GATES // DA_PIECE else None
+                    if waiting is not None:
+                        quantise(*waiting)
+                    waiting = formed
+                if piece > 0:
+                    for m in range((piece - 1) * DA_PIECE // P, piece * DA_PIECE // P):
+                        multiply(m)

@@ -81,9 +81,10 @@ def tile_lngru2dcell_v_kernel(
         rs_sb = keep.tile([P, CHUNKS], F32)
         rs_pairs = keep.tile([P, CHUNKS, 2], F32)
         powers = keep.tile([P, 2], F32)
+        eps_col = keep.tile([P, 1], F32)
         dve_sums = keep.tile([P, CHUNKS, 16], F32)
         act_stats = keep.tile([P, CHUNKS, 16], F32)
-        pool_stats = keep.tile([P, CHUNKS, 8], F32)
+        pool_stats = keep.tile([P, CHUNKS, 2], F32)
         unread_v = keep.tile([P, S], F32)
         unread_a = keep.tile([P, S], BF16)
 
@@ -107,6 +108,7 @@ def tile_lngru2dcell_v_kernel(
 
         nc.gpsimd.memset(powers[:, 0:1], -0.5)
         nc.gpsimd.memset(powers[:, 1:2], -1.0)
+        nc.gpsimd.memset(eps_col[:], EPS)
         make_identity(nc, ident_f[:])
         make_identity(nc, ident_b[:])
         nc.vector.tensor_scalar_mul(out=neg_ident_b[:], in0=ident_b[:], scalar1=-1.0)
@@ -228,24 +230,20 @@ def tile_lngru2dcell_v_kernel(
         def hidden_statistics(k):
             neg_mu = act_stats[:, k, 0:1]
             ssq = act_stats[:, k, 1:2]
-            d = act_stats[:, k, 2:3]
-            var_eps = pool_stats[:, k, 0:1]
-            rh = pool_stats[:, k, 1:2]
-            a = pool_stats[:, k, 3:4]
-            a_neg = pool_stats[:, k, 4:5]
+            var_eps = act_stats[:, k, 2:3]
             nc.scalar.mul(out=neg_mu, in_=dve_sums[:, k, 0:1], mul=-1.0 / S)
             nc.scalar.activation(out=unread_a[:], in_=hc(k), func=ACT.Square, bias=neg_mu, scale=1.0, accum_out=ssq)
-            nc.gpsimd.tensor_scalar(out=var_eps, in0=ssq, scalar1=1.0 / S, scalar2=EPS, op0=ALU.mult, op1=ALU.add)
+            nc.scalar.activation(out=var_eps, in_=ssq, func=ACT.Identity, bias=eps_col[:], scale=1.0 / S)
             nc.gpsimd.tensor_tensor(
-                out=pool_stats[:, k, 1:3], in0=var_eps.to_broadcast([P, 2]), in1=powers[:], op=ALU.pow
-            )
-            nc.gpsimd.tensor_tensor(
-                out=pool_stats[:, k, 3:5], in0=rh.to_broadcast([P, 2]), in1=rs_pairs[:, k, :], op=ALU.mult
+                out=pool_stats[:, k, 0:2], in0=var_eps.to_broadcast([P, 2]), in1=powers[:], op=ALU.pow
             )
             nc.scalar.activation(out=hc(k), in_=hc(k), func=ACT.Identity, bias=neg_mu, scale=1.0)
-            return (a, a_neg, d)
 
-        def scaled_e(k, a, a_neg, d):
+        def scaled_e(k):
+            a = act_stats[:, k, 4:5]
+            a_neg = act_stats[:, k, 5:6]
+            d = act_stats[:, k, 6:7]
+            nc.scalar.activation(out=act_stats[:, k, 4:6], in_=rs_pairs[:, k, :], func=ACT.Copy, scale=pool_stats[:, k, 0:1])
             nc.scalar.activation(out=d, in_=dve_sums[:, k, 1:2], func=ACT.Copy, scale=a_neg)
             nc.scalar.activation(out=te(k), in_=e_of(k), func=ACT.Identity, bias=d, scale=a)
 
@@ -280,7 +278,7 @@ def tile_lngru2dcell_v_kernel(
             if bwd:
                 nc.vector.tensor_scalar(
                     out=dve_sums[:, b, 8:9], in0=dve_sums[:, b, 2:3],
-                    scalar1=pool_stats[:, b, 2:3], scalar2=pool_stats[:, b, 4:5], op0=ALU.mult, op1=ALU.mult,
+                    scalar1=pool_stats[:, b, 1:2], scalar2=act_stats[:, b, 5:6], op0=ALU.mult, op1=ALU.mult,
                 )
             if fwd:
                 stt(gate(f, n_cols), rs2(f), -0.5, gate(f, n_cols), ALU.mult, ALU.add)
@@ -299,27 +297,24 @@ def tile_lngru2dcell_v_kernel(
             if fwd:
                 tt(t3(f), state(p1_sb, f), gate(f, n_cols), ALU.subtract)
             if bwd:
-                stt(gate(b, i_cols), i_factor[:], 1.0, e_of(b), ALU.mult, ALU.mult, accum_out=dve_sums[:, b, 3:4])
+                stt(te(b), gate(b, r_cols), -1.0, gate(b, n_cols), ALU.add, ALU.mult)
             if fwd:
                 stt(t3(f), t1(f), 0.5, t3(f), ALU.mult, ALU.add)
             if bwd:
-                stt(e_of(b), gate(b, r_cols), -1.0, gate(b, n_cols), ALU.add, ALU.mult)
+                stt(gate(b, n_cols), te(b), 1.0, sgn_bc[:], ALU.mult, ALU.mult, accum_out=dve_sums[:, b, 5:6])
             if fwd:
                 stt(t3(f), gate(f, i_cols), 1.0, t3(f), ALU.add, ALU.mult)
-            if bwd:
-                stt(gate(b, l_cols), l_factor[:], 1.0, hc(b), ALU.mult, ALU.mult, accum_out=dve_sums[:, b, 4:5])
-            if fwd:
+                stt(t1(f), gate(f, l_cols), -1.0, t1(f), ALU.add, ALU.mult)
                 stt(hc(f), t3(f), 0.5, gate(f, n_cols), ALU.mult, ALU.add, accum_out=dve_sums[:, f, 0:1])
-                norm_scalars = hidden_statistics(f)
+                hidden_statistics(f)
+                scale_columns(to_columns(t1(f)), t1(f), coef_of(BLOCK_L))
                 scale_columns(to_columns(t3(f)), t3(f), coef_of(BLOCK_I))
                 nc.scalar.activation(out=gate(f, n_cols), in_=gate(f, n_cols), func=ACT.Square)
+                scaled_e(f)
             if bwd:
-                stt(gate(b, n_cols), e_of(b), 1.0, sgn_bc[:], ALU.mult, ALU.mult, accum_out=dve_sums[:, b, 5:6])
-                stt(gate(b, r_cols), r_factor[:], 1.0, e_of(b), ALU.mult, ALU.mult, accum_out=dve_sums[:, b, 6:7])
-            if fwd:
-                stt(t1(f), gate(f, l_cols), -1.0, t1(f), ALU.add, ALU.mult)
-                scale_columns(to_columns(t1(f)), t1(f), coef_of(BLOCK_L))
-                scaled_e(f, *norm_scalars)
+                stt(gate(b, i_cols), i_factor[:], 1.0, e_of(b), ALU.mult, ALU.mult, accum_out=dve_sums[:, b, 3:4])
+                stt(gate(b, l_cols), l_factor[:], 1.0, hc(b), ALU.mult, ALU.mult, accum_out=dve_sums[:, b, 4:5])
+                stt(gate(b, r_cols), r_factor[:], 1.0, te(b), ALU.mult, ALU.mult, accum_out=dve_sums[:, b, 6:7])
             if bwd:
                 stt(
                     temps[b][:, 0:4, :].rearrange("p a w -> p (a w)"), gate(b, whole), 1.0, shat_of(b, whole),

@@ -99,8 +99,10 @@ def tile_lngru2dcell_v_kernel(
         )
         for c in range(PASSES):
             for j in range(PACK):
-                nc.sync.dma_start(out=h_sb[c][:, j, :], in_=shat_v[c, :, j, :])
+                nc.sync.dma_start(out=h_sb[c][:, j, n_cols], in_=shat_v[c, :, j, n_cols])
                 nc.sync.dma_start(out=g_sb[c][:, j, :], in_=gates_v[c, :, j, :])
+                nc.sync.dma_start(out=h_sb[c][:, j, 0 : 2 * S], in_=shat_v[c, :, j, 0 : 2 * S])
+                nc.sync.dma_start(out=h_sb[c][:, j, l_cols], in_=shat_v[c, :, j, l_cols])
                 if j == 0:
                     nc.sync.dma_start(out=p0_sb[:, c].rearrange("p j w -> p (j w)"), in_=p0_v[c])
                     nc.sync.dma_start(out=p1_sb[:, c].rearrange("p j w -> p (j w)"), in_=p1_v[c])
@@ -293,22 +295,24 @@ def tile_lngru2dcell_v_kernel(
             if bwd:
                 stt(e_of(b), gate(b, i_cols), -1.0, hc(b), ALU.add, ALU.mult)
                 stt(hc(b), gate(b, i_cols), 1.0, hc(b), ALU.add, ALU.mult)
-                stt(gate(b, n_cols), gate(b, n_cols), -1.0, e_of(b), ALU.add, ALU.mult)
             if fwd:
                 tt(t3(f), state(p1_sb, f), gate(f, n_cols), ALU.subtract)
             if bwd:
-                stt(te(b), gate(b, r_cols), -1.0, gate(b, n_cols), ALU.add, ALU.mult)
+                stt(gate(b, n_cols), gate(b, n_cols), -1.0, e_of(b), ALU.add, ALU.mult)
             if fwd:
                 stt(t3(f), t1(f), 0.5, t3(f), ALU.mult, ALU.add)
             if bwd:
-                stt(gate(b, n_cols), te(b), 1.0, sgn_bc[:], ALU.mult, ALU.mult, accum_out=dve_sums[:, b, 5:6])
+                stt(te(b), gate(b, r_cols), -1.0, gate(b, n_cols), ALU.add, ALU.mult)
             if fwd:
                 stt(t3(f), gate(f, i_cols), 1.0, t3(f), ALU.add, ALU.mult)
-                stt(t1(f), gate(f, l_cols), -1.0, t1(f), ALU.add, ALU.mult)
+            if bwd:
+                stt(gate(b, n_cols), te(b), 1.0, sgn_bc[:], ALU.mult, ALU.mult, accum_out=dve_sums[:, b, 5:6])
+            if fwd:
                 stt(hc(f), t3(f), 0.5, gate(f, n_cols), ALU.mult, ALU.add, accum_out=dve_sums[:, f, 0:1])
                 hidden_statistics(f)
-                scale_columns(to_columns(t1(f)), t1(f), coef_of(BLOCK_L))
                 scale_columns(to_columns(t3(f)), t3(f), coef_of(BLOCK_I))
+                stt(t1(f), gate(f, l_cols), -1.0, t1(f), ALU.add, ALU.mult)
+                scale_columns(to_columns(t1(f)), t1(f), coef_of(BLOCK_L))
                 nc.scalar.activation(out=gate(f, n_cols), in_=gate(f, n_cols), func=ACT.Square)
                 scaled_e(f)
             if bwd:

@@ -21,6 +21,8 @@ PASSES = 2
 CHUNKS = PASSES * PACK
 EPS = 1e-5
 DA_PIECE = 256
+PIECES = GATES // DA_PIECE
+EARLY = 5
 STAGED = 3
 RUN = 4
 
@@ -52,9 +54,9 @@ def tile_lngru2dcell_v_kernel(
 
     gates_v = gates.rearrange("(c p j) w -> c p j w", p=P, j=PACK)
     shat_v = shat.rearrange("(c p j) w -> c p j w", p=P, j=PACK)
-    go_v = grad_out.rearrange("(c p j) w -> c p (j w)", p=P, j=PACK)
-    p0_v = s_prev0.rearrange("(c p j) w -> c p (j w)", p=P, j=PACK)
-    p1_v = s_prev1.rearrange("(c p j) w -> c p (j w)", p=P, j=PACK)
+    go_v = grad_out.rearrange("(c p j) w -> c p j w", p=P, j=PACK)
+    p0_v = s_prev0.rearrange("(c p j) w -> c p j w", p=P, j=PACK)
+    p1_v = s_prev1.rearrange("(c p j) w -> c p j w", p=P, j=PACK)
 
     with ExitStack() as ctx:
         keep = ctx.enter_context(tc.tile_pool(name="keep", bufs=1))
@@ -77,6 +79,8 @@ def tile_lngru2dcell_v_kernel(
         neg_ident_b = keep.tile([P, P], BF16)
         vec_rows = keep.tile([P, P], BF16)
         vec_cols = keep.tile([P, 5 * SQ], F32)
+        first_row = keep.tile([P, 2 * S], BF16)
+        ones_b = keep.tile([P, P], BF16)
         coef_cols = keep.tile([P, 4 * SQ], F32)
         rs_sb = keep.tile([P, CHUNKS], F32)
         rs_pairs = keep.tile([P, CHUNKS, 2], F32)
@@ -91,22 +95,37 @@ def tile_lngru2dcell_v_kernel(
         nc.vector.memset(vec_rows[:], 0.0)
         nc.scalar.dma_start(out=vec_rows[0 : 4 * SQ, :], in_=lns_g.rearrange("(r w) -> r w", w=P))
         nc.scalar.dma_start(out=vec_rows[4 * SQ : 5 * SQ, :], in_=lns_b[n_cols].rearrange("(r w) -> r w", w=P))
-        nc.scalar.dma_start(out=sgn_bc[:], in_=lns_g[n_cols].partition_broadcast(P))
-        nc.scalar.dma_start(out=lnh_bc[:], in_=lnh_g.partition_broadcast(P))
+        nc.vector.memset(first_row[:], 0.0)
+        nc.scalar.dma_start(out=first_row[0:1, 0:S], in_=lnh_g.rearrange("(r w) -> r w", r=1))
+        nc.scalar.dma_start(out=first_row[0:1, S : 2 * S], in_=lns_g[n_cols].rearrange("(r w) -> r w", r=1))
         nc.scalar.dma_start(
             out=rs_sb[:].rearrange("p (c j) -> p c j", j=PACK),
             in_=rstd_s.rearrange("(c p j) o -> p c (j o)", p=P, j=PACK),
         )
+        def load_shat(c, j, cols):
+            nc.sync.dma_start(out=h_sb[c][:, j, cols], in_=shat_v[c, :, j, cols])
+
+        def load_gates(c, j):
+            nc.sync.dma_start(out=g_sb[c][:, j, :], in_=gates_v[c, :, j, :])
+
+        def load_states(c, rows):
+            for dst, src in ((p0_sb, p0_v), (p1_sb, p1_v), (go_sb, go_v)):
+                nc.sync.dma_start(out=dst[:, c, rows, :], in_=src[c, :, rows, :])
+
+        load_shat(0, 0, n_cols)
+        load_gates(0, 0)
+        load_states(0, slice(0, 1))
         for c in range(PASSES):
             for j in range(PACK):
-                nc.sync.dma_start(out=h_sb[c][:, j, n_cols], in_=shat_v[c, :, j, n_cols])
-                nc.sync.dma_start(out=g_sb[c][:, j, :], in_=gates_v[c, :, j, :])
-                nc.sync.dma_start(out=h_sb[c][:, j, 0 : 2 * S], in_=shat_v[c, :, j, 0 : 2 * S])
-                nc.sync.dma_start(out=h_sb[c][:, j, l_cols], in_=shat_v[c, :, j, l_cols])
-                if j == 0:
-                    nc.sync.dma_start(out=p0_sb[:, c].rearrange("p j w -> p (j w)"), in_=p0_v[c])
-                    nc.sync.dma_start(out=p1_sb[:, c].rearrange("p j w -> p (j w)"), in_=p1_v[c])
-                    nc.sync.dma_start(out=go_sb[:, c].rearrange("p j w -> p (j w)"), in_=go_v[c])
+                if c + j > 0:
+                    load_shat(c, j, whole)
+                    load_gates(c, j)
+                if c == 0 and j == 1:
+                    load_states(0, slice(1, PACK))
+                    load_shat(0, 0, slice(0, 2 * S))
+                    load_shat(0, 0, l_cols)
+                if c > 0 and j == 0:
+                    load_states(c, slice(0, PACK))
 
         nc.gpsimd.memset(powers[:, 0:1], -0.5)
         nc.gpsimd.memset(powers[:, 1:2], -1.0)
@@ -120,7 +139,13 @@ def tile_lngru2dcell_v_kernel(
         for b in range(4):
             sq = slice(b * SQ, (b + 1) * SQ)
             nc.vector.tensor_scalar_mul(out=coef_cols[:, sq], in0=vec_cols[:, sq], scalar1=BLOCK_COEF[b])
-        nc.vector.tensor_scalar_mul(out=sgn_bc[:], in0=sgn_bc[:], scalar1=BLOCK_COEF[BLOCK_N])
+        nc.vector.memset(ones_b[:], 1.0)
+        for half, (dst, factor) in enumerate(((lnh_bc, 1.0), (sgn_bc, BLOCK_COEF[BLOCK_N]))):
+            spread = psum.tile([P, S], F32, tag="bank")
+            nc.tensor.matmul(
+                out=spread[:], lhsT=ones_b[:], rhs=first_row[:, half * S : (half + 1) * S], start=True, stop=True
+            )
+            nc.vector.tensor_scalar_mul(out=dst[:], in0=spread[:], scalar1=factor)
         nc.vector.tensor_copy(out=rs_pairs[:, :, 0], in_=rs_sb[:])
         nc.vector.tensor_scalar_mul(out=rs_pairs[:, :, 1], in0=rs_sb[:], scalar1=-1.0 / S)
 
@@ -193,29 +218,54 @@ def tile_lngru2dcell_v_kernel(
         def quantise(grouped, codes, scales, x4):
             nc.vector.quantize_mx(out=codes.bitcast(x4), scales=scales, in_=grouped[:].rearrange("p w j -> p (w j)"))
 
-        def quantise_s(c):
+        def regroup_s(copy, c, half, grouped, cols):
+            src = (p0_sb, p1_sb)[half]
+            copy(out=grouped[:, cols, :].rearrange("p (q i) j -> p q j i", i=RUN), in_=regrouped(src[:, c, :, cols]))
+
+        def s_target(c, half, grouped):
+            cols = slice(half * S, (half + 1) * S)
+            return (grouped, s_codes[:, c, cols], s_scales[:, c, cols], E4M3X4)
+
+        def quantise_first_s():
             waiting = None
-            for half, src in enumerate((p0_sb, p1_sb)):
-                cols = slice(half * S, (half + 1) * S)
+            for half in range(2):
                 grouped = work.tile([P, S, PACK], BF16, align_bytes=64)
-                nc.vector.tensor_copy(
-                    out=grouped[:].rearrange("p (q i) j -> p q j i", i=RUN), in_=regrouped(src[:, c])
-                )
+                regroup_s(nc.vector.tensor_copy, 0, half, grouped, slice(0, S))
                 if waiting is not None:
                     quantise(*waiting)
-                waiting = (grouped, s_codes[:, c, cols], s_scales[:, c, cols], E4M3X4)
+                waiting = s_target(0, half, grouped)
             quantise(*waiting)
 
-        def form_da(c, piece, width):
-            cols = slice(piece * width, (piece + 1) * width)
-            grouped = work.tile([P, width, PACK], BF16, align_bytes=64)
+        second_s = {}
+
+        def regroup_second_s(quarter):
+            half = quarter // 2
+            if quarter % 2 == 0:
+                grouped = work.tile([P, S, PACK], BF16, align_bytes=64)
+                second_s[half] = s_target(1, half, grouped)
+            cols = slice((quarter % 2) * (S // 2), (quarter % 2 + 1) * (S // 2))
+            regroup_s(nc.scalar.copy, 1, half, second_s[half][0], cols)
+
+        unquantised = {}
+
+        def da_step(c, piece):
+            cols = slice(piece * DA_PIECE, (piece + 1) * DA_PIECE)
+            grouped = work.tile([P, DA_PIECE, PACK], BF16, align_bytes=64)
             tt(
                 grouped[:].rearrange("p (q i) j -> p q j i", i=RUN),
                 regrouped(g_sb[c][:, :, cols]),
                 regrouped(h_sb[c][:, :, cols]),
                 ALU.add,
             )
-            return (grouped, da_codes[:, c, cols], da_scales[:, c, cols], E5M2X4)
+            if "piece" in unquantised:
+                quantise(*unquantised["piece"])
+            unquantised["piece"] = (grouped, da_codes[:, c, cols], da_scales[:, c, cols], E5M2X4)
+
+        def fill(place):
+            if place < 2:
+                quantise(*second_s[place])
+            else:
+                da_step(0, place - 2)
 
         def prepare(k):
             bank = to_columns(shat_of(k, n_cols))
@@ -277,6 +327,8 @@ def tile_lngru2dcell_v_kernel(
             if fwd:
                 stt(rs2(f), gate(f, r_cols), 1.0, sn_banks[f][:], ALU.add, ALU.mult)
                 stt(t1(f), gate(f, l_cols), 1.0, d01_banks[f][:], ALU.add, ALU.mult)
+            else:
+                fill(0)
             if bwd:
                 nc.vector.tensor_scalar(
                     out=dve_sums[:, b, 8:9], in0=dve_sums[:, b, 2:3],
@@ -286,35 +338,45 @@ def tile_lngru2dcell_v_kernel(
                 stt(gate(f, n_cols), rs2(f), -0.5, gate(f, n_cols), ALU.mult, ALU.add)
                 nc.scalar.activation(out=gate(f, n_cols), in_=gate(f, n_cols), func=ACT.Tanh)
                 scale_columns(to_columns(rs2(f)), rs2(f), coef_of(BLOCK_R))
+            else:
+                fill(1)
             if bwd:
                 stt(hc(b), hc(b), dve_sums[:, b, 8:9], te(b), ALU.mult, ALU.add)
             if fwd:
                 stt(e_of(f), state(go_sb, f), 1.0, lnh_bc[:], ALU.mult, ALU.mult, accum_out=dve_sums[:, f, 1:2])
                 if f + 1 < CHUNKS:
                     prepare(f + 1)
+                if f // PACK == 1:
+                    regroup_second_s(f % PACK)
+            else:
+                fill(2)
             if bwd:
                 stt(e_of(b), gate(b, i_cols), -1.0, hc(b), ALU.add, ALU.mult)
                 stt(hc(b), gate(b, i_cols), 1.0, hc(b), ALU.add, ALU.mult)
-            if fwd:
-                tt(t3(f), state(p1_sb, f), gate(f, n_cols), ALU.subtract)
-            if bwd:
                 stt(gate(b, n_cols), gate(b, n_cols), -1.0, e_of(b), ALU.add, ALU.mult)
             if fwd:
-                stt(t3(f), t1(f), 0.5, t3(f), ALU.mult, ALU.add)
+                tt(t3(f), state(p1_sb, f), gate(f, n_cols), ALU.subtract)
+            else:
+                fill(3)
             if bwd:
                 stt(te(b), gate(b, r_cols), -1.0, gate(b, n_cols), ALU.add, ALU.mult)
             if fwd:
-                stt(t3(f), gate(f, i_cols), 1.0, t3(f), ALU.add, ALU.mult)
+                stt(t3(f), t1(f), 0.5, t3(f), ALU.mult, ALU.add)
+            else:
+                fill(4)
             if bwd:
                 stt(gate(b, n_cols), te(b), 1.0, sgn_bc[:], ALU.mult, ALU.mult, accum_out=dve_sums[:, b, 5:6])
             if fwd:
+                stt(t3(f), gate(f, i_cols), 1.0, t3(f), ALU.add, ALU.mult)
+                stt(t1(f), gate(f, l_cols), -1.0, t1(f), ALU.add, ALU.mult)
                 stt(hc(f), t3(f), 0.5, gate(f, n_cols), ALU.mult, ALU.add, accum_out=dve_sums[:, f, 0:1])
                 hidden_statistics(f)
-                scale_columns(to_columns(t3(f)), t3(f), coef_of(BLOCK_I))
-                stt(t1(f), gate(f, l_cols), -1.0, t1(f), ALU.add, ALU.mult)
                 scale_columns(to_columns(t1(f)), t1(f), coef_of(BLOCK_L))
-                nc.scalar.activation(out=gate(f, n_cols), in_=gate(f, n_cols), func=ACT.Square)
                 scaled_e(f)
+                scale_columns(to_columns(t3(f)), t3(f), coef_of(BLOCK_I))
+                nc.scalar.activation(out=gate(f, n_cols), in_=gate(f, n_cols), func=ACT.Square)
+            else:
+                fill(5)
             if bwd:
                 stt(gate(b, i_cols), i_factor[:], 1.0, e_of(b), ALU.mult, ALU.mult, accum_out=dve_sums[:, b, 3:4])
                 stt(gate(b, l_cols), l_factor[:], 1.0, hc(b), ALU.mult, ALU.mult, accum_out=dve_sums[:, b, 4:5])
@@ -325,46 +387,55 @@ def tile_lngru2dcell_v_kernel(
                     ALU.mult, ALU.mult, accum_out=dve_sums[:, b, 7:8],
                 )
                 mean_terms(b)
+            if not fwd:
+                fill(6)
 
         stages = {}
 
-        def multiply(m):
-            rows = slice(m * P, (m + 1) * P)
-            if m % STAGED == 0:
-                stage = work.tile([P, STAGED, 2 * S], F32, tag="tmp")
-                stages[m // STAGED] = stage
-            result = stages[m // STAGED][:, m % STAGED, :]
-            for half in range(2):
-                cols = slice(half * S, (half + 1) * S)
-                acc = psum.tile([P, S], F32, tag="bank")
-                for c in range(PASSES):
-                    nc.tensor.matmul_mx(
-                        out=acc[:],
-                        lhsT=da_codes[:, c, rows].bitcast(E5M2X4),
-                        lhsT_scale=da_scales[:, c, rows],
-                        rhs=s_codes[:, c, cols].bitcast(E4M3X4),
-                        rhs_scale=s_scales[:, c, cols],
-                        start=(c == 0),
-                        stop=(c == PASSES - 1),
-                    )
-                nc.scalar.copy(out=result[:, cols], in_=acc[:])
-            nc.sync.dma_start(out=out[rows, :], in_=result)
+        def multiply(piece):
+            blocks = range(piece * DA_PIECE // P, (piece + 1) * DA_PIECE // P)
+            banks = {}
+            for c in range(PASSES):
+                for m in blocks:
+                    for half in range(2):
+                        if c == 0:
+                            acc = psum.tile([P, S], F32, tag="bank")
+                            banks[(m, half)] = acc
+                        rows = slice(m * P, (m + 1) * P)
+                        cols = slice(half * S, (half + 1) * S)
+                        nc.tensor.matmul_mx(
+                            out=banks[(m, half)][:],
+                            lhsT=da_codes[:, c, rows].bitcast(E5M2X4),
+                            lhsT_scale=da_scales[:, c, rows],
+                            rhs=s_codes[:, c, cols].bitcast(E4M3X4),
+                            rhs_scale=s_scales[:, c, cols],
+                            start=(c == 0),
+                            stop=(c == PASSES - 1),
+                        )
+            for m in blocks:
+                if m % STAGED == 0:
+                    stage = work.tile([P, STAGED, 2 * S], F32, tag="tmp")
+                    stages[m // STAGED] = stage
+                result = stages[m // STAGED][:, m % STAGED, :]
+                for half in range(2):
+                    cols = slice(half * S, (half + 1) * S)
+                    if piece == PIECES - 1 and half == 1:
+                        nc.vector.tensor_copy(out=result[:, cols], in_=banks[(m, half)][:])
+                    else:
+                        nc.scalar.copy(out=result[:, cols], in_=banks[(m, half)][:])
+                nc.sync.dma_start(out=out[m * P : (m + 1) * P, :], in_=result)
 
         with tc.manual_schedule():
             prepare(0)
             round_of_work(0, None)
-            quantise_s(0)
+            quantise_first_s()
             for k in range(CHUNKS):
                 round_of_work(k + 1 if k + 1 < CHUNKS else None, k)
-                if k == 1:
-                    quantise_s(1)
-            waiting = None
-            for piece in range(GATES // DA_PIECE + 1):
+            for piece in range(PIECES):
                 for c in range(PASSES):
-                    formed = form_da(c, piece, DA_PIECE) if piece < GATES // DA_PIECE else None
-                    if waiting is not None:
-                        quantise(*waiting)
-                    waiting = formed
+                    if c > 0 or piece >= EARLY:
+                        da_step(c, piece)
                 if piece > 0:
-                    for m in range((piece - 1) * DA_PIECE // P, piece * DA_PIECE // P):
-                        multiply(m)
+                    multiply(piece - 1)
+            quantise(*unquantised["piece"])
+            multiply(PIECES - 1)

@@ -86,6 +86,7 @@ def tile_lngru2dcell_v_kernel(
         rs_pairs = keep.tile([P, CHUNKS, 2], F32)
         powers = keep.tile([P, 2], F32)
         eps_col = keep.tile([P, 1], F32)
+        unread_col = keep.tile([P, 1], F32)
         dve_sums = keep.tile([P, CHUNKS, 16], F32)
         act_stats = keep.tile([P, CHUNKS, 16], F32)
         pool_stats = keep.tile([P, CHUNKS, 2], F32)
@@ -105,21 +106,22 @@ def tile_lngru2dcell_v_kernel(
         def load_shat(c, j, cols):
             nc.sync.dma_start(out=h_sb[c][:, j, cols], in_=shat_v[c, :, j, cols])
 
-        def load_gates(c, j):
-            nc.sync.dma_start(out=g_sb[c][:, j, :], in_=gates_v[c, :, j, :])
+        def load_gates(c, j, cols):
+            nc.sync.dma_start(out=g_sb[c][:, j, cols], in_=gates_v[c, :, j, cols])
 
         def load_states(c, rows):
             for dst, src in ((p0_sb, p0_v), (p1_sb, p1_v), (go_sb, go_v)):
                 nc.sync.dma_start(out=dst[:, c, rows, :], in_=src[c, :, rows, :])
 
         load_shat(0, 0, n_cols)
-        load_gates(0, 0)
+        load_gates(0, 0, slice(0, 2 * S))
+        load_gates(0, 0, slice(2 * S, GATES))
         load_states(0, slice(0, 1))
         for c in range(PASSES):
             for j in range(PACK):
                 if c + j > 0:
                     load_shat(c, j, whole)
-                    load_gates(c, j)
+                    load_gates(c, j, whole)
                 if c == 0 and j == 1:
                     load_states(0, slice(1, PACK))
                     load_shat(0, 0, slice(0, 2 * S))
@@ -130,6 +132,7 @@ def tile_lngru2dcell_v_kernel(
         nc.gpsimd.memset(powers[:, 0:1], -0.5)
         nc.gpsimd.memset(powers[:, 1:2], -1.0)
         nc.gpsimd.memset(eps_col[:], EPS)
+        nc.scalar.activation(out=unread_col[:], in_=eps_col[:], func=ACT.Tanh)
         make_identity(nc, ident_f[:])
         make_identity(nc, ident_b[:])
         nc.vector.tensor_scalar_mul(out=neg_ident_b[:], in0=ident_b[:], scalar1=-1.0)
@@ -321,12 +324,11 @@ def tile_lngru2dcell_v_kernel(
                 temps[f] = tmp
             if bwd:
                 i_factor = to_rows(t3(b))
-                l_factor = to_rows(t1(b))
                 r_factor = to_rows(rs2(b))
+                l_factor = to_rows(t1(b))
                 stt(unread_v[:], e_of(b), 1.0, hc(b), ALU.mult, ALU.mult, accum_out=dve_sums[:, b, 2:3])
             if fwd:
                 stt(rs2(f), gate(f, r_cols), 1.0, sn_banks[f][:], ALU.add, ALU.mult)
-                stt(t1(f), gate(f, l_cols), 1.0, d01_banks[f][:], ALU.add, ALU.mult)
             else:
                 fill(0)
             if bwd:
@@ -335,15 +337,15 @@ def tile_lngru2dcell_v_kernel(
                     scalar1=pool_stats[:, b, 1:2], scalar2=act_stats[:, b, 5:6], op0=ALU.mult, op1=ALU.mult,
                 )
             if fwd:
-                stt(gate(f, n_cols), rs2(f), -0.5, gate(f, n_cols), ALU.mult, ALU.add)
-                nc.scalar.activation(out=gate(f, n_cols), in_=gate(f, n_cols), func=ACT.Tanh)
-                scale_columns(to_columns(rs2(f)), rs2(f), coef_of(BLOCK_R))
+                stt(t1(f), gate(f, l_cols), 1.0, d01_banks[f][:], ALU.add, ALU.mult)
             else:
                 fill(1)
             if bwd:
                 stt(hc(b), hc(b), dve_sums[:, b, 8:9], te(b), ALU.mult, ALU.add)
             if fwd:
-                stt(e_of(f), state(go_sb, f), 1.0, lnh_bc[:], ALU.mult, ALU.mult, accum_out=dve_sums[:, f, 1:2])
+                stt(gate(f, n_cols), rs2(f), -0.5, gate(f, n_cols), ALU.mult, ALU.add)
+                nc.scalar.activation(out=gate(f, n_cols), in_=gate(f, n_cols), func=ACT.Tanh)
+                scale_columns(to_columns(rs2(f)), rs2(f), coef_of(BLOCK_R))
                 if f + 1 < CHUNKS:
                     prepare(f + 1)
                 if f // PACK == 1:
@@ -368,19 +370,21 @@ def tile_lngru2dcell_v_kernel(
                 stt(gate(b, n_cols), te(b), 1.0, sgn_bc[:], ALU.mult, ALU.mult, accum_out=dve_sums[:, b, 5:6])
             if fwd:
                 stt(t3(f), gate(f, i_cols), 1.0, t3(f), ALU.add, ALU.mult)
-                stt(t1(f), gate(f, l_cols), -1.0, t1(f), ALU.add, ALU.mult)
+                stt(e_of(f), state(go_sb, f), 1.0, lnh_bc[:], ALU.mult, ALU.mult, accum_out=dve_sums[:, f, 1:2])
                 stt(hc(f), t3(f), 0.5, gate(f, n_cols), ALU.mult, ALU.add, accum_out=dve_sums[:, f, 0:1])
                 hidden_statistics(f)
-                scale_columns(to_columns(t1(f)), t1(f), coef_of(BLOCK_L))
-                scaled_e(f)
                 scale_columns(to_columns(t3(f)), t3(f), coef_of(BLOCK_I))
-                nc.scalar.activation(out=gate(f, n_cols), in_=gate(f, n_cols), func=ACT.Square)
-            else:
-                fill(5)
+                scaled_e(f)
             if bwd:
                 stt(gate(b, i_cols), i_factor[:], 1.0, e_of(b), ALU.mult, ALU.mult, accum_out=dve_sums[:, b, 3:4])
                 stt(gate(b, l_cols), l_factor[:], 1.0, hc(b), ALU.mult, ALU.mult, accum_out=dve_sums[:, b, 4:5])
                 stt(gate(b, r_cols), r_factor[:], 1.0, te(b), ALU.mult, ALU.mult, accum_out=dve_sums[:, b, 6:7])
+            if fwd:
+                stt(t1(f), gate(f, l_cols), -1.0, t1(f), ALU.add, ALU.mult)
+                scale_columns(to_columns(t1(f)), t1(f), coef_of(BLOCK_L))
+                nc.scalar.activation(out=gate(f, n_cols), in_=gate(f, n_cols), func=ACT.Square)
+            else:
+                fill(5)
             if bwd:
                 stt(
                     temps[b][:, 0:4, :].rearrange("p a w -> p (a w)"), gate(b, whole), 1.0, shat_of(b, whole),

@@ -22,11 +22,11 @@ CHUNKS = PASSES * PACK
 EPS = 1e-5
 DA_PIECE = 256
 PIECES = GATES // DA_PIECE
-EARLY = 5
-STAGED = 3
+EARLY = 2
+VECTOR_EMPTIES = 0
 RUN = 4
 
-BLOCK_COEF = (0.125, -0.25, -0.25, -0.125)
+BLOCK_COEF = (-0.25, 0.25, -0.25, -0.125)
 BLOCK_R = 0
 BLOCK_I = 1
 BLOCK_N = 2
@@ -61,7 +61,9 @@ def tile_lngru2dcell_v_kernel(
     with ExitStack() as ctx:
         keep = ctx.enter_context(tc.tile_pool(name="keep", bufs=1))
         work = ctx.enter_context(tc.tile_pool(name="work", bufs=2))
-        psum = ctx.enter_context(tc.psum_pool(name="psum", bufs=8))
+        psum_f = ctx.enter_context(tc.psum_pool(name="psum_f", bufs=3))
+        psum_n = ctx.enter_context(tc.psum_pool(name="psum_n", bufs=3))
+        psum_t = ctx.enter_context(tc.psum_pool(name="psum_t", bufs=2))
 
         g_sb = [keep.tile([P, PACK, GATES], F32, name="gates%d" % c) for c in range(PASSES)]
         h_sb = [keep.tile([P, PACK, GATES], F32, name="shat%d" % c) for c in range(PASSES)]
@@ -78,83 +80,91 @@ def tile_lngru2dcell_v_kernel(
         ident_b = keep.tile([P, P], BF16)
         neg_ident_b = keep.tile([P, P], BF16)
         vec_rows = keep.tile([P, P], BF16)
-        vec_cols = keep.tile([P, 5 * SQ], F32)
-        first_row = keep.tile([P, 2 * S], BF16)
-        ones_b = keep.tile([P, P], BF16)
+        vec_cols = keep.tile([P, 6 * SQ], F32)
         coef_cols = keep.tile([P, 4 * SQ], F32)
+        sn_cols = keep.tile([P, 2 * SQ], F32)
         rs_sb = keep.tile([P, CHUNKS], F32)
         rs_pairs = keep.tile([P, CHUNKS, 2], F32)
         powers = keep.tile([P, 2], F32)
         eps_col = keep.tile([P, 1], F32)
         unread_col = keep.tile([P, 1], F32)
-        dve_sums = keep.tile([P, CHUNKS, 16], F32)
+        dve_sums = keep.tile([P, CHUNKS, 8], F32)
         act_stats = keep.tile([P, CHUNKS, 16], F32)
         pool_stats = keep.tile([P, CHUNKS, 2], F32)
-        unread_v = keep.tile([P, S], F32)
         unread_a = keep.tile([P, S], BF16)
 
         nc.vector.memset(vec_rows[:], 0.0)
         nc.scalar.dma_start(out=vec_rows[0 : 4 * SQ, :], in_=lns_g.rearrange("(r w) -> r w", w=P))
         nc.scalar.dma_start(out=vec_rows[4 * SQ : 5 * SQ, :], in_=lns_b[n_cols].rearrange("(r w) -> r w", w=P))
-        nc.vector.memset(first_row[:], 0.0)
-        nc.scalar.dma_start(out=first_row[0:1, 0:S], in_=lnh_g.rearrange("(r w) -> r w", r=1))
-        nc.scalar.dma_start(out=first_row[0:1, S : 2 * S], in_=lns_g[n_cols].rearrange("(r w) -> r w", r=1))
+        nc.scalar.dma_start(out=vec_rows[5 * SQ : 6 * SQ, :], in_=lnh_g.rearrange("(r w) -> r w", w=P))
         nc.scalar.dma_start(
             out=rs_sb[:].rearrange("p (c j) -> p c j", j=PACK),
             in_=rstd_s.rearrange("(c p j) o -> p c (j o)", p=P, j=PACK),
         )
-        def load_shat(c, j, cols):
-            nc.sync.dma_start(out=h_sb[c][:, j, cols], in_=shat_v[c, :, j, cols])
 
-        def load_gates(c, j, cols):
-            nc.sync.dma_start(out=g_sb[c][:, j, cols], in_=gates_v[c, :, j, cols])
+        def load_shat(k, cols):
+            nc.sync.dma_start(out=h_sb[k // PACK][:, k % PACK, cols], in_=shat_v[k // PACK, :, k % PACK, cols])
+
+        def load_gates(k, cols):
+            nc.sync.dma_start(out=g_sb[k // PACK][:, k % PACK, cols], in_=gates_v[k // PACK, :, k % PACK, cols])
 
         def load_states(c, rows):
             for dst, src in ((p0_sb, p0_v), (p1_sb, p1_v), (go_sb, go_v)):
                 nc.sync.dma_start(out=dst[:, c, rows, :], in_=src[c, :, rows, :])
 
-        load_shat(0, 0, n_cols)
-        load_gates(0, 0, slice(0, 2 * S))
-        load_gates(0, 0, slice(2 * S, GATES))
-        load_states(0, slice(0, 1))
-        for c in range(PASSES):
-            for j in range(PACK):
-                if c + j > 0:
-                    load_shat(c, j, whole)
-                    load_gates(c, j, whole)
-                if c == 0 and j == 1:
-                    load_states(0, slice(1, PACK))
-                    load_shat(0, 0, slice(0, 2 * S))
-                    load_shat(0, 0, l_cols)
-                if c > 0 and j == 0:
-                    load_states(c, slice(0, PACK))
+        def load_rest_of_shat(k):
+            load_shat(k, slice(0, 2 * S))
+            load_shat(k, l_cols)
 
-        nc.gpsimd.memset(powers[:, 0:1], -0.5)
-        nc.gpsimd.memset(powers[:, 1:2], -1.0)
+        load_shat(0, n_cols)
+        load_gates(0, slice(0, 2 * S))
+        load_gates(0, slice(2 * S, GATES))
+        load_states(0, slice(0, 1))
+        load_shat(1, n_cols)
+        load_gates(1, whole)
+        load_states(0, slice(1, PACK))
+        load_shat(2, n_cols)
+        load_gates(2, whole)
+        load_rest_of_shat(0)
+        for k in range(3, CHUNKS):
+            load_shat(k, n_cols)
+            load_gates(k, whole)
+            if k == PACK - 1:
+                load_states(1, slice(0, PACK))
+            load_rest_of_shat(k - 2)
+        load_rest_of_shat(CHUNKS - 2)
+        load_rest_of_shat(CHUNKS - 1)
+
         nc.gpsimd.memset(eps_col[:], EPS)
         nc.scalar.activation(out=unread_col[:], in_=eps_col[:], func=ACT.Tanh)
         make_identity(nc, ident_f[:])
-        make_identity(nc, ident_b[:])
-        nc.vector.tensor_scalar_mul(out=neg_ident_b[:], in0=ident_b[:], scalar1=-1.0)
-        vec_bank = psum.tile([P, P], BF16, tag="bank")
+        nc.gpsimd.memset(powers[:, 0:1], -0.5)
+        nc.gpsimd.memset(powers[:, 1:2], -1.0)
+        nc.vector.tensor_copy(out=ident_b[:], in_=ident_f[:])
+        nc.vector.tensor_scalar_mul(out=neg_ident_b[:], in0=ident_f[:], scalar1=-1.0)
+        vec_bank = psum_t.tile([P, P], BF16, tag="bank")
         nc.tensor.transpose(vec_bank[:], vec_rows[:], ident_b[:])
-        nc.vector.tensor_copy(out=vec_cols[:], in_=vec_bank[:, 0 : 5 * SQ])
+        nc.vector.tensor_copy(out=vec_cols[:], in_=vec_bank[:, 0 : 6 * SQ])
+        nc.vector.tensor_scalar_mul(out=sn_cols[:, 0:SQ], in0=vec_cols[:, BLOCK_N * SQ : (BLOCK_N + 1) * SQ], scalar1=-0.5)
+        nc.vector.tensor_scalar_mul(out=sn_cols[:, SQ : 2 * SQ], in0=vec_cols[:, 4 * SQ : 5 * SQ], scalar1=-0.5)
         for b in range(4):
             sq = slice(b * SQ, (b + 1) * SQ)
             nc.vector.tensor_scalar_mul(out=coef_cols[:, sq], in0=vec_cols[:, sq], scalar1=BLOCK_COEF[b])
-        nc.vector.memset(ones_b[:], 1.0)
-        for half, (dst, factor) in enumerate(((lnh_bc, 1.0), (sgn_bc, BLOCK_COEF[BLOCK_N]))):
-            spread = psum.tile([P, S], F32, tag="bank")
-            nc.tensor.matmul(
-                out=spread[:], lhsT=ones_b[:], rhs=first_row[:, half * S : (half + 1) * S], start=True, stop=True
-            )
-            nc.vector.tensor_scalar_mul(out=dst[:], in0=spread[:], scalar1=factor)
         nc.vector.tensor_copy(out=rs_pairs[:, :, 0], in_=rs_sb[:])
         nc.vector.tensor_scalar_mul(out=rs_pairs[:, :, 1], in0=rs_sb[:], scalar1=-1.0 / S)
 
-        temps = {}
-        sn_banks = {}
-        d01_banks = {}
+        def spread(dst, first_col, factor):
+            bank = psum_f.tile([P, S], F32, tag="bank")
+            for q in range(SQ):
+                col = vec_cols[:, first_col + q : first_col + q + 1]
+                nc.tensor.transpose(bank[:, q * P : (q + 1) * P], col.to_broadcast([P, P]), ident_f[:])
+            nc.vector.tensor_scalar_mul(out=dst[:], in0=bank[:], scalar1=factor)
+
+        pairs = {}
+        quads = {}
+        sn_squares = {}
+        n_squares = {}
+        banks = {}
 
         def gate(k, cols):
             return g_sb[k // PACK][:, k % PACK, cols]
@@ -165,23 +175,23 @@ def tile_lngru2dcell_v_kernel(
         def state(p_sb, k):
             return p_sb[:, k // PACK, k % PACK, :]
 
-        def rs2(k):
-            return temps[k][:, 0, :]
+        def rs(k):
+            return pairs[k][:, 0, :]
 
         def t1(k):
-            return temps[k][:, 1, :]
+            return pairs[k][:, 1, :]
 
         def t3(k):
-            return temps[k][:, 2, :]
+            return quads[k][:, 0, :]
 
         def hc(k):
-            return temps[k][:, 3, :]
+            return quads[k][:, 1, :]
 
         def e_of(k):
-            return temps[k][:, 4, :]
+            return quads[k][:, 2, :]
 
         def te(k):
-            return temps[k][:, 5, :]
+            return quads[k][:, 3, :]
 
         def stt(out, in0, scalar, in1, op0, op1, accum_out=None):
             nc.vector.scalar_tensor_tensor(
@@ -191,16 +201,24 @@ def tile_lngru2dcell_v_kernel(
         def tt(out, in0, in1, op):
             nc.vector.tensor_tensor(out=out, in0=in0, in1=in1, op=op)
 
-        def to_columns(rows):
-            bank = psum.tile([P, S], F32, tag="bank")
-            for q in range(SQ):
-                sq = slice(q * P, (q + 1) * P)
+        def squares():
+            return [slice(q * P, (q + 1) * P) for q in range(SQ)]
+
+        def turn(pool, rows):
+            bank = pool.tile([P, S], F32, tag="bank")
+            for sq in squares():
                 nc.tensor.transpose(bank[:, sq], rows[:, sq], ident_f[:])
             return bank
 
+        def turn_sum(pool, rows_a, rows_b):
+            bank = pool.tile([P, S], F32, tag="bank")
+            for sq in squares():
+                nc.tensor.matmul(out=bank[:, sq], lhsT=rows_a[:, sq], rhs=ident_f[:], is_transpose=True, start=True, stop=False)
+                nc.tensor.matmul(out=bank[:, sq], lhsT=rows_b[:, sq], rhs=ident_f[:], is_transpose=True, start=False, stop=True)
+            return bank
+
         def scale_columns(bank, dst, scale_cols, bias_cols=None):
-            for q in range(SQ):
-                sq = slice(q * P, (q + 1) * P)
+            for q, sq in enumerate(squares()):
                 if bias_cols is None:
                     nc.scalar.activation(out=dst[:, sq], in_=bank[:, sq], func=ACT.Copy, scale=scale_cols[:, q : q + 1])
                 else:
@@ -208,9 +226,6 @@ def tile_lngru2dcell_v_kernel(
                         out=dst[:, sq], in_=bank[:, sq], func=ACT.Identity,
                         scale=scale_cols[:, q : q + 1], bias=bias_cols[:, q : q + 1],
                     )
-
-        def to_rows(squares):
-            return to_columns(squares)
 
         def coef_of(block):
             return coef_cols[:, block * SQ : (block + 1) * SQ]
@@ -264,25 +279,51 @@ def tile_lngru2dcell_v_kernel(
                 quantise(*unquantised["piece"])
             unquantised["piece"] = (grouped, da_codes[:, c, cols], da_scales[:, c, cols], E5M2X4)
 
-        def fill(place):
-            if place < 2:
-                quantise(*second_s[place])
-            else:
-                da_step(0, place - 2)
+        fillers = [lambda: quantise(*second_s[0]), lambda: quantise(*second_s[1])]
+        fillers.extend([(lambda piece=piece: da_step(0, piece)) for piece in range(EARLY)])
 
-        def prepare(k):
-            bank = to_columns(shat_of(k, n_cols))
+        counts = {"fill": 0, "acc": 0}
+
+        def fill():
+            if counts["fill"] < len(fillers):
+                fillers[counts["fill"]]()
+                counts["fill"] = counts["fill"] + 1
+
+        def ok(k):
+            return 0 <= k < CHUNKS
+
+        def tanh_of_gates(k):
             nc.scalar.activation(out=gate(k, slice(0, 2 * S)), in_=gate(k, slice(0, 2 * S)), func=ACT.Tanh, scale=0.5)
             nc.scalar.activation(out=gate(k, l_cols), in_=gate(k, l_cols), func=ACT.Tanh, scale=0.5)
-            sn_squares = work.tile([P, S], F32)
-            scale_columns(bank, sn_squares, vec_cols[:, BLOCK_N * SQ : (BLOCK_N + 1) * SQ], vec_cols[:, 4 * SQ : 5 * SQ])
-            diff = psum.tile([P, S], F32, tag="bank")
+
+        def sn_to_columns(k):
+            bank = turn(psum_t, shat_of(k, n_cols))
+            sn_sq = work.tile([P, S], F32)
+            sn_squares[k] = sn_sq
+            scale_columns(bank, sn_sq, sn_cols[:, 0:SQ], sn_cols[:, SQ : 2 * SQ])
+
+        def sn_and_difference(k):
+            banks[("sn", k)] = turn(psum_n, sn_squares[k])
+            diff = psum_n.tile([P, S], F32, tag="bank")
             nc.tensor.matmul(out=diff[:], lhsT=ident_b[:], rhs=state(p0_sb, k), start=True, stop=False)
             nc.tensor.matmul(out=diff[:], lhsT=neg_ident_b[:], rhs=state(p1_sb, k), start=False, stop=True)
-            d01_banks[k] = diff
-            sn_banks[k] = to_rows(sn_squares)
+            banks[("d01", k)] = diff
 
-        def hidden_statistics(k):
+        def candidate(k):
+            bank = turn_sum(psum_t, gate(k, n_cols), rs(k))
+            n_sq = work.tile([P, S], F32)
+            n_squares[k] = n_sq
+            nc.scalar.activation(out=n_sq[:], in_=bank[:], func=ACT.Tanh)
+
+        def candidate_to_rows(k):
+            banks[("n", k)] = turn(psum_n, n_squares[k])
+            bank = psum_n.tile([P, S], F32, tag="bank")
+            for sq in squares():
+                nc.tensor.matmul(out=bank[:, sq], lhsT=neg_ident_b[:], rhs=state(p1_sb, k)[:, sq], start=True, stop=False)
+                nc.tensor.matmul(out=bank[:, sq], lhsT=n_squares[k][:, sq], rhs=ident_f[:], is_transpose=True, start=False, stop=True)
+            banks[("np", k)] = bank
+
+        def variance(k):
             neg_mu = act_stats[:, k, 0:1]
             ssq = act_stats[:, k, 1:2]
             var_eps = act_stats[:, k, 2:3]
@@ -292,21 +333,32 @@ def tile_lngru2dcell_v_kernel(
             nc.gpsimd.tensor_tensor(
                 out=pool_stats[:, k, 0:2], in0=var_eps.to_broadcast([P, 2]), in1=powers[:], op=ALU.pow
             )
-            nc.scalar.activation(out=hc(k), in_=hc(k), func=ACT.Identity, bias=neg_mu, scale=1.0)
+
+        def covariance(k):
+            nc.scalar.activation(
+                out=act_stats[:, k, 3:4], in_=dve_sums[:, k, 1:2], func=ACT.Identity,
+                scale=act_stats[:, k, 0:1], bias=dve_sums[:, k, 2:3],
+            )
 
         def scaled_e(k):
+            neg_mu = act_stats[:, k, 0:1]
+            rh = pool_stats[:, k, 0:1]
+            rh2 = pool_stats[:, k, 1:2]
             a = act_stats[:, k, 4:5]
             a_neg = act_stats[:, k, 5:6]
-            d = act_stats[:, k, 6:7]
-            nc.scalar.activation(out=act_stats[:, k, 4:6], in_=rs_pairs[:, k, :], func=ACT.Copy, scale=pool_stats[:, k, 0:1])
-            nc.scalar.activation(out=d, in_=dve_sums[:, k, 1:2], func=ACT.Copy, scale=a_neg)
-            nc.scalar.activation(out=te(k), in_=e_of(k), func=ACT.Identity, bias=d, scale=a)
+            nc.scalar.activation(out=act_stats[:, k, 6:7], in_=act_stats[:, k, 3:4], func=ACT.Copy, scale=rh2)
+            nc.scalar.activation(
+                out=act_stats[:, k, 7:8], in_=act_stats[:, k, 6:7], func=ACT.Identity, scale=neg_mu, bias=dve_sums[:, k, 1:2]
+            )
+            nc.scalar.activation(out=act_stats[:, k, 4:6], in_=rs_pairs[:, k, :], func=ACT.Copy, scale=rh)
+            nc.scalar.activation(out=act_stats[:, k, 8:10], in_=act_stats[:, k, 6:8], func=ACT.Copy, scale=a_neg)
+            nc.scalar.activation(out=te(k), in_=e_of(k), func=ACT.Identity, bias=act_stats[:, k, 9:10], scale=a)
 
         def mean_terms(k):
-            neg_mean_f = act_stats[:, k, 8:9]
-            neg_mean_fs = act_stats[:, k, 9:10]
+            neg_mean_f = act_stats[:, k, 10:11]
+            neg_mean_fs = act_stats[:, k, 11:12]
             nc.scalar.activation(
-                out=act_stats[:, k, 10:14], in_=dve_sums[:, k, 3:7], func=ACT.Copy, scale=-1.0 / GATES,
+                out=act_stats[:, k, 12:16], in_=dve_sums[:, k, 3:7], func=ACT.Copy, scale=-1.0 / GATES,
                 accum_out=neg_mean_f,
             )
             nc.scalar.mul(out=neg_mean_fs, in_=dve_sums[:, k, 7:8], mul=-1.0 / GATES)
@@ -316,99 +368,138 @@ def tile_lngru2dcell_v_kernel(
                     out=shat_of(k, cols), in_=shat_of(k, cols), func=ACT.Identity, bias=neg_mean_f, scale=neg_mean_fs
                 )
 
-        def round_of_work(f, b):
-            fwd = f is not None
-            bwd = b is not None
-            if fwd:
-                tmp = work.tile([P, 6, S], F32)
-                temps[f] = tmp
-            if bwd:
-                i_factor = to_rows(t3(b))
-                r_factor = to_rows(rs2(b))
-                l_factor = to_rows(t1(b))
-                stt(unread_v[:], e_of(b), 1.0, hc(b), ALU.mult, ALU.mult, accum_out=dve_sums[:, b, 2:3])
-            if fwd:
-                stt(rs2(f), gate(f, r_cols), 1.0, sn_banks[f][:], ALU.add, ALU.mult)
-            else:
-                fill(0)
-            if bwd:
-                nc.vector.tensor_scalar(
-                    out=dve_sums[:, b, 8:9], in0=dve_sums[:, b, 2:3],
-                    scalar1=pool_stats[:, b, 1:2], scalar2=act_stats[:, b, 5:6], op0=ALU.mult, op1=ALU.mult,
-                )
-            if fwd:
-                stt(t1(f), gate(f, l_cols), 1.0, d01_banks[f][:], ALU.add, ALU.mult)
-            else:
-                fill(1)
-            if bwd:
-                stt(hc(b), hc(b), dve_sums[:, b, 8:9], te(b), ALU.mult, ALU.add)
-            if fwd:
-                stt(gate(f, n_cols), rs2(f), -0.5, gate(f, n_cols), ALU.mult, ALU.add)
-                nc.scalar.activation(out=gate(f, n_cols), in_=gate(f, n_cols), func=ACT.Tanh)
-                scale_columns(to_columns(rs2(f)), rs2(f), coef_of(BLOCK_R))
-                if f + 1 < CHUNKS:
-                    prepare(f + 1)
-                if f // PACK == 1:
-                    regroup_second_s(f % PACK)
-            else:
-                fill(2)
-            if bwd:
-                stt(e_of(b), gate(b, i_cols), -1.0, hc(b), ALU.add, ALU.mult)
-                stt(hc(b), gate(b, i_cols), 1.0, hc(b), ALU.add, ALU.mult)
-                stt(gate(b, n_cols), gate(b, n_cols), -1.0, e_of(b), ALU.add, ALU.mult)
-            if fwd:
-                tt(t3(f), state(p1_sb, f), gate(f, n_cols), ALU.subtract)
-            else:
-                fill(3)
-            if bwd:
-                stt(te(b), gate(b, r_cols), -1.0, gate(b, n_cols), ALU.add, ALU.mult)
-            if fwd:
-                stt(t3(f), t1(f), 0.5, t3(f), ALU.mult, ALU.add)
-            else:
-                fill(4)
-            if bwd:
-                stt(gate(b, n_cols), te(b), 1.0, sgn_bc[:], ALU.mult, ALU.mult, accum_out=dve_sums[:, b, 5:6])
-            if fwd:
-                stt(t3(f), gate(f, i_cols), 1.0, t3(f), ALU.add, ALU.mult)
-                stt(e_of(f), state(go_sb, f), 1.0, lnh_bc[:], ALU.mult, ALU.mult, accum_out=dve_sums[:, f, 1:2])
-                stt(hc(f), t3(f), 0.5, gate(f, n_cols), ALU.mult, ALU.add, accum_out=dve_sums[:, f, 0:1])
-                hidden_statistics(f)
-                scale_columns(to_columns(t3(f)), t3(f), coef_of(BLOCK_I))
-                scaled_e(f)
-            if bwd:
-                stt(gate(b, i_cols), i_factor[:], 1.0, e_of(b), ALU.mult, ALU.mult, accum_out=dve_sums[:, b, 3:4])
-                stt(gate(b, l_cols), l_factor[:], 1.0, hc(b), ALU.mult, ALU.mult, accum_out=dve_sums[:, b, 4:5])
-                stt(gate(b, r_cols), r_factor[:], 1.0, te(b), ALU.mult, ALU.mult, accum_out=dve_sums[:, b, 6:7])
-            if fwd:
-                stt(t1(f), gate(f, l_cols), -1.0, t1(f), ALU.add, ALU.mult)
-                scale_columns(to_columns(t1(f)), t1(f), coef_of(BLOCK_L))
-                nc.scalar.activation(out=gate(f, n_cols), in_=gate(f, n_cols), func=ACT.Square)
-            else:
-                fill(5)
-            if bwd:
-                stt(
-                    temps[b][:, 0:4, :].rearrange("p a w -> p (a w)"), gate(b, whole), 1.0, shat_of(b, whole),
-                    ALU.mult, ALU.mult, accum_out=dve_sums[:, b, 7:8],
-                )
-                mean_terms(b)
-            if not fwd:
-                fill(6)
+        f_banks = {}
 
-        stages = {}
+        def round_of_work(r, order):
+            k0, k1, k2, k3 = r, r + 1, r + 2, r + 3
+
+            def t0():
+                f_banks["i"] = turn(psum_f, t3(k0))
+                f_banks["l"] = turn(psum_f, t1(k0))
+                f_banks["r"] = turn(psum_f, rs(k0))
+
+            def t1_():
+                nc.scalar.activation(out=gate(k1, n_cols), in_=banks[("n", k1)][:], func=ACT.Square)
+
+            def f1():
+                quad = work.tile([P, 4, S], F32)
+                quads[k1] = quad
+                stt(e_of(k1), state(go_sb, k1), 1.0, lnh_bc[:], ALU.mult, ALU.mult, accum_out=dve_sums[:, k1, 1:2])
+
+            def f2():
+                stt(t3(k1), t1(k1), -0.5, banks[("np", k1)][:], ALU.mult, ALU.add)
+
+            def f3():
+                stt(t3(k1), gate(k1, i_cols), 1.0, t3(k1), ALU.add, ALU.mult)
+
+            def f4():
+                stt(hc(k1), t3(k1), -0.5, banks[("n", k1)][:], ALU.mult, ALU.add, accum_out=dve_sums[:, k1, 0:1])
+                variance(k1)
+                scale_columns(turn(psum_t, t3(k1)), t3(k1), coef_of(BLOCK_I))
+
+            def f5():
+                stt(te(k1), e_of(k1), 1.0, hc(k1), ALU.mult, ALU.mult, accum_out=dve_sums[:, k1, 2:3])
+                covariance(k1)
+
+            def f6():
+                stt(t1(k1), gate(k1, l_cols), -1.0, t1(k1), ALU.add, ALU.mult)
+                scale_columns(turn(psum_t, t1(k1)), t1(k1), coef_of(BLOCK_L))
+
+            def g1():
+                pair = work.tile([P, 2, S], F32)
+                pairs[k2] = pair
+                stt(rs(k2), gate(k2, r_cols), 1.0, banks[("sn", k2)][:], ALU.add, ALU.mult)
+                candidate(k2)
+                scale_columns(turn(psum_t, rs(k2)), rs(k2), coef_of(BLOCK_R))
+
+            def g2():
+                stt(t1(k2), gate(k2, l_cols), 1.0, banks[("d01", k2)][:], ALU.add, ALU.mult)
+
+            def x2():
+                if ok(k3):
+                    tanh_of_gates(k3)
+                elif r in (CHUNKS - 3, CHUNKS - 2):
+                    regroup_second_s(2 * (r - (CHUNKS - 3)))
+                    regroup_second_s(2 * (r - (CHUNKS - 3)) + 1)
+
+            def b1():
+                stt(hc(k0), hc(k0), act_stats[:, k0, 8:9], te(k0), ALU.mult, ALU.add)
+
+            def b2():
+                stt(e_of(k0), gate(k0, i_cols), -1.0, hc(k0), ALU.add, ALU.mult)
+
+            def b3():
+                stt(hc(k0), gate(k0, i_cols), 1.0, hc(k0), ALU.add, ALU.mult)
+
+            def b4():
+                stt(gate(k0, n_cols), gate(k0, n_cols), -1.0, e_of(k0), ALU.add, ALU.mult)
+
+            def b5():
+                stt(te(k0), gate(k0, r_cols), -1.0, gate(k0, n_cols), ALU.add, ALU.mult)
+
+            def b6():
+                stt(gate(k0, i_cols), f_banks["i"][:], 1.0, e_of(k0), ALU.mult, ALU.mult, accum_out=dve_sums[:, k0, 3:4])
+
+            def b7():
+                stt(gate(k0, l_cols), f_banks["l"][:], 1.0, hc(k0), ALU.mult, ALU.mult, accum_out=dve_sums[:, k0, 4:5])
+
+            def b8():
+                stt(gate(k0, r_cols), f_banks["r"][:], 1.0, te(k0), ALU.mult, ALU.mult, accum_out=dve_sums[:, k0, 6:7])
+
+            def b9():
+                stt(gate(k0, n_cols), te(k0), 1.0, sgn_bc[:], ALU.mult, ALU.mult, accum_out=dve_sums[:, k0, 5:6])
+
+            def b10():
+                stt(
+                    quads[k0][:].rearrange("p a w -> p (a w)"), gate(k0, whole), 1.0, shat_of(k0, whole),
+                    ALU.mult, ALU.mult, accum_out=dve_sums[:, k0, 7:8],
+                )
+
+            table = {
+                "T0": (k0, t0), "T1": (k1, t1_), "T2": (k0 - 1, lambda: mean_terms(k0 - 1)),
+                "F1": (k1, f1), "F2": (k1, f2), "F3": (k1, f3), "F4": (k1, f4), "F5": (k1, f5), "F6": (k1, f6),
+                "G1": (k2, g1), "G2": (k2, g2),
+                "X1": (k2, lambda: sn_and_difference(k2)), "X2": (0, x2), "X3": (k1, lambda: scaled_e(k1)),
+                "X4": (k3, lambda: sn_to_columns(k3)), "X5": (k2, lambda: candidate_to_rows(k2)),
+                "B1": (k0, b1), "B2": (k0, b2), "B3": (k0, b3), "B4": (k0, b4), "B5": (k0, b5), "B6": (k0, b6),
+                "B7": (k0, b7), "B8": (k0, b8), "B9": (k0, b9), "B10": (k0, b10),
+            }
+            for name in order.split():
+                chunk, step = table[name]
+                if ok(chunk):
+                    step()
+                elif name[0] in "FG" and r >= CHUNKS - 2:
+                    fill()
+
+        acc_pools = (psum_f, psum_f, psum_f, psum_n, psum_n, psum_n, psum_t, psum_t)
+        FIRST_SLOTS = 6
+        assert (FIRST_SLOTS // 2 + 2) * DA_PIECE >= 2 * S
+        late_slots = [t[:, j, 0 : 2 * S] for t in (g_sb[0], h_sb[0], g_sb[1], h_sb[1]) for j in range(PACK)]
+        first_slots = []
+
+        def slot(m):
+            if m >= FIRST_SLOTS:
+                return late_slots[m - FIRST_SLOTS]
+            if m % 3 == 0:
+                quad = work.tile([P, 2, 2 * S], F32)
+                pair = work.tile([P, 1, 2 * S], F32)
+                first_slots.extend([quad[:, 0, :], quad[:, 1, :], pair[:, 0, :]])
+            return first_slots[m]
 
         def multiply(piece):
             blocks = range(piece * DA_PIECE // P, (piece + 1) * DA_PIECE // P)
-            banks = {}
+            accs = {}
             for c in range(PASSES):
                 for m in blocks:
                     for half in range(2):
                         if c == 0:
-                            acc = psum.tile([P, S], F32, tag="bank")
-                            banks[(m, half)] = acc
+                            acc = acc_pools[counts["acc"] % len(acc_pools)].tile([P, S], F32, tag="bank")
+                            counts["acc"] = counts["acc"] + 1
+                            accs[(m, half)] = acc
                         rows = slice(m * P, (m + 1) * P)
                         cols = slice(half * S, (half + 1) * S)
                         nc.tensor.matmul_mx(
-                            out=banks[(m, half)][:],
+                            out=accs[(m, half)][:],
                             lhsT=da_codes[:, c, rows].bitcast(E5M2X4),
                             lhsT_scale=da_scales[:, c, rows],
                             rhs=s_codes[:, c, cols].bitcast(E4M3X4),
@@ -417,24 +508,26 @@ def tile_lngru2dcell_v_kernel(
                             stop=(c == PASSES - 1),
                         )
             for m in blocks:
-                if m % STAGED == 0:
-                    stage = work.tile([P, STAGED, 2 * S], F32, tag="tmp")
-                    stages[m // STAGED] = stage
-                result = stages[m // STAGED][:, m % STAGED, :]
+                result = slot(m)
                 for half in range(2):
                     cols = slice(half * S, (half + 1) * S)
-                    if piece == PIECES - 1 and half == 1:
-                        nc.vector.tensor_copy(out=result[:, cols], in_=banks[(m, half)][:])
+                    if half == 1 and (piece == PIECES - 1 or (m % 2 == 1 and piece >= PIECES - VECTOR_EMPTIES)):
+                        nc.vector.tensor_copy(out=result[:, cols], in_=accs[(m, half)][:])
                     else:
-                        nc.scalar.copy(out=result[:, cols], in_=banks[(m, half)][:])
+                        nc.scalar.copy(out=result[:, cols], in_=accs[(m, half)][:])
                 nc.sync.dma_start(out=out[m * P : (m + 1) * P, :], in_=result)
 
+        steady = "T0 T1 T2 F1 B1 F2 B2 F3 B3 F4 X1 B4 F5 X2 X3 B5 F6 B6 G1 X4 X5 B7 G2 B8 B9 B10"
         with tc.manual_schedule():
-            prepare(0)
-            round_of_work(0, None)
+            round_of_work(-3, "X4 X2")
+            spread(lnh_bc, 5 * SQ, 1.0)
+            spread(sgn_bc, BLOCK_N * SQ, BLOCK_COEF[BLOCK_N])
+            round_of_work(-2, "X1 G1 X5 G2 X4 X2")
+            round_of_work(-1, "T1 F1 F2 F3 F4 X1 F5 F6 G1 X5 G2 X3 X4 X2")
             quantise_first_s()
-            for k in range(CHUNKS):
-                round_of_work(k + 1 if k + 1 < CHUNKS else None, k)
+            for r in range(CHUNKS):
+                round_of_work(r, steady)
+            mean_terms(CHUNKS - 1)
             for piece in range(PIECES):
                 for c in range(PASSES):
                     if c > 0 or piece >= EARLY:

@@ -24,9 +24,10 @@ DA_PIECE = 256
 PIECES = GATES // DA_PIECE
 EARLY = 2
 VECTOR_EMPTIES = 0
+DIRECT = 2
 RUN = 4
 
-BLOCK_COEF = (-0.25, 0.25, -0.25, -0.125)
+BLOCK_COEF = (-0.25, 0.25, -0.25, 0.25)
 BLOCK_R = 0
 BLOCK_I = 1
 BLOCK_N = 2
@@ -61,9 +62,13 @@ def tile_lngru2dcell_v_kernel(
     with ExitStack() as ctx:
         keep = ctx.enter_context(tc.tile_pool(name="keep", bufs=1))
         work = ctx.enter_context(tc.tile_pool(name="work", bufs=2))
-        psum_f = ctx.enter_context(tc.psum_pool(name="psum_f", bufs=3))
-        psum_n = ctx.enter_context(tc.psum_pool(name="psum_n", bufs=3))
-        psum_t = ctx.enter_context(tc.psum_pool(name="psum_t", bufs=2))
+        psum = ctx.enter_context(tc.psum_pool(name="psum", bufs=1))
+        BANKS = {"d01": 1, "n": 1, "np": 1, "f": 3, "t": 2}
+
+        def bank_of(role, shape=(P, S), dtype=F32):
+            bank = psum.tile(list(shape), dtype, tag=role, bufs=BANKS[role])
+            return bank
+
 
         g_sb = [keep.tile([P, PACK, GATES], F32, name="gates%d" % c) for c in range(PASSES)]
         h_sb = [keep.tile([P, PACK, GATES], F32, name="shat%d" % c) for c in range(PASSES)]
@@ -79,6 +84,8 @@ def tile_lngru2dcell_v_kernel(
         ident_f = keep.tile([P, P], F32)
         ident_b = keep.tile([P, P], BF16)
         neg_ident_b = keep.tile([P, P], BF16)
+        half_ident_b = keep.tile([P, P], BF16)
+        neg_half_ident_b = keep.tile([P, P], BF16)
         vec_rows = keep.tile([P, P], BF16)
         vec_cols = keep.tile([P, 6 * SQ], F32)
         coef_cols = keep.tile([P, 4 * SQ], F32)
@@ -142,7 +149,9 @@ def tile_lngru2dcell_v_kernel(
         nc.gpsimd.memset(powers[:, 1:2], -1.0)
         nc.vector.tensor_copy(out=ident_b[:], in_=ident_f[:])
         nc.vector.tensor_scalar_mul(out=neg_ident_b[:], in0=ident_f[:], scalar1=-1.0)
-        vec_bank = psum_t.tile([P, P], BF16, tag="bank")
+        nc.vector.tensor_scalar_mul(out=half_ident_b[:], in0=ident_f[:], scalar1=0.5)
+        nc.vector.tensor_scalar_mul(out=neg_half_ident_b[:], in0=ident_f[:], scalar1=-0.5)
+        vec_bank = bank_of("t", (P, P), BF16)
         nc.tensor.transpose(vec_bank[:], vec_rows[:], ident_b[:])
         nc.vector.tensor_copy(out=vec_cols[:], in_=vec_bank[:, 0 : 6 * SQ])
         nc.vector.tensor_scalar_mul(out=sn_cols[:, 0:SQ], in0=vec_cols[:, BLOCK_N * SQ : (BLOCK_N + 1) * SQ], scalar1=-0.5)
@@ -154,7 +163,7 @@ def tile_lngru2dcell_v_kernel(
         nc.vector.tensor_scalar_mul(out=rs_pairs[:, :, 1], in0=rs_sb[:], scalar1=-1.0 / S)
 
         def spread(dst, first_col, factor):
-            bank = psum_f.tile([P, S], F32, tag="bank")
+            bank = bank_of("f")
             for q in range(SQ):
                 col = vec_cols[:, first_col + q : first_col + q + 1]
                 nc.tensor.transpose(bank[:, q * P : (q + 1) * P], col.to_broadcast([P, P]), ident_f[:])
@@ -193,6 +202,9 @@ def tile_lngru2dcell_v_kernel(
         def te(k):
             return quads[k][:, 3, :]
 
+        def n_of(k):
+            return gate(k, n_cols) if k < DIRECT else banks[("n", k)][:]
+
         def stt(out, in0, scalar, in1, op0, op1, accum_out=None):
             nc.vector.scalar_tensor_tensor(
                 out=out, in0=in0, scalar=scalar, in1=in1, op0=op0, op1=op1, accum_out=accum_out
@@ -204,14 +216,14 @@ def tile_lngru2dcell_v_kernel(
         def squares():
             return [slice(q * P, (q + 1) * P) for q in range(SQ)]
 
-        def turn(pool, rows):
-            bank = pool.tile([P, S], F32, tag="bank")
+        def turn(role, rows):
+            bank = bank_of(role)
             for sq in squares():
                 nc.tensor.transpose(bank[:, sq], rows[:, sq], ident_f[:])
             return bank
 
-        def turn_sum(pool, rows_a, rows_b):
-            bank = pool.tile([P, S], F32, tag="bank")
+        def turn_sum(role, rows_a, rows_b):
+            bank = bank_of(role)
             for sq in squares():
                 nc.tensor.matmul(out=bank[:, sq], lhsT=rows_a[:, sq], rhs=ident_f[:], is_transpose=True, start=True, stop=False)
                 nc.tensor.matmul(out=bank[:, sq], lhsT=rows_b[:, sq], rhs=ident_f[:], is_transpose=True, start=False, stop=True)
@@ -266,7 +278,7 @@ def tile_lngru2dcell_v_kernel(
 
         unquantised = {}
 
-        def da_step(c, piece):
+        def form_da(c, piece):
             cols = slice(piece * DA_PIECE, (piece + 1) * DA_PIECE)
             grouped = work.tile([P, DA_PIECE, PACK], BF16, align_bytes=64)
             tt(
@@ -275,13 +287,23 @@ def tile_lngru2dcell_v_kernel(
                 regrouped(h_sb[c][:, :, cols]),
                 ALU.add,
             )
+            return (grouped, da_codes[:, c, cols], da_scales[:, c, cols], E5M2X4)
+
+        def da_step(c, piece):
+            formed = form_da(c, piece)
             if "piece" in unquantised:
                 quantise(*unquantised["piece"])
-            unquantised["piece"] = (grouped, da_codes[:, c, cols], da_scales[:, c, cols], E5M2X4)
+            unquantised["piece"] = formed
 
-        fillers = [lambda: quantise(*second_s[0]), lambda: quantise(*second_s[1])]
-        fillers.extend([(lambda piece=piece: da_step(0, piece)) for piece in range(EARLY)])
+        def early_form(piece):
+            unquantised["early"] = form_da(0, piece)
 
+        fillers = [lambda: quantise(*second_s[0])]
+        for early in range(EARLY):
+            fillers.append(lambda piece=early: early_form(piece))
+            fillers.append(lambda: quantise(*unquantised["early"]))
+            if early == 0:
+                fillers.append(lambda: quantise(*second_s[1]))
         counts = {"fill": 0, "acc": 0}
 
         def fill():
@@ -294,34 +316,44 @@ def tile_lngru2dcell_v_kernel(
 
         def tanh_of_gates(k):
             nc.scalar.activation(out=gate(k, slice(0, 2 * S)), in_=gate(k, slice(0, 2 * S)), func=ACT.Tanh, scale=0.5)
-            nc.scalar.activation(out=gate(k, l_cols), in_=gate(k, l_cols), func=ACT.Tanh, scale=0.5)
+            nc.scalar.activation(out=gate(k, l_cols), in_=turn("t", gate(k, l_cols))[:], func=ACT.Tanh, scale=0.5)
 
         def sn_to_columns(k):
-            bank = turn(psum_t, shat_of(k, n_cols))
+            bank = turn("t", shat_of(k, n_cols))
             sn_sq = work.tile([P, S], F32)
             sn_squares[k] = sn_sq
             scale_columns(bank, sn_sq, sn_cols[:, 0:SQ], sn_cols[:, SQ : 2 * SQ])
 
-        def sn_and_difference(k):
-            banks[("sn", k)] = turn(psum_n, sn_squares[k])
-            diff = psum_n.tile([P, S], F32, tag="bank")
-            nc.tensor.matmul(out=diff[:], lhsT=ident_b[:], rhs=state(p0_sb, k), start=True, stop=False)
-            nc.tensor.matmul(out=diff[:], lhsT=neg_ident_b[:], rhs=state(p1_sb, k), start=False, stop=True)
+        def sn_to_rows(k):
+            banks[("sn", k)] = turn("f", sn_squares[k])
+
+        def difference(k):
+            diff = bank_of("d01")
+            for sq in squares():
+                nc.tensor.matmul(out=diff[:, sq], lhsT=state(p0_sb, k)[:, sq], rhs=neg_half_ident_b[:], start=True, stop=False)
+                nc.tensor.matmul(out=diff[:, sq], lhsT=state(p1_sb, k)[:, sq], rhs=half_ident_b[:], start=False, stop=True)
             banks[("d01", k)] = diff
 
         def candidate(k):
-            bank = turn_sum(psum_t, gate(k, n_cols), rs(k))
+            bank = turn_sum("t", gate(k, n_cols), rs(k))
             n_sq = work.tile([P, S], F32)
             n_squares[k] = n_sq
             nc.scalar.activation(out=n_sq[:], in_=bank[:], func=ACT.Tanh)
 
         def candidate_to_rows(k):
-            banks[("n", k)] = turn(psum_n, n_squares[k])
-            bank = psum_n.tile([P, S], F32, tag="bank")
+            bank = bank_of("np")
             for sq in squares():
                 nc.tensor.matmul(out=bank[:, sq], lhsT=neg_ident_b[:], rhs=state(p1_sb, k)[:, sq], start=True, stop=False)
-                nc.tensor.matmul(out=bank[:, sq], lhsT=n_squares[k][:, sq], rhs=ident_f[:], is_transpose=True, start=False, stop=True)
+                nc.tensor.matmul(
+                    out=bank[:, sq], lhsT=t1(k)[:, sq], rhs=ident_f[:], is_transpose=True, start=False, stop=(k < DIRECT)
+                )
+                if k >= DIRECT:
+                    nc.tensor.matmul(
+                        out=bank[:, sq], lhsT=n_squares[k][:, sq], rhs=ident_f[:], is_transpose=True, start=False, stop=True
+                    )
             banks[("np", k)] = bank
+            if k >= DIRECT:
+                banks[("n", k)] = turn("n", n_squares[k])
 
         def variance(k):
             neg_mu = act_stats[:, k, 0:1]
@@ -374,12 +406,14 @@ def tile_lngru2dcell_v_kernel(
             k0, k1, k2, k3 = r, r + 1, r + 2, r + 3
 
             def t0():
-                f_banks["i"] = turn(psum_f, t3(k0))
-                f_banks["l"] = turn(psum_f, t1(k0))
-                f_banks["r"] = turn(psum_f, rs(k0))
+                f_banks["i"] = turn("f", t3(k0))
+                f_banks["l"] = turn("f", t1(k0))
+
+            def t3_():
+                f_banks["r"] = turn("f", rs(k0))
 
             def t1_():
-                nc.scalar.activation(out=gate(k1, n_cols), in_=banks[("n", k1)][:], func=ACT.Square)
+                nc.scalar.activation(out=gate(k1, n_cols), in_=n_of(k1), func=ACT.Square)
 
             def f1():
                 quad = work.tile([P, 4, S], F32)
@@ -387,15 +421,16 @@ def tile_lngru2dcell_v_kernel(
                 stt(e_of(k1), state(go_sb, k1), 1.0, lnh_bc[:], ALU.mult, ALU.mult, accum_out=dve_sums[:, k1, 1:2])
 
             def f2():
-                stt(t3(k1), t1(k1), -0.5, banks[("np", k1)][:], ALU.mult, ALU.add)
+                tt(t3(k1), gate(k1, n_cols), banks[("np", k1)][:], ALU.add)
 
             def f3():
-                stt(t3(k1), gate(k1, i_cols), 1.0, t3(k1), ALU.add, ALU.mult)
+                n_less_c = t3(k1) if k1 < DIRECT else banks[("np", k1)][:]
+                stt(t3(k1), gate(k1, i_cols), 1.0, n_less_c, ALU.add, ALU.mult)
 
             def f4():
-                stt(hc(k1), t3(k1), -0.5, banks[("n", k1)][:], ALU.mult, ALU.add, accum_out=dve_sums[:, k1, 0:1])
+                stt(hc(k1), t3(k1), -0.5, n_of(k1), ALU.mult, ALU.add, accum_out=dve_sums[:, k1, 0:1])
                 variance(k1)
-                scale_columns(turn(psum_t, t3(k1)), t3(k1), coef_of(BLOCK_I))
+                scale_columns(turn("t", t3(k1)), t3(k1), coef_of(BLOCK_I))
 
             def f5():
                 stt(te(k1), e_of(k1), 1.0, hc(k1), ALU.mult, ALU.mult, accum_out=dve_sums[:, k1, 2:3])
@@ -403,14 +438,18 @@ def tile_lngru2dcell_v_kernel(
 
             def f6():
                 stt(t1(k1), gate(k1, l_cols), -1.0, t1(k1), ALU.add, ALU.mult)
-                scale_columns(turn(psum_t, t1(k1)), t1(k1), coef_of(BLOCK_L))
+                scale_columns(t1(k1), t1(k1), coef_of(BLOCK_L))
 
             def g1():
-                pair = work.tile([P, 2, S], F32)
+                pair = work.tile([P, 2, S], F32, bufs=3)
                 pairs[k2] = pair
                 stt(rs(k2), gate(k2, r_cols), 1.0, banks[("sn", k2)][:], ALU.add, ALU.mult)
-                candidate(k2)
-                scale_columns(turn(psum_t, rs(k2)), rs(k2), coef_of(BLOCK_R))
+                if k2 < DIRECT:
+                    tt(gate(k2, n_cols), gate(k2, n_cols), rs(k2), ALU.add)
+                    nc.scalar.activation(out=gate(k2, n_cols), in_=gate(k2, n_cols), func=ACT.Tanh)
+                else:
+                    candidate(k2)
+                scale_columns(turn("t", rs(k2)), rs(k2), coef_of(BLOCK_R))
 
             def g2():
                 stt(t1(k2), gate(k2, l_cols), 1.0, banks[("d01", k2)][:], ALU.add, ALU.mult)
@@ -456,10 +495,10 @@ def tile_lngru2dcell_v_kernel(
                 )
 
             table = {
-                "T0": (k0, t0), "T1": (k1, t1_), "T2": (k0 - 1, lambda: mean_terms(k0 - 1)),
-                "F1": (k1, f1), "F2": (k1, f2), "F3": (k1, f3), "F4": (k1, f4), "F5": (k1, f5), "F6": (k1, f6),
+                "T0": (k0, t0), "T3": (k0, t3_), "T1": (k1, t1_), "T2": (k0 - 1, lambda: mean_terms(k0 - 1)),
+                "F1": (k1, f1), "F2": (k1 if k1 < DIRECT else -1, f2), "F3": (k1, f3), "F4": (k1, f4), "F5": (k1, f5), "F6": (k1, f6),
                 "G1": (k2, g1), "G2": (k2, g2),
-                "X1": (k2, lambda: sn_and_difference(k2)), "X2": (0, x2), "X3": (k1, lambda: scaled_e(k1)),
+                "X1": (k3, lambda: difference(k3)), "X6": (k3, lambda: sn_to_rows(k3)), "X2": (0, x2), "X3": (k1, lambda: scaled_e(k1)),
                 "X4": (k3, lambda: sn_to_columns(k3)), "X5": (k2, lambda: candidate_to_rows(k2)),
                 "B1": (k0, b1), "B2": (k0, b2), "B3": (k0, b3), "B4": (k0, b4), "B5": (k0, b5), "B6": (k0, b6),
                 "B7": (k0, b7), "B8": (k0, b8), "B9": (k0, b9), "B10": (k0, b10),
@@ -468,23 +507,21 @@ def tile_lngru2dcell_v_kernel(
                 chunk, step = table[name]
                 if ok(chunk):
                     step()
-                elif name[0] in "FG" and r >= CHUNKS - 2:
+                elif name[0] in "FG" and name != "F2" and r >= CHUNKS - 2:
                     fill()
 
-        acc_pools = (psum_f, psum_f, psum_f, psum_n, psum_n, psum_n, psum_t, psum_t)
-        FIRST_SLOTS = 6
-        assert (FIRST_SLOTS // 2 + 2) * DA_PIECE >= 2 * S
-        late_slots = [t[:, j, 0 : 2 * S] for t in (g_sb[0], h_sb[0], g_sb[1], h_sb[1]) for j in range(PACK)]
-        first_slots = []
+        acc_roles = [role for role in BANKS for i in range(BANKS[role])]
+        slots = {}
 
         def slot(m):
-            if m >= FIRST_SLOTS:
-                return late_slots[m - FIRST_SLOTS]
-            if m % 3 == 0:
+            place = m % 7
+            if place in (0, 3):
                 quad = work.tile([P, 2, 2 * S], F32)
-                pair = work.tile([P, 1, 2 * S], F32)
-                first_slots.extend([quad[:, 0, :], quad[:, 1, :], pair[:, 0, :]])
-            return first_slots[m]
+                slots["quad"] = quad
+            if place in (0, 1, 3, 4):
+                return slots["quad"][:, place % 3, :]
+            pair = work.tile([P, 1, 2 * S], F32, bufs=3)
+            return pair[:, 0, :]
 
         def multiply(piece):
             blocks = range(piece * DA_PIECE // P, (piece + 1) * DA_PIECE // P)
@@ -493,7 +530,7 @@ def tile_lngru2dcell_v_kernel(
                 for m in blocks:
                     for half in range(2):
                         if c == 0:
-                            acc = acc_pools[counts["acc"] % len(acc_pools)].tile([P, S], F32, tag="bank")
+                            acc = bank_of(acc_roles[counts["acc"] % len(acc_roles)])
                             counts["acc"] = counts["acc"] + 1
                             accs[(m, half)] = acc
                         rows = slice(m * P, (m + 1) * P)
@@ -517,21 +554,24 @@ def tile_lngru2dcell_v_kernel(
                         nc.scalar.copy(out=result[:, cols], in_=accs[(m, half)][:])
                 nc.sync.dma_start(out=out[m * P : (m + 1) * P, :], in_=result)
 
-        steady = "T0 T1 T2 F1 B1 F2 B2 F3 B3 F4 X1 B4 F5 X2 X3 B5 F6 B6 G1 X4 X5 B7 G2 B8 B9 B10"
+        steady = "T0 X4 T2 F1 F2 F3 G1 T3 F4 T1 G2 X1 F6 B1 F5 X5 X2 X3 B2 B3 B4 B6 X6 B5 B7 B9 B8 B10"
         with tc.manual_schedule():
-            round_of_work(-3, "X4 X2")
             spread(lnh_bc, 5 * SQ, 1.0)
             spread(sgn_bc, BLOCK_N * SQ, BLOCK_COEF[BLOCK_N])
-            round_of_work(-2, "X1 G1 X5 G2 X4 X2")
-            round_of_work(-1, "T1 F1 F2 F3 F4 X1 F5 F6 G1 X5 G2 X3 X4 X2")
+            round_of_work(-3, "X4 X6 X2 X1")
+            round_of_work(-2, "G1 G2 X5 X4 X6 X2 X1")
+            round_of_work(-1, "F1 F2 F3 F4 T1 F6 F5 G1 G2 X5 X3 X4 X6 X2 X1")
             quantise_first_s()
             for r in range(CHUNKS):
                 round_of_work(r, steady)
+            nc.gpsimd.tensor_scalar(
+                out=pool_stats[:, 0, 0:1], in0=dve_sums[:, CHUNKS - 1, 7:8], scalar1=1.0, scalar2=0.0, op0=ALU.mult, op1=ALU.add
+            )
             mean_terms(CHUNKS - 1)
             for piece in range(PIECES):
-                for c in range(PASSES):
-                    if c > 0 or piece >= EARLY:
-                        da_step(c, piece)
+                if piece + EARLY < PIECES:
+                    da_step(0, piece + EARLY)
+                da_step(1, piece)
                 if piece > 0:
                     multiply(piece - 1)
             quantise(*unquantised["piece"])

@@ -20,10 +20,11 @@ PACK = 4
 PASSES = 2
 CHUNKS = PASSES * PACK
 EPS = 1e-5
-DA_PIECE = 256
-PIECES = GATES // DA_PIECE
+PIECE_WIDTHS = (256,) * 7 + (128,) * 2
+PIECES = len(PIECE_WIDTHS)
+assert sum(PIECE_WIDTHS) == GATES
 EARLY = 2
-VECTOR_EMPTIES = 0
+VECTOR_EMPTIES = 2
 DIRECT = 2
 RUN = 4
 
@@ -88,6 +89,7 @@ def tile_lngru2dcell_v_kernel(
         neg_half_ident_b = keep.tile([P, P], BF16)
         vec_rows = keep.tile([P, P], BF16)
         vec_cols = keep.tile([P, 6 * SQ], F32)
+        lnh_rows = keep.tile([P, P], BF16)
         coef_cols = keep.tile([P, 4 * SQ], F32)
         sn_cols = keep.tile([P, 2 * SQ], F32)
         rs_sb = keep.tile([P, CHUNKS], F32)
@@ -103,11 +105,7 @@ def tile_lngru2dcell_v_kernel(
         nc.vector.memset(vec_rows[:], 0.0)
         nc.scalar.dma_start(out=vec_rows[0 : 4 * SQ, :], in_=lns_g.rearrange("(r w) -> r w", w=P))
         nc.scalar.dma_start(out=vec_rows[4 * SQ : 5 * SQ, :], in_=lns_b[n_cols].rearrange("(r w) -> r w", w=P))
-        nc.scalar.dma_start(out=vec_rows[5 * SQ : 6 * SQ, :], in_=lnh_g.rearrange("(r w) -> r w", w=P))
-        nc.scalar.dma_start(
-            out=rs_sb[:].rearrange("p (c j) -> p c j", j=PACK),
-            in_=rstd_s.rearrange("(c p j) o -> p c (j o)", p=P, j=PACK),
-        )
+        nc.vector.memset(lnh_rows[:], 0.0)
 
         def load_shat(k, cols):
             nc.sync.dma_start(out=h_sb[k // PACK][:, k % PACK, cols], in_=shat_v[k // PACK, :, k % PACK, cols])
@@ -124,9 +122,15 @@ def tile_lngru2dcell_v_kernel(
             load_shat(k, l_cols)
 
         load_shat(0, n_cols)
-        load_gates(0, slice(0, 2 * S))
+        load_gates(0, r_cols)
+        nc.sync.dma_start(out=lnh_rows[0:SQ, :], in_=lnh_g.rearrange("(r w) -> r w", w=P))
+        load_gates(0, i_cols)
         load_gates(0, slice(2 * S, GATES))
         load_states(0, slice(0, 1))
+        nc.sync.dma_start(
+            out=rs_sb[:].rearrange("p (c j) -> p c j", j=PACK),
+            in_=rstd_s.rearrange("(c p j) o -> p c (j o)", p=P, j=PACK),
+        )
         load_shat(1, n_cols)
         load_gates(1, whole)
         load_states(0, slice(1, PACK))
@@ -153,21 +157,19 @@ def tile_lngru2dcell_v_kernel(
         nc.vector.tensor_scalar_mul(out=neg_half_ident_b[:], in0=ident_f[:], scalar1=-0.5)
         vec_bank = bank_of("t", (P, P), BF16)
         nc.tensor.transpose(vec_bank[:], vec_rows[:], ident_b[:])
-        nc.vector.tensor_copy(out=vec_cols[:], in_=vec_bank[:, 0 : 6 * SQ])
+        nc.vector.tensor_copy(out=vec_cols[:, 0 : 5 * SQ], in_=vec_bank[:, 0 : 5 * SQ])
         nc.vector.tensor_scalar_mul(out=sn_cols[:, 0:SQ], in0=vec_cols[:, BLOCK_N * SQ : (BLOCK_N + 1) * SQ], scalar1=-0.5)
         nc.vector.tensor_scalar_mul(out=sn_cols[:, SQ : 2 * SQ], in0=vec_cols[:, 4 * SQ : 5 * SQ], scalar1=-0.5)
         for b in range(4):
             sq = slice(b * SQ, (b + 1) * SQ)
             nc.vector.tensor_scalar_mul(out=coef_cols[:, sq], in0=vec_cols[:, sq], scalar1=BLOCK_COEF[b])
-        nc.vector.tensor_copy(out=rs_pairs[:, :, 0], in_=rs_sb[:])
-        nc.vector.tensor_scalar_mul(out=rs_pairs[:, :, 1], in0=rs_sb[:], scalar1=-1.0 / S)
 
         def spread(dst, first_col, factor):
             bank = bank_of("f")
             for q in range(SQ):
                 col = vec_cols[:, first_col + q : first_col + q + 1]
                 nc.tensor.transpose(bank[:, q * P : (q + 1) * P], col.to_broadcast([P, P]), ident_f[:])
-            nc.vector.tensor_scalar_mul(out=dst[:], in0=bank[:], scalar1=factor)
+            return lambda: nc.vector.tensor_scalar_mul(out=dst[:], in0=bank[:], scalar1=factor)
 
         pairs = {}
         quads = {}
@@ -279,8 +281,8 @@ def tile_lngru2dcell_v_kernel(
         unquantised = {}
 
         def form_da(c, piece):
-            cols = slice(piece * DA_PIECE, (piece + 1) * DA_PIECE)
-            grouped = work.tile([P, DA_PIECE, PACK], BF16, align_bytes=64)
+            cols = slice(sum(PIECE_WIDTHS[:piece]), sum(PIECE_WIDTHS[: piece + 1]))
+            grouped = work.tile([P, PIECE_WIDTHS[piece], PACK], BF16, align_bytes=64)
             tt(
                 grouped[:].rearrange("p (q i) j -> p q j i", i=RUN),
                 regrouped(g_sb[c][:, :, cols]),
@@ -314,8 +316,11 @@ def tile_lngru2dcell_v_kernel(
         def ok(k):
             return 0 <= k < CHUNKS
 
-        def tanh_of_gates(k):
-            nc.scalar.activation(out=gate(k, slice(0, 2 * S)), in_=gate(k, slice(0, 2 * S)), func=ACT.Tanh, scale=0.5)
+        def tanh_of(k, cols):
+            nc.scalar.activation(out=gate(k, cols), in_=gate(k, cols), func=ACT.Tanh, scale=0.5)
+
+        def tanh_of_gates(k, first=slice(0, 2 * S)):
+            tanh_of(k, first)
             nc.scalar.activation(out=gate(k, l_cols), in_=turn("t", gate(k, l_cols))[:], func=ACT.Tanh, scale=0.5)
 
         def sn_to_columns(k):
@@ -498,7 +503,7 @@ def tile_lngru2dcell_v_kernel(
                 "T0": (k0, t0), "T3": (k0, t3_), "T1": (k1, t1_), "T2": (k0 - 1, lambda: mean_terms(k0 - 1)),
                 "F1": (k1, f1), "F2": (k1 if k1 < DIRECT else -1, f2), "F3": (k1, f3), "F4": (k1, f4), "F5": (k1, f5), "F6": (k1, f6),
                 "G1": (k2, g1), "G2": (k2, g2),
-                "X1": (k3, lambda: difference(k3)), "X6": (k3, lambda: sn_to_rows(k3)), "X2": (0, x2), "X3": (k1, lambda: scaled_e(k1)),
+                "X1": (k3, lambda: difference(k3)), "X6": (k3, lambda: sn_to_rows(k3)), "X2": (0, x2), "XR": (k3, lambda: tanh_of(k3, r_cols)), "XI": (k3, lambda: tanh_of_gates(k3, i_cols)), "X3": (k1, lambda: scaled_e(k1)),
                 "X4": (k3, lambda: sn_to_columns(k3)), "X5": (k2, lambda: candidate_to_rows(k2)),
                 "B1": (k0, b1), "B2": (k0, b2), "B3": (k0, b3), "B4": (k0, b4), "B5": (k0, b5), "B6": (k0, b6),
                 "B7": (k0, b7), "B8": (k0, b8), "B9": (k0, b9), "B10": (k0, b10),
@@ -523,11 +528,14 @@ def tile_lngru2dcell_v_kernel(
             pair = work.tile([P, 1, 2 * S], F32, bufs=3)
             return pair[:, 0, :]
 
+        accs = {}
+
+        def blocks_of(piece):
+            return range(sum(PIECE_WIDTHS[:piece]) // P, sum(PIECE_WIDTHS[: piece + 1]) // P)
+
         def multiply(piece):
-            blocks = range(piece * DA_PIECE // P, (piece + 1) * DA_PIECE // P)
-            accs = {}
             for c in range(PASSES):
-                for m in blocks:
+                for m in blocks_of(piece):
                     for half in range(2):
                         if c == 0:
                             acc = bank_of(acc_roles[counts["acc"] % len(acc_roles)])
@@ -544,23 +552,38 @@ def tile_lngru2dcell_v_kernel(
                             start=(c == 0),
                             stop=(c == PASSES - 1),
                         )
-            for m in blocks:
+
+        def empty(piece):
+            for m in blocks_of(piece):
                 result = slot(m)
                 for half in range(2):
                     cols = slice(half * S, (half + 1) * S)
-                    if half == 1 and (piece == PIECES - 1 or (m % 2 == 1 and piece >= PIECES - VECTOR_EMPTIES)):
+                    if half == 1 and piece >= PIECES - VECTOR_EMPTIES:
                         nc.vector.tensor_copy(out=result[:, cols], in_=accs[(m, half)][:])
                     else:
                         nc.scalar.copy(out=result[:, cols], in_=accs[(m, half)][:])
-                nc.sync.dma_start(out=out[m * P : (m + 1) * P, :], in_=result)
+                if piece < PIECES - 1:
+                    nc.sync.dma_start(out=out[m * P : (m + 1) * P, :], in_=result)
+                else:
+                    nc.sync.dma_start(out=out[m * P : (m + 1) * P, 0:S], in_=result[:, 0:S])
+                    nc.scalar.dma_start(out=out[m * P : (m + 1) * P, S : 2 * S], in_=result[:, S : 2 * S])
 
-        steady = "T0 X4 T2 F1 F2 F3 G1 T3 F4 T1 G2 X1 F6 B1 F5 X5 X2 X3 B2 B3 B4 B6 X6 B5 B7 B9 B8 B10"
+        steady = "T0 X4 T2 F1 F2 F3 G1 T3 F4 T1 G2 X1 B1 F6 X5 X2 B2 B3 B4 B6 X6 B5 B7 B9 B8 F5 X3 B10"
         with tc.manual_schedule():
-            spread(lnh_bc, 5 * SQ, 1.0)
-            spread(sgn_bc, BLOCK_N * SQ, BLOCK_COEF[BLOCK_N])
-            round_of_work(-3, "X4 X6 X2 X1")
-            round_of_work(-2, "G1 G2 X5 X4 X6 X2 X1")
-            round_of_work(-1, "F1 F2 F3 F4 T1 F6 F5 G1 G2 X5 X3 X4 X6 X2 X1")
+            round_of_work(-3, "XR X4")
+            lnh_bank = bank_of("t", (P, P), BF16)
+            nc.tensor.transpose(lnh_bank[:], lnh_rows[:], ident_b[:])
+            nc.vector.tensor_copy(out=vec_cols[:, 5 * SQ : 6 * SQ], in_=lnh_bank[:, 0:SQ])
+            round_of_work(-3, "X6 XI X1")
+            copy_lnh = spread(lnh_bc, 5 * SQ, 1.0)
+            round_of_work(-2, "G1 G2 X5")
+            copy_lnh()
+            nc.vector.tensor_copy(out=rs_pairs[:, :, 0], in_=rs_sb[:])
+            nc.vector.tensor_scalar_mul(out=rs_pairs[:, :, 1], in0=rs_sb[:], scalar1=-1.0 / S)
+            round_of_work(-2, "X4 X6 X2 X1")
+            copy_sgn = spread(sgn_bc, BLOCK_N * SQ, BLOCK_COEF[BLOCK_N])
+            round_of_work(-1, "F1 F2 F3 F4 T1 F6 F5 G1 G2 X5 X4 X6 X2 X3 X1")
+            copy_sgn()
             quantise_first_s()
             for r in range(CHUNKS):
                 round_of_work(r, steady)
@@ -574,5 +597,9 @@ def tile_lngru2dcell_v_kernel(
                 da_step(1, piece)
                 if piece > 0:
                     multiply(piece - 1)
+                if piece > 1:
+                    empty(piece - 2)
             quantise(*unquantised["piece"])
             multiply(PIECES - 1)
+            empty(PIECES - 2)
+            empty(PIECES - 1)

@@ -261,7 +261,7 @@ def tile_lngru2dcell_v_kernel(
         def quantise_first_s():
             waiting = None
             for half in range(2):
-                grouped = work.tile([P, S, PACK], BF16, align_bytes=64)
+                grouped = work.tile([P, S, PACK], BF16, align_bytes=64, bufs=3)
                 regroup_s(nc.vector.tensor_copy, 0, half, grouped, slice(0, S))
                 if waiting is not None:
                     quantise(*waiting)
@@ -273,7 +273,7 @@ def tile_lngru2dcell_v_kernel(
         def regroup_second_s(quarter):
             half = quarter // 2
             if quarter % 2 == 0:
-                grouped = work.tile([P, S, PACK], BF16, align_bytes=64)
+                grouped = work.tile([P, S, PACK], BF16, align_bytes=64, bufs=3)
                 second_s[half] = s_target(1, half, grouped)
             cols = slice((quarter % 2) * (S // 2), (quarter % 2 + 1) * (S // 2))
             regroup_s(nc.scalar.copy, 1, half, second_s[half][0], cols)
@@ -282,7 +282,7 @@ def tile_lngru2dcell_v_kernel(
 
         def form_da(c, piece):
             cols = slice(sum(PIECE_WIDTHS[:piece]), sum(PIECE_WIDTHS[: piece + 1]))
-            grouped = work.tile([P, PIECE_WIDTHS[piece], PACK], BF16, align_bytes=64)
+            grouped = work.tile([P, PIECE_WIDTHS[piece], PACK], BF16, align_bytes=64, bufs=3)
             tt(
                 grouped[:].rearrange("p (q i) j -> p q j i", i=RUN),
                 regrouped(g_sb[c][:, :, cols]),
@@ -300,17 +300,18 @@ def tile_lngru2dcell_v_kernel(
         def early_form(piece):
             unquantised["early"] = form_da(0, piece)
 
-        fillers = [lambda: quantise(*second_s[0])]
-        for early in range(EARLY):
-            fillers.append(lambda piece=early: early_form(piece))
-            fillers.append(lambda: quantise(*unquantised["early"]))
-            if early == 0:
-                fillers.append(lambda: quantise(*second_s[1]))
+        assert EARLY == 2
+        quantise_early = lambda: quantise(*unquantised["early"])
+        fillers = [
+            lambda: quantise(*second_s[0]), lambda: early_form(0), quantise_early, lambda: quantise(*second_s[1]),
+            None, None, None, lambda: early_form(1), quantise_early,
+        ]
         counts = {"fill": 0, "acc": 0}
 
         def fill():
             if counts["fill"] < len(fillers):
-                fillers[counts["fill"]]()
+                if fillers[counts["fill"]] is not None:
+                    fillers[counts["fill"]]()
                 counts["fill"] = counts["fill"] + 1
 
         def ok(k):
@@ -420,9 +421,11 @@ def tile_lngru2dcell_v_kernel(
             def t1_():
                 nc.scalar.activation(out=gate(k1, n_cols), in_=n_of(k1), func=ACT.Square)
 
-            def f1():
+            def a1():
                 quad = work.tile([P, 4, S], F32)
                 quads[k1] = quad
+
+            def f1():
                 stt(e_of(k1), state(go_sb, k1), 1.0, lnh_bc[:], ALU.mult, ALU.mult, accum_out=dve_sums[:, k1, 1:2])
 
             def f2():
@@ -449,6 +452,8 @@ def tile_lngru2dcell_v_kernel(
                 pair = work.tile([P, 2, S], F32, bufs=3)
                 pairs[k2] = pair
                 stt(rs(k2), gate(k2, r_cols), 1.0, banks[("sn", k2)][:], ALU.add, ALU.mult)
+
+            def g3():
                 if k2 < DIRECT:
                     tt(gate(k2, n_cols), gate(k2, n_cols), rs(k2), ALU.add)
                     nc.scalar.activation(out=gate(k2, n_cols), in_=gate(k2, n_cols), func=ACT.Tanh)
@@ -473,7 +478,7 @@ def tile_lngru2dcell_v_kernel(
                 stt(e_of(k0), gate(k0, i_cols), -1.0, hc(k0), ALU.add, ALU.mult)
 
             def b3():
-                stt(hc(k0), gate(k0, i_cols), 1.0, hc(k0), ALU.add, ALU.mult)
+                stt(t3(k0), gate(k0, i_cols), 1.0, hc(k0), ALU.add, ALU.mult)
 
             def b4():
                 stt(gate(k0, n_cols), gate(k0, n_cols), -1.0, e_of(k0), ALU.add, ALU.mult)
@@ -485,7 +490,7 @@ def tile_lngru2dcell_v_kernel(
                 stt(gate(k0, i_cols), f_banks["i"][:], 1.0, e_of(k0), ALU.mult, ALU.mult, accum_out=dve_sums[:, k0, 3:4])
 
             def b7():
-                stt(gate(k0, l_cols), f_banks["l"][:], 1.0, hc(k0), ALU.mult, ALU.mult, accum_out=dve_sums[:, k0, 4:5])
+                stt(gate(k0, l_cols), f_banks["l"][:], 1.0, t3(k0), ALU.mult, ALU.mult, accum_out=dve_sums[:, k0, 4:5])
 
             def b8():
                 stt(gate(k0, r_cols), f_banks["r"][:], 1.0, te(k0), ALU.mult, ALU.mult, accum_out=dve_sums[:, k0, 6:7])
@@ -501,7 +506,7 @@ def tile_lngru2dcell_v_kernel(
 
             table = {
                 "T0": (k0, t0), "T3": (k0, t3_), "T1": (k1, t1_), "T2": (k0 - 1, lambda: mean_terms(k0 - 1)),
-                "F1": (k1, f1), "F2": (k1 if k1 < DIRECT else -1, f2), "F3": (k1, f3), "F4": (k1, f4), "F5": (k1, f5), "F6": (k1, f6),
+                "A1": (k1, a1), "G3": (k2, g3), "F1": (k1, f1), "F2": (k1 if k1 < DIRECT else -1, f2), "F3": (k1, f3), "F4": (k1, f4), "F5": (k1, f5), "F6": (k1, f6),
                 "G1": (k2, g1), "G2": (k2, g2),
                 "X1": (k3, lambda: difference(k3)), "X6": (k3, lambda: sn_to_rows(k3)), "X2": (0, x2), "XR": (k3, lambda: tanh_of(k3, r_cols)), "XI": (k3, lambda: tanh_of_gates(k3, i_cols)), "X3": (k1, lambda: scaled_e(k1)),
                 "X4": (k3, lambda: sn_to_columns(k3)), "X5": (k2, lambda: candidate_to_rows(k2)),
@@ -512,7 +517,7 @@ def tile_lngru2dcell_v_kernel(
                 chunk, step = table[name]
                 if ok(chunk):
                     step()
-                elif name[0] in "FG" and name != "F2" and r >= CHUNKS - 2:
+                elif name[0] in "FG" and name not in ("F2", "G3") and r >= CHUNKS - 2:
                     fill()
 
         acc_roles = [role for role in BANKS for i in range(BANKS[role])]
@@ -568,7 +573,7 @@ def tile_lngru2dcell_v_kernel(
                     nc.sync.dma_start(out=out[m * P : (m + 1) * P, 0:S], in_=result[:, 0:S])
                     nc.scalar.dma_start(out=out[m * P : (m + 1) * P, S : 2 * S], in_=result[:, S : 2 * S])
 
-        steady = "T0 X4 T2 F1 F2 F3 G1 T3 F4 T1 G2 X1 B1 F6 X5 X2 B2 B3 B4 B6 X6 B5 B7 B9 B8 F5 X3 B10"
+        steady = "T0 X4 T2 G1 G3 T3 A1 F2 F1 F3 G2 X1 F4 T1 B1 F6 X5 X2 B2 B3 B4 B6 X6 B5 B7 B9 B8 F5 X3 B10"
         with tc.manual_schedule():
             round_of_work(-3, "XR X4")
             lnh_bank = bank_of("t", (P, P), BF16)
@@ -576,16 +581,17 @@ def tile_lngru2dcell_v_kernel(
             nc.vector.tensor_copy(out=vec_cols[:, 5 * SQ : 6 * SQ], in_=lnh_bank[:, 0:SQ])
             round_of_work(-3, "X6 XI X1")
             copy_lnh = spread(lnh_bc, 5 * SQ, 1.0)
-            round_of_work(-2, "G1 G2 X5")
+            round_of_work(-2, "G1 G3 G2 X5")
             copy_lnh()
             nc.vector.tensor_copy(out=rs_pairs[:, :, 0], in_=rs_sb[:])
             nc.vector.tensor_scalar_mul(out=rs_pairs[:, :, 1], in0=rs_sb[:], scalar1=-1.0 / S)
             round_of_work(-2, "X4 X6 X2 X1")
             copy_sgn = spread(sgn_bc, BLOCK_N * SQ, BLOCK_COEF[BLOCK_N])
-            round_of_work(-1, "F1 F2 F3 F4 T1 F6 F5 G1 G2 X5 X4 X6 X2 X3 X1")
+            round_of_work(-1, "A1 F2 F1 F3 F6 F4 T1 G1 F5 G2 G3 X5 X4 X6 X2 X3 X1")
             copy_sgn()
             quantise_first_s()
-            for r in range(CHUNKS):
+            round_of_work(0, "T0 X4 T2 A1 F2 F1 F3 G1 G3 T3 F4 T1 G2 X1 B1 F6 X5 X2 B2 B3 B4 B6 X6 B5 B7 B9 B8 F5 X3 B10")
+            for r in range(1, CHUNKS):
                 round_of_work(r, steady)
             nc.gpsimd.tensor_scalar(
                 out=pool_stats[:, 0, 0:1], in0=dve_sums[:, CHUNKS - 1, 7:8], scalar1=1.0, scalar2=0.0, op0=ALU.mult, op1=ALU.add

@@ -304,7 +304,7 @@ def tile_lngru2dcell_v_kernel(
         quantise_early = lambda: quantise(*unquantised["early"])
         fillers = [
             lambda: quantise(*second_s[0]), lambda: early_form(0), quantise_early, lambda: quantise(*second_s[1]),
-            None, None, None, lambda: early_form(1), quantise_early,
+            None, None, lambda: early_form(1), quantise_early,
         ]
         counts = {"fill": 0, "acc": 0}
 
@@ -448,6 +448,13 @@ def tile_lngru2dcell_v_kernel(
                 stt(t1(k1), gate(k1, l_cols), -1.0, t1(k1), ALU.add, ALU.mult)
                 scale_columns(t1(k1), t1(k1), coef_of(BLOCK_L))
 
+            def w6():
+                nc.gpsimd.tensor_scalar(
+                    out=te(k1), in0=gate(k1, l_cols), scalar1=1.0, scalar2=-1.0, op0=ALU.mult, op1=ALU.add
+                )
+                nc.gpsimd.tensor_tensor(out=t1(k1), in0=te(k1), in1=t1(k1), op=ALU.mult)
+                scale_columns(t1(k1), t1(k1), coef_of(BLOCK_L))
+
             def g1():
                 pair = work.tile([P, 2, S], F32, bufs=3)
                 pairs[k2] = pair
@@ -506,7 +513,7 @@ def tile_lngru2dcell_v_kernel(
 
             table = {
                 "T0": (k0, t0), "T3": (k0, t3_), "T1": (k1, t1_), "T2": (k0 - 1, lambda: mean_terms(k0 - 1)),
-                "A1": (k1, a1), "G3": (k2, g3), "F1": (k1, f1), "F2": (k1 if k1 < DIRECT else -1, f2), "F3": (k1, f3), "F4": (k1, f4), "F5": (k1, f5), "F6": (k1, f6),
+                "A1": (k1, a1), "W6": (k1, w6), "G3": (k2, g3), "F1": (k1, f1), "F2": (k1 if k1 < DIRECT else -1, f2), "F3": (k1, f3), "F4": (k1, f4), "F5": (k1, f5), "F6": (k1, f6),
                 "G1": (k2, g1), "G2": (k2, g2),
                 "X1": (k3, lambda: difference(k3)), "X6": (k3, lambda: sn_to_rows(k3)), "X2": (0, x2), "XR": (k3, lambda: tanh_of(k3, r_cols)), "XI": (k3, lambda: tanh_of_gates(k3, i_cols)), "X3": (k1, lambda: scaled_e(k1)),
                 "X4": (k3, lambda: sn_to_columns(k3)), "X5": (k2, lambda: candidate_to_rows(k2)),
@@ -573,7 +580,7 @@ def tile_lngru2dcell_v_kernel(
                     nc.sync.dma_start(out=out[m * P : (m + 1) * P, 0:S], in_=result[:, 0:S])
                     nc.scalar.dma_start(out=out[m * P : (m + 1) * P, S : 2 * S], in_=result[:, S : 2 * S])
 
-        steady = "T0 X4 T2 G1 G3 T3 A1 F2 F1 F3 G2 X1 F4 T1 B1 F6 X5 X2 B2 B3 B4 B6 X6 B5 B7 B9 B8 F5 X3 B10"
+        steady = "T0 X4 T2 A1 W6 G1 G3 T3 F3 G2 X1 F4 T1 B1 F1 X5 X2 B2 B3 B4 B6 X6 B5 B7 B9 B8 F5 X3 B10"
         with tc.manual_schedule():
             round_of_work(-3, "XR X4")
             lnh_bank = bank_of("t", (P, P), BF16)
@@ -593,9 +600,6 @@ def tile_lngru2dcell_v_kernel(
             round_of_work(0, "T0 X4 T2 A1 F2 F1 F3 G1 G3 T3 F4 T1 G2 X1 B1 F6 X5 X2 B2 B3 B4 B6 X6 B5 B7 B9 B8 F5 X3 B10")
             for r in range(1, CHUNKS):
                 round_of_work(r, steady)
-            nc.gpsimd.tensor_scalar(
-                out=pool_stats[:, 0, 0:1], in0=dve_sums[:, CHUNKS - 1, 7:8], scalar1=1.0, scalar2=0.0, op0=ALU.mult, op1=ALU.add
-            )
             mean_terms(CHUNKS - 1)
             for piece in range(PIECES):
                 if piece + EARLY < PIECES:

@@ -26,7 +26,7 @@ assert sum(PIECE_WIDTHS) == GATES
 EARLY = 2
 VECTOR_EMPTIES = 2
 DIRECT = 2
-RUN = 4
+RUN = 8
 
 BLOCK_COEF = (-0.25, 0.25, -0.25, 0.25)
 BLOCK_R = 0

@@ -258,25 +258,19 @@ def tile_lngru2dcell_v_kernel(
             cols = slice(half * S, (half + 1) * S)
             return (grouped, s_codes[:, c, cols], s_scales[:, c, cols], E4M3X4)
 
-        def quantise_first_s():
-            waiting = None
-            for half in range(2):
-                grouped = work.tile([P, S, PACK], BF16, align_bytes=64, bufs=3)
-                regroup_s(nc.vector.tensor_copy, 0, half, grouped, slice(0, S))
-                if waiting is not None:
-                    quantise(*waiting)
-                waiting = s_target(0, half, grouped)
-            quantise(*waiting)
-
+        first_s = {}
         second_s = {}
 
-        def regroup_second_s(quarter):
+        def regroup_by_scalar(c, targets, quarter):
             half = quarter // 2
             if quarter % 2 == 0:
                 grouped = work.tile([P, S, PACK], BF16, align_bytes=64, bufs=3)
-                second_s[half] = s_target(1, half, grouped)
+                targets[half] = s_target(c, half, grouped)
             cols = slice((quarter % 2) * (S // 2), (quarter % 2 + 1) * (S // 2))
-            regroup_s(nc.scalar.copy, 1, half, second_s[half][0], cols)
+            regroup_s(nc.scalar.copy, c, half, targets[half][0], cols)
+
+        def regroup_second_s(quarter):
+            regroup_by_scalar(1, second_s, quarter)
 
         unquantised = {}
 
@@ -477,6 +471,9 @@ def tile_lngru2dcell_v_kernel(
                 elif r in (CHUNKS - 3, CHUNKS - 2):
                     regroup_second_s(2 * (r - (CHUNKS - 3)))
                     regroup_second_s(2 * (r - (CHUNKS - 3)) + 1)
+                elif r == CHUNKS - 1:
+                    for quarter in range(4):
+                        regroup_by_scalar(0, first_s, quarter)
 
             def b1():
                 stt(hc(k0), hc(k0), act_stats[:, k0, 8:9], te(k0), ALU.mult, ALU.add)
@@ -596,11 +593,12 @@ def tile_lngru2dcell_v_kernel(
             copy_sgn = spread(sgn_bc, BLOCK_N * SQ, BLOCK_COEF[BLOCK_N])
             round_of_work(-1, "A1 F2 F1 F3 F6 F4 T1 G1 F5 G2 G3 X5 X4 X6 X2 X3 X1")
             copy_sgn()
-            quantise_first_s()
             round_of_work(0, "T0 X4 T2 A1 F2 F1 F3 G1 G3 T3 F4 T1 G2 X1 B1 F6 X5 X2 B2 B3 B4 B6 X6 B5 B7 B9 B8 F5 X3 B10")
             for r in range(1, CHUNKS):
                 round_of_work(r, steady)
             mean_terms(CHUNKS - 1)
+            quantise(*first_s[0])
+            quantise(*first_s[1])
             for piece in range(PIECES):
                 if piece + EARLY < PIECES:
                     da_step(0, piece + EARLY)

@@ -23,12 +23,13 @@ EPS = 1e-5
 PIECE_WIDTHS = (256,) * 7 + (128,) * 2
 PIECES = len(PIECE_WIDTHS)
 assert sum(PIECE_WIDTHS) == GATES
-EARLY = 2
+EARLY = 0
 VECTOR_EMPTIES = 2
 DIRECT = 2
+S_PIECE = 256
 RUN = 8
 
-BLOCK_COEF = (-0.25, 0.25, -0.25, 0.25)
+BLOCK_COEF = (-0.5, 1.0, -0.5, 0.5)
 BLOCK_R = 0
 BLOCK_I = 1
 BLOCK_N = 2
@@ -75,7 +76,7 @@ def tile_lngru2dcell_v_kernel(
         h_sb = [keep.tile([P, PACK, GATES], F32, name="shat%d" % c) for c in range(PASSES)]
         p0_sb = keep.tile([P, PASSES, PACK, S], BF16)
         p1_sb = keep.tile([P, PASSES, PACK, S], BF16)
-        go_sb = keep.tile([P, PASSES, PACK, S], BF16)
+        go_sb = keep.tile([P, PACK, S], BF16)
         s_codes = keep.tile([P, PASSES, 2 * S], U32, align_bytes=64)
         s_scales = keep.tile([P, PASSES, 2 * S], U8, align_bytes=64)
         da_codes = keep.tile([P, PASSES, GATES], U32, align_bytes=64)
@@ -114,8 +115,11 @@ def tile_lngru2dcell_v_kernel(
             nc.sync.dma_start(out=g_sb[k // PACK][:, k % PACK, cols], in_=gates_v[k // PACK, :, k % PACK, cols])
 
         def load_states(c, rows):
-            for dst, src in ((p0_sb, p0_v), (p1_sb, p1_v), (go_sb, go_v)):
+            for dst, src in ((p0_sb, p0_v), (p1_sb, p1_v)):
                 nc.sync.dma_start(out=dst[:, c, rows, :], in_=src[c, :, rows, :])
+
+        def load_grad_out(c, rows):
+            nc.sync.dma_start(out=go_sb[:, rows, :], in_=go_v[c, :, rows, :])
 
         def load_rest_of_shat(k):
             load_shat(k, slice(0, 2 * S))
@@ -127,6 +131,7 @@ def tile_lngru2dcell_v_kernel(
         load_gates(0, i_cols)
         load_gates(0, slice(2 * S, GATES))
         load_states(0, slice(0, 1))
+        load_grad_out(0, slice(0, 1))
         nc.sync.dma_start(
             out=rs_sb[:].rearrange("p (c j) -> p c j", j=PACK),
             in_=rstd_s.rearrange("(c p j) o -> p c (j o)", p=P, j=PACK),
@@ -134,6 +139,7 @@ def tile_lngru2dcell_v_kernel(
         load_shat(1, n_cols)
         load_gates(1, whole)
         load_states(0, slice(1, PACK))
+        load_grad_out(0, slice(1, PACK))
         load_shat(2, n_cols)
         load_gates(2, whole)
         load_rest_of_shat(0)
@@ -147,7 +153,7 @@ def tile_lngru2dcell_v_kernel(
         load_rest_of_shat(CHUNKS - 1)
 
         nc.gpsimd.memset(eps_col[:], EPS)
-        nc.scalar.activation(out=unread_col[:], in_=eps_col[:], func=ACT.Tanh)
+        nc.scalar.activation(out=unread_col[:], in_=eps_col[:], func=ACT.Sigmoid)
         make_identity(nc, ident_f[:])
         nc.gpsimd.memset(powers[:, 0:1], -0.5)
         nc.gpsimd.memset(powers[:, 1:2], -1.0)
@@ -250,27 +256,26 @@ def tile_lngru2dcell_v_kernel(
         def quantise(grouped, codes, scales, x4):
             nc.vector.quantize_mx(out=codes.bitcast(x4), scales=scales, in_=grouped[:].rearrange("p w j -> p (w j)"))
 
-        def regroup_s(copy, c, half, grouped, cols):
-            src = (p0_sb, p1_sb)[half]
-            copy(out=grouped[:, cols, :].rearrange("p (q i) j -> p q j i", i=RUN), in_=regrouped(src[:, c, :, cols]))
+        counts = {"fill": 0, "acc": 0, "regrouped": 0, "quantised": 0, "early": 0}
+        S_PIECES = 2 * S // S_PIECE
+        regrouped_s = []
 
-        def s_target(c, half, grouped):
-            cols = slice(half * S, (half + 1) * S)
-            return (grouped, s_codes[:, c, cols], s_scales[:, c, cols], E4M3X4)
+        def regroup_next_s():
+            c, piece = divmod(counts["regrouped"], S_PIECES)
+            counts["regrouped"] = counts["regrouped"] + 1
+            cols = slice(piece * S_PIECE, (piece + 1) * S_PIECE)
+            src = (p0_sb, p1_sb)[cols.start // S]
+            grouped = work.tile([P, S_PIECE, PACK], BF16, align_bytes=64, bufs=3)
+            copy = (nc.vector.tensor_copy, nc.scalar.copy)[c]
+            copy(
+                out=grouped[:].rearrange("p (q i) j -> p q j i", i=RUN),
+                in_=regrouped(src[:, c, :, cols.start % S : cols.start % S + S_PIECE]),
+            )
+            regrouped_s.append((grouped, s_codes[:, c, cols], s_scales[:, c, cols], E4M3X4))
 
-        first_s = {}
-        second_s = {}
-
-        def regroup_by_scalar(c, targets, quarter):
-            half = quarter // 2
-            if quarter % 2 == 0:
-                grouped = work.tile([P, S, PACK], BF16, align_bytes=64, bufs=3)
-                targets[half] = s_target(c, half, grouped)
-            cols = slice((quarter % 2) * (S // 2), (quarter % 2 + 1) * (S // 2))
-            regroup_s(nc.scalar.copy, c, half, targets[half][0], cols)
-
-        def regroup_second_s(quarter):
-            regroup_by_scalar(1, second_s, quarter)
+        def quantise_next_s():
+            quantise(*regrouped_s[counts["quantised"]])
+            counts["quantised"] = counts["quantised"] + 1
 
         unquantised = {}
 
@@ -291,16 +296,21 @@ def tile_lngru2dcell_v_kernel(
                 quantise(*unquantised["piece"])
             unquantised["piece"] = formed
 
-        def early_form(piece):
-            unquantised["early"] = form_da(0, piece)
+        early_pieces = []
 
-        assert EARLY == 2
-        quantise_early = lambda: quantise(*unquantised["early"])
+        def form_early():
+            early_pieces.append(form_da(0, len(early_pieces)))
+
+        def quantise_early():
+            quantise(*early_pieces[counts["early"]])
+            counts["early"] = counts["early"] + 1
+
+        assert EARLY == 0 and S_PIECES == 4
         fillers = [
-            lambda: quantise(*second_s[0]), lambda: early_form(0), quantise_early, lambda: quantise(*second_s[1]),
-            None, None, lambda: early_form(1), quantise_early,
+            regroup_next_s, regroup_next_s, quantise_next_s, regroup_next_s, quantise_next_s, regroup_next_s, quantise_next_s,
+            quantise_next_s,
+            quantise_next_s,
         ]
-        counts = {"fill": 0, "acc": 0}
 
         def fill():
             if counts["fill"] < len(fillers):
@@ -312,10 +322,16 @@ def tile_lngru2dcell_v_kernel(
             return 0 <= k < CHUNKS
 
         def tanh_of(k, cols):
-            nc.scalar.activation(out=gate(k, cols), in_=gate(k, cols), func=ACT.Tanh, scale=0.5)
+            if cols.start < S:
+                nc.scalar.activation(out=gate(k, r_cols), in_=gate(k, r_cols), func=ACT.Tanh, scale=0.5)
+            if cols.stop > S:
+                nc.scalar.activation(out=gate(k, i_cols), in_=gate(k, i_cols), func=ACT.Sigmoid)
 
         def tanh_of_gates(k, first=slice(0, 2 * S)):
             tanh_of(k, first)
+            tanh_of_l(k)
+
+        def tanh_of_l(k):
             nc.scalar.activation(out=gate(k, l_cols), in_=turn("t", gate(k, l_cols))[:], func=ACT.Tanh, scale=0.5)
 
         def sn_to_columns(k):
@@ -403,35 +419,38 @@ def tile_lngru2dcell_v_kernel(
         f_banks = {}
 
         def round_of_work(r, order):
-            k0, k1, k2, k3 = r, r + 1, r + 2, r + 3
+            km, k0, k1, k2, k3 = r - 1, r, r + 1, r + 2, r + 3
 
             def t0():
                 f_banks["i"] = turn("f", t3(k0))
                 f_banks["l"] = turn("f", t1(k0))
 
             def t3_():
-                f_banks["r"] = turn("f", rs(k0))
+                f_banks["r"] = turn("f", rs(km))
 
             def t1_():
                 nc.scalar.activation(out=gate(k1, n_cols), in_=n_of(k1), func=ACT.Square)
 
             def a1():
-                quad = work.tile([P, 4, S], F32)
+                quad = work.tile([P, 4, S], F32, bufs=3)
                 quads[k1] = quad
 
             def f1():
-                stt(e_of(k1), state(go_sb, k1), 1.0, lnh_bc[:], ALU.mult, ALU.mult, accum_out=dve_sums[:, k1, 1:2])
+                stt(e_of(k1), go_sb[:, k1 % PACK, :], 1.0, lnh_bc[:], ALU.mult, ALU.mult, accum_out=dve_sums[:, k1, 1:2])
+                if k1 < PACK:
+                    load_grad_out(1, slice(k1, k1 + 1))
 
             def f2():
                 tt(t3(k1), gate(k1, n_cols), banks[("np", k1)][:], ALU.add)
 
             def f3():
                 n_less_c = t3(k1) if k1 < DIRECT else banks[("np", k1)][:]
-                stt(t3(k1), gate(k1, i_cols), 1.0, n_less_c, ALU.add, ALU.mult)
+                stt(t3(k1), gate(k1, i_cols), 1.0, n_less_c, ALU.mult, ALU.mult)
 
             def f4():
-                stt(hc(k1), t3(k1), -0.5, n_of(k1), ALU.mult, ALU.add, accum_out=dve_sums[:, k1, 0:1])
-                variance(k1)
+                stt(hc(k1), t3(k1), -1.0, n_of(k1), ALU.mult, ALU.add, accum_out=dve_sums[:, k1, 0:1])
+
+            def f7():
                 scale_columns(turn("t", t3(k1)), t3(k1), coef_of(BLOCK_I))
 
             def f5():
@@ -442,15 +461,20 @@ def tile_lngru2dcell_v_kernel(
                 stt(t1(k1), gate(k1, l_cols), -1.0, t1(k1), ALU.add, ALU.mult)
                 scale_columns(t1(k1), t1(k1), coef_of(BLOCK_L))
 
+            def z_():
+                nc.gpsimd.tensor_tensor(out=e_of(k1), in0=gate(km, i_cols), in1=hc(km), op=ALU.mult)
+
+            def w7():
+                scale_columns(t1(k1), t1(k1), coef_of(BLOCK_L))
+
             def w6():
                 nc.gpsimd.tensor_scalar(
                     out=te(k1), in0=gate(k1, l_cols), scalar1=1.0, scalar2=-1.0, op0=ALU.mult, op1=ALU.add
                 )
                 nc.gpsimd.tensor_tensor(out=t1(k1), in0=te(k1), in1=t1(k1), op=ALU.mult)
-                scale_columns(t1(k1), t1(k1), coef_of(BLOCK_L))
 
             def g1():
-                pair = work.tile([P, 2, S], F32, bufs=3)
+                pair = work.tile([P, 2, S], F32, bufs=4)
                 pairs[k2] = pair
                 stt(rs(k2), gate(k2, r_cols), 1.0, banks[("sn", k2)][:], ALU.add, ALU.mult)
 
@@ -460,20 +484,12 @@ def tile_lngru2dcell_v_kernel(
                     nc.scalar.activation(out=gate(k2, n_cols), in_=gate(k2, n_cols), func=ACT.Tanh)
                 else:
                     candidate(k2)
+
+            def g4():
                 scale_columns(turn("t", rs(k2)), rs(k2), coef_of(BLOCK_R))
 
             def g2():
                 stt(t1(k2), gate(k2, l_cols), 1.0, banks[("d01", k2)][:], ALU.add, ALU.mult)
-
-            def x2():
-                if ok(k3):
-                    tanh_of_gates(k3)
-                elif r in (CHUNKS - 3, CHUNKS - 2):
-                    regroup_second_s(2 * (r - (CHUNKS - 3)))
-                    regroup_second_s(2 * (r - (CHUNKS - 3)) + 1)
-                elif r == CHUNKS - 1:
-                    for quarter in range(4):
-                        regroup_by_scalar(0, first_s, quarter)
 
             def b1():
                 stt(hc(k0), hc(k0), act_stats[:, k0, 8:9], te(k0), ALU.mult, ALU.add)
@@ -482,7 +498,7 @@ def tile_lngru2dcell_v_kernel(
                 stt(e_of(k0), gate(k0, i_cols), -1.0, hc(k0), ALU.add, ALU.mult)
 
             def b3():
-                stt(t3(k0), gate(k0, i_cols), 1.0, hc(k0), ALU.add, ALU.mult)
+                stt(hc(k0), gate(k0, i_cols), 1.0, hc(k0), ALU.mult, ALU.mult)
 
             def b4():
                 stt(gate(k0, n_cols), gate(k0, n_cols), -1.0, e_of(k0), ALU.add, ALU.mult)
@@ -491,50 +507,51 @@ def tile_lngru2dcell_v_kernel(
                 stt(te(k0), gate(k0, r_cols), -1.0, gate(k0, n_cols), ALU.add, ALU.mult)
 
             def b6():
-                stt(gate(k0, i_cols), f_banks["i"][:], 1.0, e_of(k0), ALU.mult, ALU.mult, accum_out=dve_sums[:, k0, 3:4])
+                stt(gate(km, i_cols), f_banks["i"][:], 1.0, e_of(km), ALU.mult, ALU.mult, accum_out=dve_sums[:, km, 3:4])
 
             def b7():
-                stt(gate(k0, l_cols), f_banks["l"][:], 1.0, t3(k0), ALU.mult, ALU.mult, accum_out=dve_sums[:, k0, 4:5])
+                i_dh = e_of(km + 2) if ok(km + 2) else hc(km)
+                stt(gate(km, l_cols), f_banks["l"][:], 1.0, i_dh, ALU.mult, ALU.mult, accum_out=dve_sums[:, km, 4:5])
 
             def b8():
-                stt(gate(k0, r_cols), f_banks["r"][:], 1.0, te(k0), ALU.mult, ALU.mult, accum_out=dve_sums[:, k0, 6:7])
+                stt(gate(km, r_cols), f_banks["r"][:], 1.0, te(km), ALU.mult, ALU.mult, accum_out=dve_sums[:, km, 6:7])
 
             def b9():
-                stt(gate(k0, n_cols), te(k0), 1.0, sgn_bc[:], ALU.mult, ALU.mult, accum_out=dve_sums[:, k0, 5:6])
+                stt(gate(km, n_cols), te(km), 1.0, sgn_bc[:], ALU.mult, ALU.mult, accum_out=dve_sums[:, km, 5:6])
 
             def b10():
                 stt(
-                    quads[k0][:].rearrange("p a w -> p (a w)"), gate(k0, whole), 1.0, shat_of(k0, whole),
-                    ALU.mult, ALU.mult, accum_out=dve_sums[:, k0, 7:8],
+                    quads[km][:].rearrange("p a w -> p (a w)"), gate(km, whole), 1.0, shat_of(km, whole),
+                    ALU.mult, ALU.mult, accum_out=dve_sums[:, km, 7:8],
                 )
 
             table = {
-                "T0": (k0, t0), "T3": (k0, t3_), "T1": (k1, t1_), "T2": (k0 - 1, lambda: mean_terms(k0 - 1)),
-                "A1": (k1, a1), "W6": (k1, w6), "G3": (k2, g3), "F1": (k1, f1), "F2": (k1 if k1 < DIRECT else -1, f2), "F3": (k1, f3), "F4": (k1, f4), "F5": (k1, f5), "F6": (k1, f6),
+                "T0": (k0, t0), "T3": (km, t3_), "T1": (k1, t1_), "T2": (km - 1, lambda: mean_terms(km - 1)),
+                "R": (0, regroup_next_s), "V": (0, fill),
+                "A1": (k1, a1), "W6": (k1, w6), "G3": (k2, g3), "G4": (k2, g4), "F7": (k1, f7), "F8": (k1, lambda: variance(k1)),
+                "X7": (k3, lambda: tanh_of(k3, slice(0, 2 * S))), "X8": (k3, lambda: tanh_of_l(k3)), "F1": (k1, f1), "F2": (k1 if k1 < DIRECT else -1, f2), "F3": (k1, f3), "F4": (k1, f4), "F5": (k1, f5), "F6": (k1, f6),
                 "G1": (k2, g1), "G2": (k2, g2),
-                "X1": (k3, lambda: difference(k3)), "X6": (k3, lambda: sn_to_rows(k3)), "X2": (0, x2), "XR": (k3, lambda: tanh_of(k3, r_cols)), "XI": (k3, lambda: tanh_of_gates(k3, i_cols)), "X3": (k1, lambda: scaled_e(k1)),
+                "X1": (k3, lambda: difference(k3)), "X6": (k3, lambda: sn_to_rows(k3)), "X2": (k3, lambda: tanh_of_gates(k3)), "XR": (k3, lambda: tanh_of(k3, r_cols)), "XI": (k3, lambda: tanh_of_gates(k3, i_cols)), "X3": (k1, lambda: scaled_e(k1)),
                 "X4": (k3, lambda: sn_to_columns(k3)), "X5": (k2, lambda: candidate_to_rows(k2)),
-                "B1": (k0, b1), "B2": (k0, b2), "B3": (k0, b3), "B4": (k0, b4), "B5": (k0, b5), "B6": (k0, b6),
-                "B7": (k0, b7), "B8": (k0, b8), "B9": (k0, b9), "B10": (k0, b10),
+                "B1": (k0, b1), "B2": (k0, b2), "B3": (-1 if ok(k0 + 2) else k0, b3), "Z": (km if ok(k1) else -1, z_), "W7": (k1, w7), "B4": (k0, b4), "B5": (k0, b5), "B6": (km, b6),
+                "B7": (km, b7), "B8": (km, b8), "B9": (km, b9), "B10": (km, b10),
             }
             for name in order.split():
                 chunk, step = table[name]
                 if ok(chunk):
                     step()
-                elif name[0] in "FG" and name not in ("F2", "G3") and r >= CHUNKS - 2:
-                    fill()
 
         acc_roles = [role for role in BANKS for i in range(BANKS[role])]
         slots = {}
 
         def slot(m):
-            place = m % 7
-            if place in (0, 3):
-                quad = work.tile([P, 2, 2 * S], F32)
+            place = m % 10
+            if place in (0, 3, 6):
+                quad = work.tile([P, 2, 2 * S], F32, bufs=3)
                 slots["quad"] = quad
-            if place in (0, 1, 3, 4):
+            if place in (0, 1, 3, 4, 6, 7):
                 return slots["quad"][:, place % 3, :]
-            pair = work.tile([P, 1, 2 * S], F32, bufs=3)
+            pair = work.tile([P, 1, 2 * S], F32, bufs=4)
             return pair[:, 0, :]
 
         accs = {}
@@ -577,7 +594,7 @@ def tile_lngru2dcell_v_kernel(
                     nc.sync.dma_start(out=out[m * P : (m + 1) * P, 0:S], in_=result[:, 0:S])
                     nc.scalar.dma_start(out=out[m * P : (m + 1) * P, S : 2 * S], in_=result[:, S : 2 * S])
 
-        steady = "T0 X4 T2 A1 W6 G1 G3 T3 F3 G2 X1 F4 T1 B1 F1 X5 X2 B2 B3 B4 B6 X6 B5 B7 B9 B8 F5 X3 B10"
+        steady = "T1 T2 A1 Z W6 G1 G3 T3 F3 G2 F4 F8 X4 X7 X8 B6 B7 B8 X5 W7 G4 F7 X1 B1 B9 B2 F1 B4 F5 B5 X3 X6 T0 B10"
         with tc.manual_schedule():
             round_of_work(-3, "XR X4")
             lnh_bank = bank_of("t", (P, P), BF16)
@@ -585,20 +602,24 @@ def tile_lngru2dcell_v_kernel(
             nc.vector.tensor_copy(out=vec_cols[:, 5 * SQ : 6 * SQ], in_=lnh_bank[:, 0:SQ])
             round_of_work(-3, "X6 XI X1")
             copy_lnh = spread(lnh_bc, 5 * SQ, 1.0)
-            round_of_work(-2, "G1 G3 G2 X5")
+            round_of_work(-2, "G1 G3 G4 G2 X5")
             copy_lnh()
             nc.vector.tensor_copy(out=rs_pairs[:, :, 0], in_=rs_sb[:])
             nc.vector.tensor_scalar_mul(out=rs_pairs[:, :, 1], in0=rs_sb[:], scalar1=-1.0 / S)
             round_of_work(-2, "X4 X6 X2 X1")
             copy_sgn = spread(sgn_bc, BLOCK_N * SQ, BLOCK_COEF[BLOCK_N])
-            round_of_work(-1, "A1 F2 F1 F3 F6 F4 T1 G1 F5 G2 G3 X5 X4 X6 X2 X3 X1")
+            round_of_work(-1, "A1 F2 F1 F3 F6 F4 F8 F7 T1 G1 F5 G2 G3 G4 X5 X4 X6 X2 X3 X1")
             copy_sgn()
-            round_of_work(0, "T0 X4 T2 A1 F2 F1 F3 G1 G3 T3 F4 T1 G2 X1 B1 F6 X5 X2 B2 B3 B4 B6 X6 B5 B7 B9 B8 F5 X3 B10")
-            for r in range(1, CHUNKS):
+            round_of_work(0, "X4 A1 F2 F1 F3 G1 G3 G4 F4 F8 F7 T1 G2 X1 B1 F6 X5 X2 B2 F5 B4 V X3 B5 X6 T0 V V V V V V V")
+            for r in range(1, CHUNKS - 3):
                 round_of_work(r, steady)
+            round_of_work(CHUNKS - 3, "T1 T2 A1 Z W6 G1 G3 T3 F3 G2 F4 F8 B6 B7 B8 X5 W7 G4 F7 B1 B9 B2 F1 B4 F5 B5 X3 T0 B10")
+            round_of_work(CHUNKS - 2, "T1 T2 A1 Z W6 T3 B8 F3 B1 F4 F8 B6 B7 W7 F7 B9 B2 F1 B4 B3 F5 B5 X3 T0 B10")
+            round_of_work(CHUNKS - 1, "T2 R R R T3 B6 B7 B1 B9 B2 B8 B4 B3 B5 T0 B10")
+            round_of_work(CHUNKS, "T2 T3 B9 B6 B7 B8 V R B10")
             mean_terms(CHUNKS - 1)
-            quantise(*first_s[0])
-            quantise(*first_s[1])
+            for piece in range(S_PIECES - 1):
+                quantise_next_s()
             for piece in range(PIECES):
                 if piece + EARLY < PIECES:
                     da_step(0, piece + EARLY)

@@ -507,14 +507,14 @@ def tile_lngru2dcell_v_kernel(
                 stt(te(k0), gate(k0, r_cols), -1.0, gate(k0, n_cols), ALU.add, ALU.mult)
 
             def b6():
-                stt(gate(km, i_cols), f_banks["i"][:], 1.0, e_of(km), ALU.mult, ALU.mult, accum_out=dve_sums[:, km, 3:4])
+                stt(gate(km, i_cols), e_of(km), 1.0, f_banks["i"][:], ALU.mult, ALU.mult, accum_out=dve_sums[:, km, 3:4])
 
             def b7():
                 i_dh = e_of(km + 2) if ok(km + 2) else hc(km)
-                stt(gate(km, l_cols), f_banks["l"][:], 1.0, i_dh, ALU.mult, ALU.mult, accum_out=dve_sums[:, km, 4:5])
+                stt(gate(km, l_cols), i_dh, 1.0, f_banks["l"][:], ALU.mult, ALU.mult, accum_out=dve_sums[:, km, 4:5])
 
             def b8():
-                stt(gate(km, r_cols), f_banks["r"][:], 1.0, te(km), ALU.mult, ALU.mult, accum_out=dve_sums[:, km, 6:7])
+                stt(gate(km, r_cols), te(km), 1.0, f_banks["r"][:], ALU.mult, ALU.mult, accum_out=dve_sums[:, km, 6:7])
 
             def b9():
                 stt(gate(km, n_cols), te(km), 1.0, sgn_bc[:], ALU.mult, ALU.mult, accum_out=dve_sums[:, km, 5:6])

@@ -29,7 +29,7 @@ DIRECT = 2
 S_PIECE = 256
 RUN = 8
 
-BLOCK_COEF = (-0.5, 1.0, -0.5, 0.5)
+BLOCK_COEF = (-0.5, 1.0, -0.5, -1.0)
 BLOCK_R = 0
 BLOCK_I = 1
 BLOCK_N = 2
@@ -86,8 +86,6 @@ def tile_lngru2dcell_v_kernel(
         ident_f = keep.tile([P, P], F32)
         ident_b = keep.tile([P, P], BF16)
         neg_ident_b = keep.tile([P, P], BF16)
-        half_ident_b = keep.tile([P, P], BF16)
-        neg_half_ident_b = keep.tile([P, P], BF16)
         vec_rows = keep.tile([P, P], BF16)
         vec_cols = keep.tile([P, 6 * SQ], F32)
         lnh_rows = keep.tile([P, P], BF16)
@@ -159,8 +157,6 @@ def tile_lngru2dcell_v_kernel(
         nc.gpsimd.memset(powers[:, 1:2], -1.0)
         nc.vector.tensor_copy(out=ident_b[:], in_=ident_f[:])
         nc.vector.tensor_scalar_mul(out=neg_ident_b[:], in0=ident_f[:], scalar1=-1.0)
-        nc.vector.tensor_scalar_mul(out=half_ident_b[:], in0=ident_f[:], scalar1=0.5)
-        nc.vector.tensor_scalar_mul(out=neg_half_ident_b[:], in0=ident_f[:], scalar1=-0.5)
         vec_bank = bank_of("t", (P, P), BF16)
         nc.tensor.transpose(vec_bank[:], vec_rows[:], ident_b[:])
         nc.vector.tensor_copy(out=vec_cols[:, 0 : 5 * SQ], in_=vec_bank[:, 0 : 5 * SQ])
@@ -332,7 +328,7 @@ def tile_lngru2dcell_v_kernel(
             tanh_of_l(k)
 
         def tanh_of_l(k):
-            nc.scalar.activation(out=gate(k, l_cols), in_=turn("t", gate(k, l_cols))[:], func=ACT.Tanh, scale=0.5)
+            nc.scalar.activation(out=gate(k, l_cols), in_=turn("t", gate(k, l_cols))[:], func=ACT.Sigmoid, scale=-1.0)
 
         def sn_to_columns(k):
             bank = turn("t", shat_of(k, n_cols))
@@ -346,8 +342,8 @@ def tile_lngru2dcell_v_kernel(
         def difference(k):
             diff = bank_of("d01")
             for sq in squares():
-                nc.tensor.matmul(out=diff[:, sq], lhsT=state(p0_sb, k)[:, sq], rhs=neg_half_ident_b[:], start=True, stop=False)
-                nc.tensor.matmul(out=diff[:, sq], lhsT=state(p1_sb, k)[:, sq], rhs=half_ident_b[:], start=False, stop=True)
+                nc.tensor.matmul(out=diff[:, sq], lhsT=state(p0_sb, k)[:, sq], rhs=ident_b[:], start=True, stop=False)
+                nc.tensor.matmul(out=diff[:, sq], lhsT=state(p1_sb, k)[:, sq], rhs=neg_ident_b[:], start=False, stop=True)
             banks[("d01", k)] = diff
 
         def candidate(k):
@@ -388,7 +384,7 @@ def tile_lngru2dcell_v_kernel(
                 scale=act_stats[:, k, 0:1], bias=dve_sums[:, k, 2:3],
             )
 
-        def scaled_e(k):
+        def scaled_e(k, whole_chunk=True):
             neg_mu = act_stats[:, k, 0:1]
             rh = pool_stats[:, k, 0:1]
             rh2 = pool_stats[:, k, 1:2]
@@ -400,7 +396,13 @@ def tile_lngru2dcell_v_kernel(
             )
             nc.scalar.activation(out=act_stats[:, k, 4:6], in_=rs_pairs[:, k, :], func=ACT.Copy, scale=rh)
             nc.scalar.activation(out=act_stats[:, k, 8:10], in_=act_stats[:, k, 6:8], func=ACT.Copy, scale=a_neg)
-            nc.scalar.activation(out=te(k), in_=e_of(k), func=ACT.Identity, bias=act_stats[:, k, 9:10], scale=a)
+            if whole_chunk:
+                nc.scalar.activation(out=te(k), in_=e_of(k), func=ACT.Identity, bias=act_stats[:, k, 9:10], scale=a)
+
+        def scaled_e_by_gpsimd(k):
+            nc.gpsimd.tensor_scalar(
+                out=te(k), in0=e_of(k), scalar1=act_stats[:, k, 4:5], scalar2=act_stats[:, k, 9:10], op0=ALU.mult, op1=ALU.add
+            )
 
         def mean_terms(k):
             neg_mean_f = act_stats[:, k, 10:11]
@@ -458,7 +460,7 @@ def tile_lngru2dcell_v_kernel(
                 covariance(k1)
 
             def f6():
-                stt(t1(k1), gate(k1, l_cols), -1.0, t1(k1), ALU.add, ALU.mult)
+                stt(t1(k1), gate(k1, l_cols), 1.0, t1(k1), ALU.mult, ALU.mult)
                 scale_columns(t1(k1), t1(k1), coef_of(BLOCK_L))
 
             def z_():
@@ -468,10 +470,7 @@ def tile_lngru2dcell_v_kernel(
                 scale_columns(t1(k1), t1(k1), coef_of(BLOCK_L))
 
             def w6():
-                nc.gpsimd.tensor_scalar(
-                    out=te(k1), in0=gate(k1, l_cols), scalar1=1.0, scalar2=-1.0, op0=ALU.mult, op1=ALU.add
-                )
-                nc.gpsimd.tensor_tensor(out=t1(k1), in0=te(k1), in1=t1(k1), op=ALU.mult)
+                nc.gpsimd.tensor_tensor(out=t1(k1), in0=gate(k1, l_cols), in1=t1(k1), op=ALU.mult)
 
             def g1():
                 pair = work.tile([P, 2, S], F32, bufs=4)
@@ -489,7 +488,7 @@ def tile_lngru2dcell_v_kernel(
                 scale_columns(turn("t", rs(k2)), rs(k2), coef_of(BLOCK_R))
 
             def g2():
-                stt(t1(k2), gate(k2, l_cols), 1.0, banks[("d01", k2)][:], ALU.add, ALU.mult)
+                stt(t1(k2), gate(k2, l_cols), -1.0, banks[("d01", k2)][:], ALU.add, ALU.mult)
 
             def b1():
                 stt(hc(k0), hc(k0), act_stats[:, k0, 8:9], te(k0), ALU.mult, ALU.add)
@@ -531,7 +530,7 @@ def tile_lngru2dcell_v_kernel(
                 "A1": (k1, a1), "W6": (k1, w6), "G3": (k2, g3), "G4": (k2, g4), "F7": (k1, f7), "F8": (k1, lambda: variance(k1)),
                 "X7": (k3, lambda: tanh_of(k3, slice(0, 2 * S))), "X8": (k3, lambda: tanh_of_l(k3)), "F1": (k1, f1), "F2": (k1 if k1 < DIRECT else -1, f2), "F3": (k1, f3), "F4": (k1, f4), "F5": (k1, f5), "F6": (k1, f6),
                 "G1": (k2, g1), "G2": (k2, g2),
-                "X1": (k3, lambda: difference(k3)), "X6": (k3, lambda: sn_to_rows(k3)), "X2": (k3, lambda: tanh_of_gates(k3)), "XR": (k3, lambda: tanh_of(k3, r_cols)), "XI": (k3, lambda: tanh_of_gates(k3, i_cols)), "X3": (k1, lambda: scaled_e(k1)),
+                "X1": (k3, lambda: difference(k3)), "X6": (k3, lambda: sn_to_rows(k3)), "X2": (k3, lambda: tanh_of_gates(k3)), "XR": (k3, lambda: tanh_of(k3, r_cols)), "XI": (k3, lambda: tanh_of_gates(k3, i_cols)), "X3": (k1, lambda: scaled_e(k1)), "X9": (k1, lambda: scaled_e(k1, False)), "Y": (k0, lambda: scaled_e_by_gpsimd(k0)),
                 "X4": (k3, lambda: sn_to_columns(k3)), "X5": (k2, lambda: candidate_to_rows(k2)),
                 "B1": (k0, b1), "B2": (k0, b2), "B3": (-1 if ok(k0 + 2) else k0, b3), "Z": (km if ok(k1) else -1, z_), "W7": (k1, w7), "B4": (k0, b4), "B5": (k0, b5), "B6": (km, b6),
                 "B7": (km, b7), "B8": (km, b8), "B9": (km, b9), "B10": (km, b10),
@@ -594,7 +593,7 @@ def tile_lngru2dcell_v_kernel(
                     nc.sync.dma_start(out=out[m * P : (m + 1) * P, 0:S], in_=result[:, 0:S])
                     nc.scalar.dma_start(out=out[m * P : (m + 1) * P, S : 2 * S], in_=result[:, S : 2 * S])
 
-        steady = "T1 T2 A1 Z W6 G1 G3 T3 F3 G2 F4 F8 X4 X7 X8 B6 B7 B8 X5 W7 G4 F7 X1 B1 B9 B2 F1 B4 F5 B5 X3 X6 T0 B10"
+        steady = "T1 T2 A1 Z Y W6 G1 G3 T3 F3 G2 F4 F8 X4 X7 X8 B6 B7 B8 X5 W7 G4 F7 X1 B1 B9 B2 F1 B4 F5 B5 X9 X6 T0 B10"
         with tc.manual_schedule():
             round_of_work(-3, "XR X4")
             lnh_bank = bank_of("t", (P, P), BF16)
@@ -610,11 +609,11 @@ def tile_lngru2dcell_v_kernel(
             copy_sgn = spread(sgn_bc, BLOCK_N * SQ, BLOCK_COEF[BLOCK_N])
             round_of_work(-1, "A1 F2 F1 F3 F6 F4 F8 F7 T1 G1 F5 G2 G3 G4 X5 X4 X6 X2 X3 X1")
             copy_sgn()
-            round_of_work(0, "X4 A1 F2 F1 F3 G1 G3 G4 F4 F8 F7 T1 G2 X1 B1 F6 X5 X2 B2 F5 B4 V X3 B5 X6 T0 V V V V V V V")
+            round_of_work(0, "X4 A1 F2 F1 F3 G1 G3 G4 F4 F8 F7 T1 G2 X1 B1 F6 X5 X2 B2 F5 B4 V X9 B5 X6 T0 V V V V V V V")
             for r in range(1, CHUNKS - 3):
                 round_of_work(r, steady)
-            round_of_work(CHUNKS - 3, "T1 T2 A1 Z W6 G1 G3 T3 F3 G2 F4 F8 B6 B7 B8 X5 W7 G4 F7 B1 B9 B2 F1 B4 F5 B5 X3 T0 B10")
-            round_of_work(CHUNKS - 2, "T1 T2 A1 Z W6 T3 B8 F3 B1 F4 F8 B6 B7 W7 F7 B9 B2 F1 B4 B3 F5 B5 X3 T0 B10")
+            round_of_work(CHUNKS - 3, "T1 T2 A1 Z Y W6 G1 G3 T3 F3 G2 F4 F8 B6 B7 B8 X5 W7 G4 F7 B1 B9 B2 F1 B4 F5 B5 X9 T0 B10")
+            round_of_work(CHUNKS - 2, "T1 T2 A1 Z Y W6 T3 B8 F3 B9 F4 F8 B6 B7 W7 F7 B1 F1 B2 F5 B4 B3 B5 X3 T0 B10")
             round_of_work(CHUNKS - 1, "T2 R R R T3 B6 B7 B1 B9 B2 B8 B4 B3 B5 T0 B10")
             round_of_work(CHUNKS, "T2 T3 B9 B6 B7 B8 V R B10")
             mean_terms(CHUNKS - 1)

@@ -404,7 +404,7 @@ def tile_lngru2dcell_v_kernel(
                 out=te(k), in0=e_of(k), scalar1=act_stats[:, k, 4:5], scalar2=act_stats[:, k, 9:10], op0=ALU.mult, op1=ALU.add
             )
 
-        def mean_terms(k):
+        def mean_terms(k, pieces=1):
             neg_mean_f = act_stats[:, k, 10:11]
             neg_mean_fs = act_stats[:, k, 11:12]
             nc.scalar.activation(
@@ -412,8 +412,8 @@ def tile_lngru2dcell_v_kernel(
                 accum_out=neg_mean_f,
             )
             nc.scalar.mul(out=neg_mean_fs, in_=dve_sums[:, k, 7:8], mul=-1.0 / GATES)
-            for block in range(4):
-                cols = slice(block * S, (block + 1) * S)
+            for piece in range(pieces):
+                cols = slice(piece * GATES // pieces, (piece + 1) * GATES // pieces)
                 nc.scalar.activation(
                     out=shat_of(k, cols), in_=shat_of(k, cols), func=ACT.Identity, bias=neg_mean_f, scale=neg_mean_fs
                 )
@@ -616,7 +616,7 @@ def tile_lngru2dcell_v_kernel(
             round_of_work(CHUNKS - 2, "T1 T2 A1 Z Y W6 T3 B8 F3 B9 F4 F8 B6 B7 W7 F7 B1 F1 B2 F5 B4 B3 B5 X3 T0 B10")
             round_of_work(CHUNKS - 1, "T2 R R R T3 B6 B7 B1 B9 B2 B8 B4 B3 B5 T0 B10")
             round_of_work(CHUNKS, "T2 T3 B9 B6 B7 B8 V R B10")
-            mean_terms(CHUNKS - 1)
+            mean_terms(CHUNKS - 1, 4)
             for piece in range(S_PIECES - 1):
                 quantise_next_s()
             for piece in range(PIECES):

@@ -437,8 +437,16 @@ def tile_lngru2dcell_v_kernel(
                 quad = work.tile([P, 4, S], F32, bufs=3)
                 quads[k1] = quad
 
+            def k1_():
+                bank = bank_of("np")
+                for q in range(SQ):
+                    col = vec_cols[:, 5 * SQ + q : 5 * SQ + q + 1]
+                    nc.tensor.transpose(bank[:, q * P : (q + 1) * P], col.to_broadcast([P, P]), ident_f[:])
+                banks[("lnh", k1)] = bank
+
             def f1():
-                stt(e_of(k1), go_sb[:, k1 % PACK, :], 1.0, lnh_bc[:], ALU.mult, ALU.mult, accum_out=dve_sums[:, k1, 1:2])
+                lnh = banks[("lnh", k1)][:] if ("lnh", k1) in banks else lnh_bc[:]
+                stt(e_of(k1), go_sb[:, k1 % PACK, :], 1.0, lnh, ALU.mult, ALU.mult, accum_out=dve_sums[:, k1, 1:2])
                 if k1 < PACK:
                     load_grad_out(1, slice(k1, k1 + 1))
 
@@ -530,7 +538,7 @@ def tile_lngru2dcell_v_kernel(
                 "A1": (k1, a1), "W6": (k1, w6), "G3": (k2, g3), "G4": (k2, g4), "F7": (k1, f7), "F8": (k1, lambda: variance(k1)),
                 "X7": (k3, lambda: tanh_of(k3, slice(0, 2 * S))), "X8": (k3, lambda: tanh_of_l(k3)), "F1": (k1, f1), "F2": (k1 if k1 < DIRECT else -1, f2), "F3": (k1, f3), "F4": (k1, f4), "F5": (k1, f5), "F6": (k1, f6),
                 "G1": (k2, g1), "G2": (k2, g2),
-                "X1": (k3, lambda: difference(k3)), "X6": (k3, lambda: sn_to_rows(k3)), "X2": (k3, lambda: tanh_of_gates(k3)), "XR": (k3, lambda: tanh_of(k3, r_cols)), "XI": (k3, lambda: tanh_of_gates(k3, i_cols)), "X3": (k1, lambda: scaled_e(k1)), "X9": (k1, lambda: scaled_e(k1, False)), "Y": (k0, lambda: scaled_e_by_gpsimd(k0)),
+                "X1": (k3, lambda: difference(k3)), "X6": (k3, lambda: sn_to_rows(k3)), "X2": (k3, lambda: tanh_of_gates(k3)), "XR": (k3, lambda: tanh_of(k3, r_cols)), "XI": (k3, lambda: tanh_of_gates(k3, i_cols)), "X3": (k1, lambda: scaled_e(k1)), "K1": (k1, k1_), "X9": (k1, lambda: scaled_e(k1, False)), "Y": (k0, lambda: scaled_e_by_gpsimd(k0)),
                 "X4": (k3, lambda: sn_to_columns(k3)), "X5": (k2, lambda: candidate_to_rows(k2)),
                 "B1": (k0, b1), "B2": (k0, b2), "B3": (-1 if ok(k0 + 2) else k0, b3), "Z": (km if ok(k1) else -1, z_), "W7": (k1, w7), "B4": (k0, b4), "B5": (k0, b5), "B6": (km, b6),
                 "B7": (km, b7), "B8": (km, b8), "B9": (km, b9), "B10": (km, b10),
@@ -593,7 +601,7 @@ def tile_lngru2dcell_v_kernel(
                     nc.sync.dma_start(out=out[m * P : (m + 1) * P, 0:S], in_=result[:, 0:S])
                     nc.scalar.dma_start(out=out[m * P : (m + 1) * P, S : 2 * S], in_=result[:, S : 2 * S])
 
-        steady = "T1 T2 A1 Z Y W6 G1 G3 T3 F3 G2 F4 F8 X4 X7 X8 B6 B7 B8 X5 W7 G4 F7 X1 B1 B9 B2 F1 B4 F5 B5 X9 X6 T0 B10"
+        steady = "T1 T2 A1 Z Y W6 G1 G3 T3 F3 K1 G2 F4 F8 X4 X7 X8 B7 B6 F1 X5 W7 G4 F7 X1 B1 B9 B2 B8 B4 F5 B5 X9 X6 T0 B10"
         with tc.manual_schedule():
             round_of_work(-3, "XR X4")
             lnh_bank = bank_of("t", (P, P), BF16)
@@ -612,7 +620,7 @@ def tile_lngru2dcell_v_kernel(
             round_of_work(0, "X4 A1 F2 F1 F3 G1 G3 G4 F4 F8 F7 T1 G2 X1 B1 F6 X5 X2 B2 F5 B4 V X9 B5 X6 T0 V V V V V V V")
             for r in range(1, CHUNKS - 3):
                 round_of_work(r, steady)
-            round_of_work(CHUNKS - 3, "T1 T2 A1 Z Y W6 G1 G3 T3 F3 G2 F4 F8 B6 B7 B8 X5 W7 G4 F7 B1 B9 B2 F1 B4 F5 B5 X9 T0 B10")
+            round_of_work(CHUNKS - 3, "T1 T2 A1 Z Y W6 G1 G3 T3 F3 K1 G2 F4 F8 B7 B6 F1 X5 W7 G4 F7 B1 B9 B2 B8 B4 F5 B5 X9 T0 B10")
             round_of_work(CHUNKS - 2, "T1 T2 A1 Z Y W6 T3 B8 F3 B9 F4 F8 B6 B7 W7 F7 B1 F1 B2 F5 B4 B3 B5 X3 T0 B10")
             round_of_work(CHUNKS - 1, "T2 R R R T3 B6 B7 B1 B9 B2 B8 B4 B3 B5 T0 B10")
             round_of_work(CHUNKS, "T2 T3 B9 B6 B7 B8 V R B10")

from contextlib import ExitStack

import concourse.mybir as mybir
from concourse.masks import make_identity

F32 = mybir.dt.float32
BF16 = mybir.dt.bfloat16
U32 = mybir.dt.uint32
U8 = mybir.dt.uint8
E4M3X4 = mybir.dt.float8_e4m3fn_x4
E5M2X4 = mybir.dt.float8_e5m2_x4
ALU = mybir.AluOpType
ACT = mybir.ActivationFunctionType

P = 128
S = 512
SQ = S // P
GATES = 4 * S
PACK = 4
PASSES = 2
CHUNKS = PASSES * PACK
EPS = 1e-5
PIECE_WIDTHS = (256,) * 7 + (128,) * 2
PIECES = len(PIECE_WIDTHS)
assert sum(PIECE_WIDTHS) == GATES
EARLY = 0
VECTOR_EMPTIES = 2
DIRECT = 2
S_PIECE = 256
RUN = 8

BLOCK_COEF = (-0.5, 1.0, -0.5, -1.0)
BLOCK_R = 0
BLOCK_I = 1
BLOCK_N = 2
BLOCK_L = 3

FLOPS = 2 * GATES * (2 * S) * (PASSES * PACK * P)
BYTES = (
    2 * (PASSES * PACK * P) * GATES * 4
    + 3 * (PASSES * PACK * P) * S * 2
    + (PASSES * PACK * P) * 4
    + (GATES + S + S) * 2
    + GATES * 2 * S * 4
)


def tile_lngru2dcell_v_kernel(
    tc, x, s_prev0, s_prev1, Wi, Ws, lni_g, lni_b, lns_g, lns_b, lnh_g, lnh_b, gates, shat, rstd_s, grad_out, out
):
    nc = tc.nc
    r_cols = slice(BLOCK_R * S, (BLOCK_R + 1) * S)
    i_cols = slice(BLOCK_I * S, (BLOCK_I + 1) * S)
    n_cols = slice(BLOCK_N * S, (BLOCK_N + 1) * S)
    l_cols = slice(BLOCK_L * S, (BLOCK_L + 1) * S)
    whole = slice(0, GATES)

    gates_v = gates.rearrange("(c p j) w -> c p j w", p=P, j=PACK)
    shat_v = shat.rearrange("(c p j) w -> c p j w", p=P, j=PACK)
    go_v = grad_out.rearrange("(c p j) w -> c p j w", p=P, j=PACK)
    p0_v = s_prev0.rearrange("(c p j) w -> c p j w", p=P, j=PACK)
    p1_v = s_prev1.rearrange("(c p j) w -> c p j w", p=P, j=PACK)

    with ExitStack() as ctx:
        keep = ctx.enter_context(tc.tile_pool(name="keep", bufs=1))
        work = ctx.enter_context(tc.tile_pool(name="work", bufs=2))
        psum = ctx.enter_context(tc.psum_pool(name="psum", bufs=1))
        BANKS = {"d01": 1, "n": 1, "np": 1, "f": 3, "t": 2}

        def bank_of(role, shape=(P, S), dtype=F32):
            bank = psum.tile(list(shape), dtype, tag=role, bufs=BANKS[role])
            return bank


        g_sb = [keep.tile([P, PACK, GATES], F32, name="gates%d" % c) for c in range(PASSES)]
        h_sb = [keep.tile([P, PACK, GATES], F32, name="shat%d" % c) for c in range(PASSES)]
        p0_sb = keep.tile([P, PASSES, PACK, S], BF16)
        p1_sb = keep.tile([P, PASSES, PACK, S], BF16)
        go_sb = keep.tile([P, PACK, S], BF16)
        s_codes = keep.tile([P, PASSES, 2 * S], U32, align_bytes=64)
        s_scales = keep.tile([P, PASSES, 2 * S], U8, align_bytes=64)
        da_codes = keep.tile([P, PASSES, GATES], U32, align_bytes=64)
        da_scales = keep.tile([P, PASSES, GATES], U8, align_bytes=64)
        sgn_bc = keep.tile([P, S], BF16)
        lnh_bc = keep.tile([P, S], BF16)
        ident_f = keep.tile([P, P], F32)
        ident_b = keep.tile([P, P], BF16)
        neg_ident_b = keep.tile([P, P], BF16)
        vec_rows = keep.tile([P, P], BF16)
        vec_cols = keep.tile([P, 6 * SQ], F32)
        lnh_rows = keep.tile([P, P], BF16)
        coef_cols = keep.tile([P, 4 * SQ], F32)
        sn_cols = keep.tile([P, 2 * SQ], F32)
        rs_sb = keep.tile([P, CHUNKS], F32)
        rs_pairs = keep.tile([P, CHUNKS, 2], F32)
        powers = keep.tile([P, 2], F32)
        eps_col = keep.tile([P, 1], F32)
        unread_col = keep.tile([P, 1], F32)
        dve_sums = keep.tile([P, CHUNKS, 8], F32)
        act_stats = keep.tile([P, CHUNKS, 16], F32)
        pool_stats = keep.tile([P, CHUNKS, 2], F32)
        unread_a = keep.tile([P, S], BF16)

        nc.vector.memset(vec_rows[:], 0.0)
        nc.scalar.dma_start(out=vec_rows[0 : 4 * SQ, :], in_=lns_g.rearrange("(r w) -> r w", w=P))
        nc.scalar.dma_start(out=vec_rows[4 * SQ : 5 * SQ, :], in_=lns_b[n_cols].rearrange("(r w) -> r w", w=P))
        nc.vector.memset(lnh_rows[:], 0.0)

        def load_shat(k, cols):
            nc.sync.dma_start(out=h_sb[k // PACK][:, k % PACK, cols], in_=shat_v[k // PACK, :, k % PACK, cols])

        def load_gates(k, cols):
            nc.sync.dma_start(out=g_sb[k // PACK][:, k % PACK, cols], in_=gates_v[k // PACK, :, k % PACK, cols])

        def load_states(c, rows):
            for dst, src in ((p0_sb, p0_v), (p1_sb, p1_v)):
                nc.sync.dma_start(out=dst[:, c, rows, :], in_=src[c, :, rows, :])

        def load_grad_out(c, rows):
            nc.sync.dma_start(out=go_sb[:, rows, :], in_=go_v[c, :, rows, :])

        def load_rest_of_shat(k):
            load_shat(k, slice(0, 2 * S))
            load_shat(k, l_cols)

        load_shat(0, n_cols)
        load_gates(0, r_cols)
        nc.sync.dma_start(out=lnh_rows[0:SQ, :], in_=lnh_g.rearrange("(r w) -> r w", w=P))
        load_gates(0, i_cols)
        load_gates(0, slice(2 * S, GATES))
        load_states(0, slice(0, 1))
        load_grad_out(0, slice(0, 1))
        nc.sync.dma_start(
            out=rs_sb[:].rearrange("p (c j) -> p c j", j=PACK),
            in_=rstd_s.rearrange("(c p j) o -> p c (j o)", p=P, j=PACK),
        )
        load_shat(1, n_cols)
        load_gates(1, whole)
        load_states(0, slice(1, PACK))
        load_grad_out(0, slice(1, PACK))
        load_shat(2, n_cols)
        load_gates(2, whole)
        load_rest_of_shat(0)
        for k in range(3, CHUNKS):
            load_shat(k, n_cols)
            load_gates(k, whole)
            if k == PACK - 1:
                load_states(1, slice(0, PACK))
            load_rest_of_shat(k - 2)
        load_rest_of_shat(CHUNKS - 2)
        load_rest_of_shat(CHUNKS - 1)

        nc.gpsimd.memset(eps_col[:], EPS)
        nc.scalar.activation(out=unread_col[:], in_=eps_col[:], func=ACT.Sigmoid)
        make_identity(nc, ident_f[:])
        nc.gpsimd.memset(powers[:, 0:1], -0.5)
        nc.gpsimd.memset(powers[:, 1:2], -1.0)
        nc.vector.tensor_copy(out=ident_b[:], in_=ident_f[:])
        nc.vector.tensor_scalar_mul(out=neg_ident_b[:], in0=ident_f[:], scalar1=-1.0)
        vec_bank = bank_of("t", (P, P), BF16)
        nc.tensor.transpose(vec_bank[:], vec_rows[:], ident_b[:])
        nc.vector.tensor_copy(out=vec_cols[:, 0 : 5 * SQ], in_=vec_bank[:, 0 : 5 * SQ])
        nc.vector.tensor_scalar_mul(out=sn_cols[:, 0:SQ], in0=vec_cols[:, BLOCK_N * SQ : (BLOCK_N + 1) * SQ], scalar1=-0.5)
        nc.vector.tensor_scalar_mul(out=sn_cols[:, SQ : 2 * SQ], in0=vec_cols[:, 4 * SQ : 5 * SQ], scalar1=-0.5)
        for b in range(4):
            sq = slice(b * SQ, (b + 1) * SQ)
            nc.vector.tensor_scalar_mul(out=coef_cols[:, sq], in0=vec_cols[:, sq], scalar1=BLOCK_COEF[b])

        def spread(dst, first_col, factor):
            bank = bank_of("f")
            for q in range(SQ):
                col = vec_cols[:, first_col + q : first_col + q + 1]
                nc.tensor.transpose(bank[:, q * P : (q + 1) * P], col.to_broadcast([P, P]), ident_f[:])
            return lambda: nc.vector.tensor_scalar_mul(out=dst[:], in0=bank[:], scalar1=factor)

        pairs = {}
        quads = {}
        sn_squares = {}
        n_squares = {}
        banks = {}

        def gate(k, cols):
            return g_sb[k // PACK][:, k % PACK, cols]

        def shat_of(k, cols):
            return h_sb[k // PACK][:, k % PACK, cols]

        def state(p_sb, k):
            return p_sb[:, k // PACK, k % PACK, :]

        def rs(k):
            return pairs[k][:, 0, :]

        def t1(k):
            return pairs[k][:, 1, :]

        def t3(k):
            return quads[k][:, 0, :]

        def hc(k):
            return quads[k][:, 1, :]

        def e_of(k):
            return quads[k][:, 2, :]

        def te(k):
            return quads[k][:, 3, :]

        def n_of(k):
            return gate(k, n_cols) if k < DIRECT else banks[("n", k)][:]

        def stt(out, in0, scalar, in1, op0, op1, accum_out=None):
            nc.vector.scalar_tensor_tensor(
                out=out, in0=in0, scalar=scalar, in1=in1, op0=op0, op1=op1, accum_out=accum_out
            )

        def tt(out, in0, in1, op):
            nc.vector.tensor_tensor(out=out, in0=in0, in1=in1, op=op)

        def squares():
            return [slice(q * P, (q + 1) * P) for q in range(SQ)]

        def turn(role, rows):
            bank = bank_of(role)
            for sq in squares():
                nc.tensor.transpose(bank[:, sq], rows[:, sq], ident_f[:])
            return bank

        def turn_sum(role, rows_a, rows_b):
            bank = bank_of(role)
            for sq in squares():
                nc.tensor.matmul(out=bank[:, sq], lhsT=rows_a[:, sq], rhs=ident_f[:], is_transpose=True, start=True, stop=False)
                nc.tensor.matmul(out=bank[:, sq], lhsT=rows_b[:, sq], rhs=ident_f[:], is_transpose=True, start=False, stop=True)
            return bank

        def scale_columns(bank, dst, scale_cols, bias_cols=None):
            for q, sq in enumerate(squares()):
                if bias_cols is None:
                    nc.scalar.activation(out=dst[:, sq], in_=bank[:, sq], func=ACT.Copy, scale=scale_cols[:, q : q + 1])
                else:
                    nc.scalar.activation(
                        out=dst[:, sq], in_=bank[:, sq], func=ACT.Identity,
                        scale=scale_cols[:, q : q + 1], bias=bias_cols[:, q : q + 1],
                    )

        def coef_of(block):
            return coef_cols[:, block * SQ : (block + 1) * SQ]

        def regrouped(rows):
            return rows.rearrange("p j (q i) -> p q j i", i=RUN)

        def quantise(grouped, codes, scales, x4):
            nc.vector.quantize_mx(out=codes.bitcast(x4), scales=scales, in_=grouped[:].rearrange("p w j -> p (w j)"))

        counts = {"fill": 0, "acc": 0, "regrouped": 0, "quantised": 0, "early": 0}
        S_PIECES = 2 * S // S_PIECE
        regrouped_s = []

        def regroup_next_s():
            c, piece = divmod(counts["regrouped"], S_PIECES)
            counts["regrouped"] = counts["regrouped"] + 1
            cols = slice(piece * S_PIECE, (piece + 1) * S_PIECE)
            src = (p0_sb, p1_sb)[cols.start // S]
            grouped = work.tile([P, S_PIECE, PACK], BF16, align_bytes=64, bufs=3)
            copy = (nc.vector.tensor_copy, nc.scalar.copy)[c]
            copy(
                out=grouped[:].rearrange("p (q i) j -> p q j i", i=RUN),
                in_=regrouped(src[:, c, :, cols.start % S : cols.start % S + S_PIECE]),
            )
            regrouped_s.append((grouped, s_codes[:, c, cols], s_scales[:, c, cols], E4M3X4))

        def quantise_next_s():
            quantise(*regrouped_s[counts["quantised"]])
            counts["quantised"] = counts["quantised"] + 1

        unquantised = {}

        def form_da(c, piece):
            cols = slice(sum(PIECE_WIDTHS[:piece]), sum(PIECE_WIDTHS[: piece + 1]))
            grouped = work.tile([P, PIECE_WIDTHS[piece], PACK], BF16, align_bytes=64, bufs=3)
            tt(
                grouped[:].rearrange("p (q i) j -> p q j i", i=RUN),
                regrouped(g_sb[c][:, :, cols]),
                regrouped(h_sb[c][:, :, cols]),
                ALU.add,
            )
            return (grouped, da_codes[:, c, cols], da_scales[:, c, cols], E5M2X4)

        def da_step(c, piece):
            formed = form_da(c, piece)
            if "piece" in unquantised:
                quantise(*unquantised["piece"])
            unquantised["piece"] = formed

        early_pieces = []

        def form_early():
            early_pieces.append(form_da(0, len(early_pieces)))

        def quantise_early():
            quantise(*early_pieces[counts["early"]])
            counts["early"] = counts["early"] + 1

        assert EARLY == 0 and S_PIECES == 4
        fillers = [
            regroup_next_s, regroup_next_s, quantise_next_s, regroup_next_s, quantise_next_s, regroup_next_s, quantise_next_s,
            quantise_next_s,
            quantise_next_s,
        ]

        def fill():
            if counts["fill"] < len(fillers):
                if fillers[counts["fill"]] is not None:
                    fillers[counts["fill"]]()
                counts["fill"] = counts["fill"] + 1

        def ok(k):
            return 0 <= k < CHUNKS

        def tanh_of(k, cols):
            if cols.start < S:
                nc.scalar.activation(out=gate(k, r_cols), in_=gate(k, r_cols), func=ACT.Tanh, scale=0.5)
            if cols.stop > S:
                nc.scalar.activation(out=gate(k, i_cols), in_=gate(k, i_cols), func=ACT.Sigmoid)

        def tanh_of_gates(k, first=slice(0, 2 * S)):
            tanh_of(k, first)
            tanh_of_l(k)

        def tanh_of_l(k):
            nc.scalar.activation(out=gate(k, l_cols), in_=turn("t", gate(k, l_cols))[:], func=ACT.Sigmoid, scale=-1.0)

        def sn_to_columns(k):
            bank = turn("t", shat_of(k, n_cols))
            sn_sq = work.tile([P, S], F32)
            sn_squares[k] = sn_sq
            scale_columns(bank, sn_sq, sn_cols[:, 0:SQ], sn_cols[:, SQ : 2 * SQ])

        def sn_to_rows(k):
            banks[("sn", k)] = turn("f", sn_squares[k])

        def difference(k):
            diff = bank_of("d01")
            for sq in squares():
                nc.tensor.matmul(out=diff[:, sq], lhsT=state(p0_sb, k)[:, sq], rhs=ident_b[:], start=True, stop=False)
                nc.tensor.matmul(out=diff[:, sq], lhsT=state(p1_sb, k)[:, sq], rhs=neg_ident_b[:], start=False, stop=True)
            banks[("d01", k)] = diff

        def candidate(k):
            bank = turn_sum("t", gate(k, n_cols), rs(k))
            n_sq = work.tile([P, S], F32)
            n_squares[k] = n_sq
            nc.scalar.activation(out=n_sq[:], in_=bank[:], func=ACT.Tanh)

        def candidate_to_rows(k):
            bank = bank_of("np")
            for sq in squares():
                nc.tensor.matmul(out=bank[:, sq], lhsT=neg_ident_b[:], rhs=state(p1_sb, k)[:, sq], start=True, stop=False)
                nc.tensor.matmul(
                    out=bank[:, sq], lhsT=t1(k)[:, sq], rhs=ident_f[:], is_transpose=True, start=False, stop=(k < DIRECT)
                )
                if k >= DIRECT:
                    nc.tensor.matmul(
                        out=bank[:, sq], lhsT=n_squares[k][:, sq], rhs=ident_f[:], is_transpose=True, start=False, stop=True
                    )
            banks[("np", k)] = bank
            if k >= DIRECT:
                banks[("n", k)] = turn("n", n_squares[k])

        def variance(k):
            neg_mu = act_stats[:, k, 0:1]
            ssq = act_stats[:, k, 1:2]
            var_eps = act_stats[:, k, 2:3]
            nc.scalar.mul(out=neg_mu, in_=dve_sums[:, k, 0:1], mul=-1.0 / S)
            nc.scalar.activation(out=unread_a[:], in_=hc(k), func=ACT.Square, bias=neg_mu, scale=1.0, accum_out=ssq)
            nc.scalar.activation(out=var_eps, in_=ssq, func=ACT.Identity, bias=eps_col[:], scale=1.0 / S)
            nc.gpsimd.tensor_tensor(
                out=pool_stats[:, k, 0:2], in0=var_eps.to_broadcast([P, 2]), in1=powers[:], op=ALU.pow
            )

        def covariance(k):
            nc.scalar.activation(
                out=act_stats[:, k, 3:4], in_=dve_sums[:, k, 1:2], func=ACT.Identity,
                scale=act_stats[:, k, 0:1], bias=dve_sums[:, k, 2:3],
            )

        def scaled_e(k, whole_chunk=True):
            neg_mu = act_stats[:, k, 0:1]
            rh = pool_stats[:, k, 0:1]
            rh2 = pool_stats[:, k, 1:2]
            a = act_stats[:, k, 4:5]
            a_neg = act_stats[:, k, 5:6]
            nc.scalar.activation(out=act_stats[:, k, 6:7], in_=act_stats[:, k, 3:4], func=ACT.Copy, scale=rh2)
            nc.scalar.activation(
                out=act_stats[:, k, 7:8], in_=act_stats[:, k, 6:7], func=ACT.Identity, scale=neg_mu, bias=dve_sums[:, k, 1:2]
            )
            nc.scalar.activation(out=act_stats[:, k, 4:6], in_=rs_pairs[:, k, :], func=ACT.Copy, scale=rh)
            nc.scalar.activation(out=act_stats[:, k, 8:10], in_=act_stats[:, k, 6:8], func=ACT.Copy, scale=a_neg)
            if whole_chunk:
                nc.scalar.activation(out=te(k), in_=e_of(k), func=ACT.Identity, bias=act_stats[:, k, 9:10], scale=a)

        def scaled_e_by_gpsimd(k):
            nc.gpsimd.tensor_scalar(
                out=te(k), in0=e_of(k), scalar1=act_stats[:, k, 4:5], scalar2=act_stats[:, k, 9:10], op0=ALU.mult, op1=ALU.add
            )

        def mean_terms(k, pieces=1):
            neg_mean_f = act_stats[:, k, 10:11]
            neg_mean_fs = act_stats[:, k, 11:12]
            nc.scalar.activation(
                out=act_stats[:, k, 12:16], in_=dve_sums[:, k, 3:7], func=ACT.Copy, scale=-1.0 / GATES,
                accum_out=neg_mean_f,
            )
            nc.scalar.mul(out=neg_mean_fs, in_=dve_sums[:, k, 7:8], mul=-1.0 / GATES)
            for piece in range(pieces):
                cols = slice(piece * GATES // pieces, (piece + 1) * GATES // pieces)
                nc.scalar.activation(
                    out=shat_of(k, cols), in_=shat_of(k, cols), func=ACT.Identity, bias=neg_mean_f, scale=neg_mean_fs
                )

        f_banks = {}

        def round_of_work(r, order):
            km, k0, k1, k2, k3 = r - 1, r, r + 1, r + 2, r + 3

            def t0():
                f_banks["i"] = turn("f", t3(k0))
                f_banks["l"] = turn("f", t1(k0))

            def t3_():
                f_banks["r"] = turn("f", rs(km))

            def t1_():
                nc.scalar.activation(out=gate(k1, n_cols), in_=n_of(k1), func=ACT.Square)

            def a1():
                quad = work.tile([P, 4, S], F32, bufs=3)
                quads[k1] = quad

            def k1_():
                bank = bank_of("np")
                for q in range(SQ):
                    col = vec_cols[:, 5 * SQ + q : 5 * SQ + q + 1]
                    nc.tensor.transpose(bank[:, q * P : (q + 1) * P], col.to_broadcast([P, P]), ident_f[:])
                banks[("lnh", k1)] = bank

            def f1():
                lnh = banks[("lnh", k1)][:] if ("lnh", k1) in banks else lnh_bc[:]
                stt(e_of(k1), go_sb[:, k1 % PACK, :], 1.0, lnh, ALU.mult, ALU.mult, accum_out=dve_sums[:, k1, 1:2])
                if k1 < PACK:
                    load_grad_out(1, slice(k1, k1 + 1))

            def f2():
                tt(t3(k1), gate(k1, n_cols), banks[("np", k1)][:], ALU.add)

            def f3():
                n_less_c = t3(k1) if k1 < DIRECT else banks[("np", k1)][:]
                stt(t3(k1), gate(k1, i_cols), 1.0, n_less_c, ALU.mult, ALU.mult)

            def f4():
                stt(hc(k1), t3(k1), -1.0, n_of(k1), ALU.mult, ALU.add, accum_out=dve_sums[:, k1, 0:1])

            def f7():
                scale_columns(turn("t", t3(k1)), t3(k1), coef_of(BLOCK_I))

            def f5():
                stt(te(k1), e_of(k1), 1.0, hc(k1), ALU.mult, ALU.mult, accum_out=dve_sums[:, k1, 2:3])
                covariance(k1)

            def f6():
                stt(t1(k1), gate(k1, l_cols), 1.0, t1(k1), ALU.mult, ALU.mult)
                scale_columns(t1(k1), t1(k1), coef_of(BLOCK_L))

            def z_():
                nc.gpsimd.tensor_tensor(out=e_of(k1), in0=gate(km, i_cols), in1=hc(km), op=ALU.mult)

            def w7():
                scale_columns(t1(k1), t1(k1), coef_of(BLOCK_L))

            def w6():
                nc.gpsimd.tensor_tensor(out=t1(k1), in0=gate(k1, l_cols), in1=t1(k1), op=ALU.mult)

            def g1():
                pair = work.tile([P, 2, S], F32, bufs=4)
                pairs[k2] = pair
                stt(rs(k2), gate(k2, r_cols), 1.0, banks[("sn", k2)][:], ALU.add, ALU.mult)

            def g3():
                if k2 < DIRECT:
                    tt(gate(k2, n_cols), gate(k2, n_cols), rs(k2), ALU.add)
                    nc.scalar.activation(out=gate(k2, n_cols), in_=gate(k2, n_cols), func=ACT.Tanh)
                else:
                    candidate(k2)

            def g4():
                scale_columns(turn("t", rs(k2)), rs(k2), coef_of(BLOCK_R))

            def g2():
                stt(t1(k2), gate(k2, l_cols), -1.0, banks[("d01", k2)][:], ALU.add, ALU.mult)

            def b1():
                stt(hc(k0), hc(k0), act_stats[:, k0, 8:9], te(k0), ALU.mult, ALU.add)

            def b2():
                stt(e_of(k0), gate(k0, i_cols), -1.0, hc(k0), ALU.add, ALU.mult)

            def b3():
                stt(hc(k0), gate(k0, i_cols), 1.0, hc(k0), ALU.mult, ALU.mult)

            def b4():
                stt(gate(k0, n_cols), gate(k0, n_cols), -1.0, e_of(k0), ALU.add, ALU.mult)

            def b5():
                stt(te(k0), gate(k0, r_cols), -1.0, gate(k0, n_cols), ALU.add, ALU.mult)

            def b6():
                stt(gate(km, i_cols), e_of(km), 1.0, f_banks["i"][:], ALU.mult, ALU.mult, accum_out=dve_sums[:, km, 3:4])

            def b7():
                i_dh = e_of(km + 2) if ok(km + 2) else hc(km)
                stt(gate(km, l_cols), i_dh, 1.0, f_banks["l"][:], ALU.mult, ALU.mult, accum_out=dve_sums[:, km, 4:5])

            def b8():
                stt(gate(km, r_cols), te(km), 1.0, f_banks["r"][:], ALU.mult, ALU.mult, accum_out=dve_sums[:, km, 6:7])

            def b9():
                stt(gate(km, n_cols), te(km), 1.0, sgn_bc[:], ALU.mult, ALU.mult, accum_out=dve_sums[:, km, 5:6])

            def b10():
                stt(
                    quads[km][:].rearrange("p a w -> p (a w)"), gate(km, whole), 1.0, shat_of(km, whole),
                    ALU.mult, ALU.mult, accum_out=dve_sums[:, km, 7:8],
                )

            table = {
                "T0": (k0, t0), "T3": (km, t3_), "T1": (k1, t1_), "T2": (km - 1, lambda: mean_terms(km - 1)),
                "R": (0, regroup_next_s), "V": (0, fill),
                "A1": (k1, a1), "W6": (k1, w6), "G3": (k2, g3), "G4": (k2, g4), "F7": (k1, f7), "F8": (k1, lambda: variance(k1)),
                "X7": (k3, lambda: tanh_of(k3, slice(0, 2 * S))), "X8": (k3, lambda: tanh_of_l(k3)), "F1": (k1, f1), "F2": (k1 if k1 < DIRECT else -1, f2), "F3": (k1, f3), "F4": (k1, f4), "F5": (k1, f5), "F6": (k1, f6),
                "G1": (k2, g1), "G2": (k2, g2),
                "X1": (k3, lambda: difference(k3)), "X6": (k3, lambda: sn_to_rows(k3)), "X2": (k3, lambda: tanh_of_gates(k3)), "XR": (k3, lambda: tanh_of(k3, r_cols)), "XI": (k3, lambda: tanh_of_gates(k3, i_cols)), "X3": (k1, lambda: scaled_e(k1)), "K1": (k1, k1_), "X9": (k1, lambda: scaled_e(k1, False)), "Y": (k0, lambda: scaled_e_by_gpsimd(k0)),
                "X4": (k3, lambda: sn_to_columns(k3)), "X5": (k2, lambda: candidate_to_rows(k2)),
                "B1": (k0, b1), "B2": (k0, b2), "B3": (-1 if ok(k0 + 2) else k0, b3), "Z": (km if ok(k1) else -1, z_), "W7": (k1, w7), "B4": (k0, b4), "B5": (k0, b5), "B6": (km, b6),
                "B7": (km, b7), "B8": (km, b8), "B9": (km, b9), "B10": (km, b10),
            }
            for name in order.split():
                chunk, step = table[name]
                if ok(chunk):
                    step()

        acc_roles = [role for role in BANKS for i in range(BANKS[role])]
        slots = {}

        def slot(m):
            place = m % 10
            if place in (0, 3, 6):
                quad = work.tile([P, 2, 2 * S], F32, bufs=3)
                slots["quad"] = quad
            if place in (0, 1, 3, 4, 6, 7):
                return slots["quad"][:, place % 3, :]
            pair = work.tile([P, 1, 2 * S], F32, bufs=4)
            return pair[:, 0, :]

        accs = {}

        def blocks_of(piece):
            return range(sum(PIECE_WIDTHS[:piece]) // P, sum(PIECE_WIDTHS[: piece + 1]) // P)

        def multiply(piece):
            for c in range(PASSES):
                for m in blocks_of(piece):
                    for half in range(2):
                        if c == 0:
                            acc = bank_of(acc_roles[counts["acc"] % len(acc_roles)])
                            counts["acc"] = counts["acc"] + 1
                            accs[(m, half)] = acc
                        rows = slice(m * P, (m + 1) * P)
                        cols = slice(half * S, (half + 1) * S)
                        nc.tensor.matmul_mx(
                            out=accs[(m, half)][:],
                            lhsT=da_codes[:, c, rows].bitcast(E5M2X4),
                            lhsT_scale=da_scales[:, c, rows],
                            rhs=s_codes[:, c, cols].bitcast(E4M3X4),
                            rhs_scale=s_scales[:, c, cols],
                            start=(c == 0),
                            stop=(c == PASSES - 1),
                        )

        def empty(piece):
            for m in blocks_of(piece):
                result = slot(m)
                for half in range(2):
                    cols = slice(half * S, (half + 1) * S)
                    if half == 1 and piece >= PIECES - VECTOR_EMPTIES:
                        nc.vector.tensor_copy(out=result[:, cols], in_=accs[(m, half)][:])
                    else:
                        nc.scalar.copy(out=result[:, cols], in_=accs[(m, half)][:])
                if piece < PIECES - 1:
                    nc.sync.dma_start(out=out[m * P : (m + 1) * P, :], in_=result)
                else:
                    nc.sync.dma_start(out=out[m * P : (m + 1) * P, 0:S], in_=result[:, 0:S])
                    nc.scalar.dma_start(out=out[m * P : (m + 1) * P, S : 2 * S], in_=result[:, S : 2 * S])

        steady = "T1 T2 A1 Z Y W6 G1 G3 T3 F3 K1 G2 F4 F8 X4 X7 X8 B7 B6 F1 X5 W7 G4 F7 X1 B1 B9 B2 B8 B4 F5 B5 X9 X6 T0 B10"
        with tc.manual_schedule():
            round_of_work(-3, "XR X4")
            lnh_bank = bank_of("t", (P, P), BF16)
            nc.tensor.transpose(lnh_bank[:], lnh_rows[:], ident_b[:])
            nc.vector.tensor_copy(out=vec_cols[:, 5 * SQ : 6 * SQ], in_=lnh_bank[:, 0:SQ])
            round_of_work(-3, "X6 XI X1")
            copy_lnh = spread(lnh_bc, 5 * SQ, 1.0)
            round_of_work(-2, "G1 G3 G4 G2 X5")
            copy_lnh()
            nc.vector.tensor_copy(out=rs_pairs[:, :, 0], in_=rs_sb[:])
            nc.vector.tensor_scalar_mul(out=rs_pairs[:, :, 1], in0=rs_sb[:], scalar1=-1.0 / S)
            round_of_work(-2, "X4 X6 X2 X1")
            copy_sgn = spread(sgn_bc, BLOCK_N * SQ, BLOCK_COEF[BLOCK_N])
            round_of_work(-1, "A1 F2 F1 F3 F6 F4 F8 F7 T1 G1 F5 G2 G3 G4 X5 X4 X6 X2 X3 X1")
            copy_sgn()
            round_of_work(0, "X4 A1 F2 F1 F3 G1 G3 G4 F4 F8 F7 T1 G2 X1 B1 F6 X5 X2 B2 F5 B4 V X9 B5 X6 T0 V V V V V V V")
            for r in range(1, CHUNKS - 3):
                round_of_work(r, steady)
            round_of_work(CHUNKS - 3, "T1 T2 A1 Z Y W6 G1 G3 T3 F3 K1 G2 F4 F8 B7 B6 F1 X5 W7 G4 F7 B1 B9 B2 B8 B4 F5 B5 X9 T0 B10")
            round_of_work(CHUNKS - 2, "T1 T2 A1 Z Y W6 T3 B8 F3 B9 F4 F8 B6 B7 W7 F7 B1 F1 B2 F5 B4 B3 B5 X3 T0 B10")
            round_of_work(CHUNKS - 1, "T2 R R R T3 B6 B7 B1 B9 B2 B8 B4 B3 B5 T0 B10")
            round_of_work(CHUNKS, "T2 T3 B9 B6 B7 B8 V R B10")
            mean_terms(CHUNKS - 1, 4)
            for piece in range(S_PIECES - 1):
                quantise_next_s()
            for piece in range(PIECES):
                if piece + EARLY < PIECES:
                    da_step(0, piece + EARLY)
                da_step(1, piece)
                if piece > 0:
                    multiply(piece - 1)
                if piece > 1:
                    empty(piece - 2)
            quantise(*unquantised["piece"])
            multiply(PIECES - 1)
            empty(PIECES - 2)
            empty(PIECES - 1)
